import numpy as np
import ml_dtypes


def mxq(x, axis, fmt="e4m3"):
    dtype, down = {"e4m3": (ml_dtypes.float8_e4m3fn, 7), "e5m2": (ml_dtypes.float8_e5m2, 14)}[fmt]
    v = np.moveaxis(np.asarray(x, np.float32).astype(ml_dtypes.bfloat16).astype(np.float64), axis, -1)
    blocks = v.reshape(v.shape[:-1] + (-1, 32))
    amax = np.abs(blocks).max(-1, keepdims=True)
    byte = np.maximum(np.where(amax > 0, np.frexp(amax)[1] - 1 + 127, 0) - down, 1)
    scale = np.exp2(byte - 127.0)
    codes = (blocks / scale).astype(np.float32).astype(dtype).astype(np.float64)
    return np.moveaxis((codes * scale).reshape(v.shape), -1, axis)


WIDE = False


def mx_kscale(k):
    if not WIDE:
        return np.ones(k)
    levels = np.array([10, -10, 5, -5, 0])
    a = np.random.permutation(np.resize(levels, k // 512 * 4)).reshape(k // 512, 4)
    idx = np.arange(k)
    return np.exp2(a[idx // 512, idx % 128 // 32])


BF16 = ml_dtypes.bfloat16


def bf(x):
    return np.asarray(x, np.float32).astype(BF16)


def f64(x):
    return np.asarray(x).astype(np.float64)


B, N, LD, HID = 4, 255, 512, 1024
NE = N + 1
DT, DX = 5e-4, 1e-3
FLUX_SCALE = 0.25
EH = 0.5
ET = 13


def erfc_pos(a):
    a = np.minimum(a, 9.0)
    acc = np.zeros_like(a)
    for n in range(ET):
        t2 = ((n + 0.5) * EH) ** 2
        acc += np.exp(-t2) / (t2 + a * a)
    return 2.0 * EH * a * np.exp(-a * a) / np.pi * acc + 2.0 / (1.0 + np.exp(2.0 * np.pi * a / EH))


def erf(z):
    return np.sign(z) * (1.0 - erfc_pos(np.abs(z)))


def gelu(v):
    return 0.5 * v * (1.0 + erf(v / np.sqrt(2.0)))


def setup_inputs():
    s = mx_kscale(HID)
    return {"edge_hid": bf(gelu(np.random.standard_normal((B, NE, HID)) * 1.4) * s),
            "u": bf(np.random.random((B, N))),
            "enc": bf((1.0 + 0.5 * np.random.standard_normal(LD)) / np.sqrt(LD)),
            "W2": bf(np.random.standard_normal((HID, HID)) * 1.2 / np.sqrt(HID) / s[:, None]),
            "b2": bf(np.random.standard_normal(HID) * 0.5),
            "W3": bf(np.random.standard_normal((HID, LD)) * 1.8 / np.sqrt(HID)),
            "b3": bf(np.random.standard_normal(LD) * 0.5)}


def reference(edge_hid, u, enc, W2, b2, W3, b3):
    u, enc = f64(u), f64(enc)
    h = u[..., None] * enc
    x = gelu((mxq(f64(edge_hid), 2, "e4m3") @ mxq(f64(W2), 0, "e4m3")) + f64(b2))
    flux = np.tanh((mxq(x, 2, "e4m3") @ mxq(f64(W3), 0, "e4m3")) + f64(b3)) * FLUX_SCALE
    h_new = h - (DT / DX) * (flux[:, 1:] - flux[:, :-1])
    dec = enc / (np.sum(enc * enc) + 1e-12)
    return np.sum(h_new * dec, axis=-1)

@@ -1,0 +1,318 @@
+from contextlib import ExitStack
+
+import concourse.mybir as mybir
+from concourse.masks import make_identity
+
+F32 = mybir.dt.float32
+BF16 = mybir.dt.bfloat16
+U32 = mybir.dt.uint32
+U8 = mybir.dt.uint8
+FP8X4 = mybir.dt.float8_e4m3fn_x4
+ACT = mybir.ActivationFunctionType
+ALU = mybir.AluOpType
+
+P = 128
+NB = 4
+NE = 256
+NC = 255
+HID = 1024
+LD = 512
+COEF = 0.5 * 0.25
+BLOCKS = ((0,), (1, 2,), (3,))
+
+FLOPS = 2 * NB * NE * HID * HID + 2 * NB * NE * HID * LD
+
+ORDER = (
+    ("tE", 0, 0), ("tE", 0, 1), ("vecT", 0, 0), ("cE", 0, 0), ("cE", 0, 1), ("rW2", 0, 0),
+    ("cols", 0, 0), ("qE", 0, 0), ("qW2", 0, 0), ("rW2", 0, 1), ("tE", 1, 0), ("tE", 1, 1),
+    ("ssum", 0, 0), ("cE", 1, 0), ("cE", 1, 1), ("qW2", 0, 1), ("coef", 0, 0), ("rW2", 1, 0),
+    ("mm1", 0, 0), ("mm1", 1, 0), ("gelu", 0, 0), ("mm1", 2, 0), ("gelu", 1, 0), ("mm1", 3, 0),
+    ("gelu", 2, 0), ("rW2", 1, 1), ("gelu", 3, 0), ("tE", 2, 0), ("qW2", 1, 0), ("tE", 2, 1),
+    ("cE", 2, 0), ("qW2", 1, 1), ("cE", 2, 1), ("tE", 3, 0), ("rX", 0, 0), ("mm1", 4, 0),
+    ("cE", 3, 0), ("qE", 1, 0), ("mm1", 5, 0), ("mm1", 6, 0), ("gelu", 4, 0), ("qX", 0, 0),
+    ("mm1", 7, 0), ("gelu", 5, 0), ("qE", 2, 0), ("tE", 3, 1), ("gelu", 6, 0), ("gelu", 7, 0),
+    ("rW3", 0, 0), ("mm1", 0, 1), ("cE", 3, 1), ("mm1", 1, 1), ("gelu", 0, 1), ("rX", 1, 0),
+    ("mm1", 2, 1), ("gelu", 1, 1), ("qE", 3, 0), ("mm1", 3, 1), ("gelu", 2, 1), ("mm1", 4, 1),
+    ("qX", 1, 0), ("qW3", 0, 0), ("gelu", 3, 1), ("mm1", 5, 1), ("rW3", 1, 0), ("gelu", 4, 1),
+    ("mm1", 6, 1), ("gelu", 5, 1), ("mm1", 7, 1), ("rX", 0, 1), ("gelu", 6, 1), ("mm1", 0, 2),
+    ("mm1", 1, 2), ("gelu", 7, 1), ("mm1", 2, 2), ("mm1", 3, 2), ("qW3", 1, 0), ("gelu", 0, 2),
+    ("mm1", 4, 2), ("gelu", 1, 2), ("mm1", 5, 2), ("qX", 0, 1), ("gelu", 2, 2), ("mm1", 6, 2),
+    ("gelu", 3, 2), ("mm1", 7, 2), ("rX", 1, 1), ("gelu", 4, 2), ("mm2a", 0, 0), ("mm2b", 0, 0),
+    ("gelu", 5, 2), ("mm2a", 1, 0), ("mm2b", 1, 0), ("gelu", 6, 2), ("mm2a", 2, 0), ("mm2b", 2, 0),
+    ("rX", 0, 2), ("gelu", 7, 2), ("mm2a", 3, 0), ("mm2b", 3, 0), ("tanh", 0, 0), ("mm2a", 0, 1),
+    ("qX", 1, 1), ("tanh", 1, 0), ("mm2a", 1, 1), ("tanh", 2, 0), ("mm2a", 2, 1), ("qX", 0, 2),
+    ("tanh", 3, 0), ("mm2b", 0, 1), ("rX", 1, 2), ("mm2b", 1, 1), ("tanh", 0, 1), ("mm2b", 2, 1),
+    ("vs", 0, 0), ("mm2a", 3, 1), ("qX", 1, 2), ("tanh", 1, 1), ("mm2b", 3, 1), ("vs", 1, 0),
+    ("mm2a", 0, 2), ("vs", 2, 0), ("mm2b", 0, 2), ("tanh", 2, 1), ("mm2a", 1, 2), ("mm2b", 1, 2),
+    ("vs", 3, 0), ("mm2a", 2, 2), ("mm2b", 2, 2), ("tanh", 3, 1), ("vs", 0, 1), ("mm2a", 3, 2),
+    ("ws", 0, 0), ("vs", 1, 1), ("tanh", 0, 2), ("mm2b", 3, 2), ("tanh", 1, 2), ("vs", 2, 1),
+    ("tanh", 2, 2), ("tanh", 3, 2), ("vs", 3, 1), ("vs", 0, 2), ("ws", 1, 0), ("vs", 1, 2),
+    ("vs", 2, 2), ("ws", 2, 0), ("vs", 3, 2), ("ws", 3, 0), ("f1", 0, 0), ("f2", 0, 0),
+)
+
+
+def tile_fluxgnn1dlatent_pb_kernel(tc, edge_hid, u, enc, W2, b2, W3, b3, out):
+    nc = tc.nc
+    with ExitStack() as ctx:
+        keep = ctx.enter_context(tc.tile_pool(name="keep", bufs=1))
+        psum = ctx.enter_context(tc.psum_pool(name="psum", bufs=1))
+        ctx.enter_context(tc.manual_schedule())
+        nblk = len(BLOCKS)
+        width = [NE * len(bs) for bs in BLOCKS]
+        home = {}
+        for k, bs in enumerate(BLOCKS):
+            for i, b in enumerate(bs):
+                home[b] = (k, i)
+
+        e_raw = [keep.tile([P, 2, HID], BF16, name="e_raw%d" % b) for b in range(NB)]
+        e_grp = [keep.tile([P, 2, 4 * NE], BF16, name="e_grp%d" % b, align_bytes=64) for b in range(NB)]
+        e_cod = [keep.tile([P, 2, width[k]], U32, name="e_cod%d" % k, align_bytes=64) for k in range(nblk)]
+        e_scl = [keep.tile([P, 2, width[k]], U8, name="e_scl%d" % k, align_bytes=64) for k in range(nblk)]
+        w2_raw = [keep.tile([P, 8, 512], BF16, name="w2_raw%d" % h) for h in range(2)]
+        w2_grp = [keep.tile([P, 2, 2048], BF16, name="w2_grp%d" % h, align_bytes=64) for h in range(2)]
+        w2_cod = [keep.tile([P, 2, 512], U32, name="w2_cod%d" % h, align_bytes=64) for h in range(2)]
+        w2_scl = [keep.tile([P, 2, 512], U8, name="w2_scl%d" % h, align_bytes=64) for h in range(2)]
+        w3_raw = [keep.tile([P, 4, LD], BF16, name="w3_raw%d" % g) for g in range(2)]
+        w3_grp = [keep.tile([P, 4 * LD], BF16, name="w3_grp%d" % g, align_bytes=64) for g in range(2)]
+        w3_cod = [keep.tile([P, LD], U32, name="w3_cod%d" % g, align_bytes=64) for g in range(2)]
+        w3_scl = [keep.tile([P, LD], U8, name="w3_scl%d" % g, align_bytes=64) for g in range(2)]
+        x_pln = [[keep.tile([P, 4, width[k]], BF16, name="x_pln%d_%d" % (g, k)) for k in range(nblk)] for g in range(2)]
+        x_grp = [
+            [keep.tile([P, 4 * width[k]], BF16, name="x_grp%d_%d" % (g, k), align_bytes=64) for k in range(nblk)]
+            for g in range(2)
+        ]
+        x_cod = [
+            [keep.tile([P, width[k]], U32, name="x_cod%d_%d" % (g, k), align_bytes=64) for k in range(nblk)]
+            for g in range(2)
+        ]
+        x_scl = [
+            [keep.tile([P, width[k]], U8, name="x_scl%d_%d" % (g, k), align_bytes=64) for k in range(nblk)]
+            for g in range(2)
+        ]
+        t_sb = [[keep.tile([P, width[k]], F32, name="t_sb%d_%d" % (ct, k)) for k in range(nblk)] for ct in range(4)]
+        wsum = [keep.tile([P, width[k]], F32, name="wsum%d" % k) for k in range(nblk)]
+
+        ident = keep.tile([P, P], F32, name="ident")
+        pick = keep.tile([P, NB * P], F32, name="pick")
+        vec_rows = keep.tile([16, P], BF16, name="vec_rows")
+        vec_f32 = keep.tile([P, P], F32, name="vec_f32")
+        cols = keep.tile([P, 16], F32, name="cols")
+        zero1 = keep.tile([P, 1], F32, name="zero1")
+        junk1 = keep.tile([P, 1], F32, name="junk1")
+        u_bf = keep.tile([NB, NC], BF16, name="u_bf")
+        u_s = keep.tile([NB, NC], F32, name="u_s")
+        den = keep.tile([P, 1], F32, name="den")
+        rinv = keep.tile([P, 1], F32, name="rinv")
+        c_u = keep.tile([P, 1], F32, name="c_u")
+        c_pos = keep.tile([P, 1], F32, name="c_pos")
+        c_neg = keep.tile([P, 1], F32, name="c_neg")
+        part = keep.tile([NB, NC], F32, name="part")
+        res = keep.tile([NB, NC], F32, name="res")
+        bank = {}
+
+        nc.scalar.dma_start(out=vec_rows[0:8, :], in_=b2.rearrange("(j c) -> j c", c=P))
+        nc.scalar.dma_start(out=vec_rows[8:12, :], in_=b3.rearrange("(j c) -> j c", c=P))
+        nc.scalar.dma_start(out=vec_rows[12:16, :], in_=enc.rearrange("(j c) -> j c", c=P))
+        nc.scalar.dma_start(out=u_bf[:], in_=u)
+
+        def load_w2(h, g):
+            for j in (2 * g, 2 * g + 1):
+                nc.sync.dma_start(
+                    out=w2_raw[h][:, 2 * j : 2 * j + 2, :],
+                    in_=W2[256 * j : 256 * j + 256, 512 * h : 512 * h + 512].rearrange("(p e) n -> p e n", e=2),
+                )
+
+        def load_e(b):
+            nc.sync.dma_start(out=e_raw[b][:], in_=edge_hid[b, :, :].rearrange("(j p) k -> p j k", p=P))
+
+        def load_w3(g):
+            nc.sync.dma_start(
+                out=w3_raw[g][:], in_=W3[512 * g : 512 * g + 512, :].rearrange("(t p) c -> p t c", p=P)
+            )
+
+        load_e(0)
+        load_w2(0, 0)
+        load_w2(0, 1)
+        load_e(1)
+        load_w2(1, 0)
+        load_w2(1, 1)
+        load_e(2)
+        load_e(3)
+        load_w3(0)
+        load_w3(1)
+
+        nc.vector.memset(zero1[:], 0.0)
+        nc.scalar.activation(out=junk1[:], in_=zero1[:], func=ACT.Gelu)
+        nc.vector.memset(vec_f32[:], 0.0)
+        make_identity(nc, ident[:])
+        nc.gpsimd.memset(pick[:], 0.0)
+        nc.gpsimd.memset(pick[:, 0 : (NB - 1) * (P + 1) + 1 : P + 1], 1.0)
+        nc.vector.tensor_copy(out=vec_f32[0:16, :], in_=vec_rows[:])
+
+        def regroup(dst, src):
+            nc.vector.tensor_copy(
+                out=dst.rearrange("p (c i t) -> p c t i", i=4, t=4),
+                in_=src.rearrange("p t (c i) -> p c t i", i=4),
+            )
+
+        def op_vecT(a, b):
+            bank["vec"] = psum.tile([P, P], F32, name="vec_t", tag="tp", bufs=2)
+            nc.tensor.transpose(bank["vec"][:], vec_f32[:], ident[:])
+
+        def op_cols(a, b):
+            nc.vector.tensor_copy(out=cols[:], in_=bank["vec"][:, 0:16])
+
+        def op_ssum(a, b):
+            bank["ssum"] = psum.tile([P, 1], F32, name="ssum", tag="g", bufs=1)
+            for ct in range(4):
+                nc.tensor.matmul(
+                    out=bank["ssum"][:],
+                    lhsT=cols[:, 12 + ct : 13 + ct].to_broadcast([P, P]),
+                    rhs=cols[:, 12 + ct : 13 + ct],
+                    start=(ct == 0),
+                    stop=(ct == 3),
+                )
+
+        def op_coef(a, b):
+            ssum = bank["ssum"]
+            nc.vector.tensor_scalar_add(out=den[:], in0=ssum[:], scalar1=1e-12)
+            nc.vector.reciprocal(out=rinv[:], in_=den[:])
+            nc.vector.tensor_mul(out=c_u[:], in0=ssum[:], in1=rinv[:])
+            nc.vector.tensor_scalar_mul(out=c_pos[:], in0=rinv[:], scalar1=COEF)
+            nc.vector.tensor_scalar_mul(out=c_neg[:], in0=rinv[:], scalar1=-COEF)
+            nc.vector.tensor_scalar_mul(out=u_s[:], in0=u_bf[:], scalar1=c_u[0:NB, 0:1])
+
+        def op_rW2(h, g):
+            regroup(w2_grp[h][:, g, :], w2_raw[h][:, 4 * g : 4 * g + 4, :])
+
+        def op_qW2(h, g):
+            nc.vector.quantize_mx(
+                out=w2_cod[h][:, g, :].bitcast(FP8X4), scales=w2_scl[h][:, g, :], in_=w2_grp[h][:, g, :]
+            )
+
+        def op_rW3(g, b):
+            regroup(w3_grp[g][:], w3_raw[g][:])
+
+        def op_qW3(g, b):
+            nc.vector.quantize_mx(out=w3_cod[g][:].bitcast(FP8X4), scales=w3_scl[g][:], in_=w3_grp[g][:])
+
+        def op_tE(b, g):
+            tp = psum.tile([P, 2, NE], F32, name="tp", tag="tp", bufs=2)
+            bank[("tp", b, g)] = tp
+            for jj in range(2):
+                words = e_raw[b][:, jj, :].bitcast(F32)
+                for uu in range(2):
+                    w0 = 256 * g + 128 * uu
+                    nc.tensor.transpose(tp[:, uu, P * jj : P * jj + P], words[:, w0 : w0 + P], ident[:])
+
+        def op_cE(b, g):
+            nc.scalar.copy(
+                out=e_grp[b][:, g, :].bitcast(F32).rearrange("p (r w) -> p r w", w=2),
+                in_=bank[("tp", b, g)][:].rearrange("p w r -> p r w"),
+            )
+
+        def op_qE(b, z):
+            k, i = home[b]
+            for g in range(2):
+                nc.vector.quantize_mx(
+                    out=e_cod[k][:, g, NE * i : NE * i + NE].bitcast(FP8X4),
+                    scales=e_scl[k][:, g, NE * i : NE * i + NE],
+                    in_=e_grp[b][:, g, :],
+                )
+
+        def op_mm1(m, k):
+            h, t = divmod(m, 4)
+            acc = psum.tile([P, 512], F32, name="acc1", tag="mm", bufs=5)
+            bank[("a1", m, k)] = acc
+            for g in range(2):
+                nc.tensor.matmul_mx(
+                    out=acc[:, 0 : width[k]],
+                    lhsT=w2_cod[h][:, g, P * t : P * t + P].bitcast(FP8X4),
+                    lhsT_scale=w2_scl[h][:, g, P * t : P * t + P],
+                    rhs=e_cod[k][:, g, :].bitcast(FP8X4),
+                    rhs_scale=e_scl[k][:, g, :],
+                    start=(g == 0),
+                    stop=(g == 1),
+                )
+
+        def op_gelu(m, k):
+            h, t = divmod(m, 4)
+            nc.scalar.activation(
+                out=x_pln[h][k][:, t, :], in_=bank[("a1", m, k)][:, 0 : width[k]], func=ACT.Gelu, bias=cols[:, m : m + 1]
+            )
+
+        def op_rX(g, k):
+            regroup(x_grp[g][k][:], x_pln[g][k][:])
+
+        def op_qX(g, k):
+            nc.vector.quantize_mx(out=x_cod[g][k][:].bitcast(FP8X4), scales=x_scl[g][k][:], in_=x_grp[g][k][:])
+
+        def mm2(ct, k, g):
+            nc.tensor.matmul_mx(
+                out=bank[("a2", ct, k)][:, 0 : width[k]],
+                lhsT=w3_cod[g][:, P * ct : P * ct + P].bitcast(FP8X4),
+                lhsT_scale=w3_scl[g][:, P * ct : P * ct + P],
+                rhs=x_cod[g][k][:].bitcast(FP8X4),
+                rhs_scale=x_scl[g][k][:],
+                start=(g == 0),
+                stop=(g == 1),
+            )
+
+        def op_mm2a(ct, k):
+            bank[("a2", ct, k)] = psum.tile([P, 512], F32, name="acc2", tag="mm", bufs=5)
+            mm2(ct, k, 0)
+
+        def op_mm2b(ct, k):
+            mm2(ct, k, 1)
+
+        def op_tanh(ct, k):
+            nc.scalar.activation(
+                out=t_sb[ct][k][:], in_=bank[("a2", ct, k)][:, 0 : width[k]], func=ACT.Tanh, bias=cols[:, 8 + ct : 9 + ct]
+            )
+
+        def op_vs(ct, k):
+            if ct == 0:
+                nc.vector.tensor_scalar_mul(out=wsum[k][:], in0=t_sb[ct][k][:], scalar1=cols[:, 12:13])
+            else:
+                nc.vector.scalar_tensor_tensor(
+                    out=wsum[k][:],
+                    in0=t_sb[ct][k][:],
+                    scalar=cols[:, 12 + ct : 13 + ct],
+                    in1=wsum[k][:],
+                    op0=ALU.mult,
+                    op1=ALU.add,
+                )
+
+        def op_ws(b, z):
+            k, i = home[b]
+            if b == 0:
+                bank["gsum"] = psum.tile([P, NE], F32, name="gsum", tag="g", bufs=1)
+            nc.tensor.matmul(
+                out=bank["gsum"][:],
+                lhsT=pick[:, P * b : P * b + P],
+                rhs=wsum[k][:, NE * i : NE * i + NE],
+                start=(b == 0),
+                stop=(b == NB - 1),
+            )
+
+        def op_f1(a, b):
+            nc.vector.scalar_tensor_tensor(
+                out=part[:], in0=bank["gsum"][0:NB, 0:NC], scalar=c_pos[0:NB, 0:1], in1=u_s[:], op0=ALU.mult, op1=ALU.add
+            )
+
+        def op_f2(a, b):
+            nc.vector.scalar_tensor_tensor(
+                out=res[:], in0=bank["gsum"][0:NB, 1:NE], scalar=c_neg[0:NB, 0:1], in1=part[:], op0=ALU.mult, op1=ALU.add
+            )
+
+        ops = {
+            "vecT": op_vecT, "cols": op_cols, "ssum": op_ssum, "coef": op_coef,
+            "rW2": op_rW2, "qW2": op_qW2, "rW3": op_rW3, "qW3": op_qW3,
+            "tE": op_tE, "cE": op_cE, "qE": op_qE, "mm1": op_mm1, "gelu": op_gelu,
+            "rX": op_rX, "qX": op_qX, "mm2a": op_mm2a, "mm2b": op_mm2b, "tanh": op_tanh,
+            "vs": op_vs, "ws": op_ws, "f1": op_f1, "f2": op_f2,
+        }
+        for name, a, b in ORDER:
+            ops[name](a, b)
+
+        nc.sync.dma_start(out=out, in_=res[:])

@@ -19,35 +19,38 @@ HID = 1024
 LD = 512
 COEF = 0.5 * 0.25
 BLOCKS = ((0,), (1, 2,), (3,))
+DIRECT = (0, 3)
+S_COLS = {(0, 0): 208, (0, 1): 208}
 
 FLOPS = 2 * NB * NE * HID * HID + 2 * NB * NE * HID * LD
 
 ORDER = (
-    ("tE", 0, 0), ("tE", 0, 1), ("vecT", 0, 0), ("cE", 0, 0), ("cE", 0, 1), ("rW2", 0, 0),
-    ("cols", 0, 0), ("qE", 0, 0), ("qW2", 0, 0), ("rW2", 0, 1), ("tE", 1, 0), ("tE", 1, 1),
-    ("ssum", 0, 0), ("cE", 1, 0), ("cE", 1, 1), ("qW2", 0, 1), ("coef", 0, 0), ("rW2", 1, 0),
-    ("mm1", 0, 0), ("mm1", 1, 0), ("gelu", 0, 0), ("mm1", 2, 0), ("gelu", 1, 0), ("mm1", 3, 0),
-    ("gelu", 2, 0), ("rW2", 1, 1), ("gelu", 3, 0), ("tE", 2, 0), ("qW2", 1, 0), ("tE", 2, 1),
-    ("cE", 2, 0), ("qW2", 1, 1), ("cE", 2, 1), ("tE", 3, 0), ("rX", 0, 0), ("mm1", 4, 0),
-    ("cE", 3, 0), ("qE", 1, 0), ("mm1", 5, 0), ("mm1", 6, 0), ("gelu", 4, 0), ("qX", 0, 0),
-    ("mm1", 7, 0), ("gelu", 5, 0), ("qE", 2, 0), ("tE", 3, 1), ("gelu", 6, 0), ("gelu", 7, 0),
-    ("rW3", 0, 0), ("mm1", 0, 1), ("cE", 3, 1), ("mm1", 1, 1), ("gelu", 0, 1), ("rX", 1, 0),
-    ("mm1", 2, 1), ("gelu", 1, 1), ("qE", 3, 0), ("mm1", 3, 1), ("gelu", 2, 1), ("mm1", 4, 1),
-    ("qX", 1, 0), ("qW3", 0, 0), ("gelu", 3, 1), ("mm1", 5, 1), ("rW3", 1, 0), ("gelu", 4, 1),
-    ("mm1", 6, 1), ("gelu", 5, 1), ("mm1", 7, 1), ("rX", 0, 1), ("gelu", 6, 1), ("mm1", 0, 2),
-    ("mm1", 1, 2), ("gelu", 7, 1), ("mm1", 2, 2), ("mm1", 3, 2), ("qW3", 1, 0), ("gelu", 0, 2),
-    ("mm1", 4, 2), ("gelu", 1, 2), ("mm1", 5, 2), ("qX", 0, 1), ("gelu", 2, 2), ("mm1", 6, 2),
-    ("gelu", 3, 2), ("mm1", 7, 2), ("rX", 1, 1), ("gelu", 4, 2), ("mm2a", 0, 0), ("mm2b", 0, 0),
-    ("gelu", 5, 2), ("mm2a", 1, 0), ("mm2b", 1, 0), ("gelu", 6, 2), ("mm2a", 2, 0), ("mm2b", 2, 0),
-    ("rX", 0, 2), ("gelu", 7, 2), ("mm2a", 3, 0), ("mm2b", 3, 0), ("tanh", 0, 0), ("mm2a", 0, 1),
-    ("qX", 1, 1), ("tanh", 1, 0), ("mm2a", 1, 1), ("tanh", 2, 0), ("mm2a", 2, 1), ("qX", 0, 2),
-    ("tanh", 3, 0), ("mm2b", 0, 1), ("rX", 1, 2), ("mm2b", 1, 1), ("tanh", 0, 1), ("mm2b", 2, 1),
-    ("vs", 0, 0), ("mm2a", 3, 1), ("qX", 1, 2), ("tanh", 1, 1), ("mm2b", 3, 1), ("vs", 1, 0),
-    ("mm2a", 0, 2), ("vs", 2, 0), ("mm2b", 0, 2), ("tanh", 2, 1), ("mm2a", 1, 2), ("mm2b", 1, 2),
-    ("vs", 3, 0), ("mm2a", 2, 2), ("mm2b", 2, 2), ("tanh", 3, 1), ("vs", 0, 1), ("mm2a", 3, 2),
-    ("ws", 0, 0), ("vs", 1, 1), ("tanh", 0, 2), ("mm2b", 3, 2), ("tanh", 1, 2), ("vs", 2, 1),
-    ("tanh", 2, 2), ("tanh", 3, 2), ("vs", 3, 1), ("vs", 0, 2), ("ws", 1, 0), ("vs", 1, 2),
-    ("vs", 2, 2), ("ws", 2, 0), ("vs", 3, 2), ("ws", 3, 0), ("f1", 0, 0), ("f2", 0, 0),
+    ("rW2", 0, 0), ("sW2", 0, 0), ("tE", 0, 0), ("qW2", 0, 0), ("tE", 0, 1), ("vecT", 0, 0),
+    ("rW2", 0, 1), ("sW2", 0, 1), ("cE", 0, 1), ("rW2", 1, 0), ("cE", 0, 0), ("cols", 0, 0),
+    ("tE", 1, 1), ("ssum", 0, 0), ("qW2", 0, 1), ("tE", 1, 0), ("qE", 0, 0), ("cE", 1, 1),
+    ("den", 0, 0), ("cE", 1, 0), ("qW2", 1, 0), ("rinv", 0, 0), ("mm1", 3, 0), ("mm1", 0, 0),
+    ("rW2", 1, 1), ("tE", 2, 0), ("gelu", 0, 0), ("gelu", 3, 0), ("tE", 2, 1), ("cE", 2, 0),
+    ("coef", 0, 0), ("qE", 1, 0), ("mm1", 2, 0), ("cE", 2, 1), ("mm1", 1, 0), ("tE", 3, 1),
+    ("qW2", 1, 1), ("gelu", 2, 0), ("gelu", 1, 0), ("tE", 3, 0), ("qE", 2, 0), ("cE", 3, 1),
+    ("mm1", 6, 0), ("cE", 3, 0), ("mm1", 4, 0), ("rW3", 1, 0), ("mm1", 2, 1), ("gelu", 4, 0),
+    ("mm1", 7, 0), ("gelu", 6, 0), ("mm1", 0, 1), ("qE", 3, 0), ("gelu", 2, 1), ("mm1", 3, 1),
+    ("gelu", 7, 0), ("rW3", 0, 0), ("gelu", 0, 1), ("mm1", 6, 2), ("mm1", 1, 1), ("gelu", 3, 1),
+    ("rX", 0, 0), ("mm1", 5, 0), ("gelu", 6, 2), ("mm1", 5, 1), ("gelu", 1, 1), ("qW3", 0, 0),
+    ("mm1", 1, 2), ("mm1", 5, 2), ("gelu", 5, 1), ("qX", 0, 0), ("mm1", 7, 1), ("qW3", 1, 0),
+    ("gelu", 5, 0), ("mm1", 4, 2), ("gelu", 1, 2), ("mm1", 6, 1), ("rX", 1, 0), ("gelu", 7, 1),
+    ("mm1", 4, 1), ("rX", 0, 1), ("gelu", 5, 2), ("gelu", 6, 1), ("mm2a", 3, 0), ("mm1", 3, 2),
+    ("gelu", 4, 2), ("qX", 1, 0), ("mm1", 0, 2), ("gelu", 3, 2), ("mm2a", 0, 0), ("qX", 0, 1),
+    ("gelu", 4, 1), ("mm2b", 3, 0), ("mm2a", 1, 0), ("mm2b", 0, 0), ("mm2b", 1, 0), ("tanh", 3, 0),
+    ("mm1", 2, 2), ("rX", 1, 1), ("gelu", 0, 2), ("mm1", 7, 2), ("tanh", 1, 0), ("wsd", 3, 0),
+    ("gelu", 7, 2), ("mm2a", 2, 0), ("tanh", 0, 0), ("mm2a", 0, 1), ("qX", 1, 1), ("gelu", 2, 2),
+    ("mm2a", 3, 1), ("mm2b", 2, 0), ("wsd", 1, 0), ("rX", 0, 2), ("tanh", 2, 0), ("mm2b", 0, 1),
+    ("mm2a", 1, 1), ("qX", 0, 2), ("tanh", 0, 1), ("mm2a", 2, 1), ("mm2b", 1, 1), ("rX", 1, 2),
+    ("wsd", 2, 0), ("tanh", 1, 1), ("mm2b", 2, 1), ("qX", 1, 2), ("mm2a", 2, 2), ("mm2b", 3, 1),
+    ("tanh", 2, 1), ("vs", 0, 1), ("mm2b", 2, 2), ("mm2a", 0, 2), ("vs", 1, 1), ("mm2a", 3, 2),
+    ("tanh", 2, 2), ("mm2b", 3, 2), ("wsd", 0, 0), ("tanh", 3, 1), ("vs", 2, 1), ("mm2a", 1, 2),
+    ("wsd", 2, 3), ("tanh", 3, 2), ("vs", 3, 1), ("mm2b", 0, 2), ("mm2b", 1, 2), ("wsd", 3, 3),
+    ("tanh", 0, 2), ("tanh", 1, 2), ("ws", 1, 0), ("ws", 2, 0), ("wsd", 0, 3), ("wsd", 1, 3),
+    ("f1", 0, 0), ("f2", 0, 0),
 )
 
 
@@ -63,6 +66,7 @@ def tile_fluxgnn1dlatent_pb_kernel(tc, edge_hid, u, enc, W2, b2, W3, b3, out):
         for k, bs in enumerate(BLOCKS):
             for i, b in enumerate(bs):
                 home[b] = (k, i)
+        sums = [op for op in ORDER if op[0] in ("ws", "wsd")]
 
         e_raw = [keep.tile([P, 2, HID], BF16, name="e_raw%d" % b) for b in range(NB)]
         e_grp = [keep.tile([P, 2, 4 * NE], BF16, name="e_grp%d" % b, align_bytes=64) for b in range(NB)]
@@ -94,6 +98,9 @@ def tile_fluxgnn1dlatent_pb_kernel(tc, edge_hid, u, enc, W2, b2, W3, b3, out):
 
         ident = keep.tile([P, P], F32, name="ident")
         pick = keep.tile([P, NB * P], F32, name="pick")
+        pick_enc = {}
+        for b in DIRECT:
+            pick_enc[b] = keep.tile([P, 4 * P], F32, name="pick_enc%d" % b)
         vec_rows = keep.tile([16, P], BF16, name="vec_rows")
         vec_f32 = keep.tile([P, P], F32, name="vec_f32")
         cols = keep.tile([P, 16], F32, name="cols")
@@ -130,29 +137,31 @@ def tile_fluxgnn1dlatent_pb_kernel(tc, edge_hid, u, enc, W2, b2, W3, b3, out):
                 out=w3_raw[g][:], in_=W3[512 * g : 512 * g + 512, :].rearrange("(t p) c -> p t c", p=P)
             )
 
-        load_e(0)
         load_w2(0, 0)
+        load_e(0)
         load_w2(0, 1)
-        load_e(1)
         load_w2(1, 0)
+        load_e(1)
         load_w2(1, 1)
         load_e(2)
         load_e(3)
         load_w3(0)
         load_w3(1)
 
-        nc.vector.memset(zero1[:], 0.0)
+        nc.gpsimd.memset(zero1[:], 0.0)
         nc.scalar.activation(out=junk1[:], in_=zero1[:], func=ACT.Gelu)
-        nc.vector.memset(vec_f32[:], 0.0)
         make_identity(nc, ident[:])
+        nc.gpsimd.memset(vec_f32[:], 0.0)
+        nc.gpsimd.tensor_copy(out=vec_f32[0:16, :], in_=vec_rows[:])
         nc.gpsimd.memset(pick[:], 0.0)
         nc.gpsimd.memset(pick[:, 0 : (NB - 1) * (P + 1) + 1 : P + 1], 1.0)
-        nc.vector.tensor_copy(out=vec_f32[0:16, :], in_=vec_rows[:])
+        for b in DIRECT:
+            nc.gpsimd.memset(pick_enc[b][:], 0.0)
 
-        def regroup(dst, src):
-            nc.vector.tensor_copy(
-                out=dst.rearrange("p (c i t) -> p c t i", i=4, t=4),
-                in_=src.rearrange("p t (c i) -> p c t i", i=4),
+        def regroup(engine_copy, dst, src, c0, c1):
+            engine_copy(
+                out=dst[:, 4 * c0 : 4 * c1].rearrange("p (c i t) -> p c t i", i=4, t=4),
+                in_=src[:, :, c0:c1].rearrange("p t (c i) -> p c t i", i=4),
             )
 
         def op_vecT(a, b):
@@ -160,7 +169,9 @@ def tile_fluxgnn1dlatent_pb_kernel(tc, edge_hid, u, enc, W2, b2, W3, b3, out):
             nc.tensor.transpose(bank["vec"][:], vec_f32[:], ident[:])
 
         def op_cols(a, b):
-            nc.vector.tensor_copy(out=cols[:], in_=bank["vec"][:, 0:16])
+            nc.scalar.copy(out=cols[:], in_=bank["vec"][:, 0:16])
+            for d in DIRECT:
+                nc.gpsimd.tensor_copy(out=pick_enc[d][:, d : 4 * P : P], in_=cols[:, 12:16])
 
         def op_ssum(a, b):
             bank["ssum"] = psum.tile([P, 1], F32, name="ssum", tag="g", bufs=1)
@@ -173,17 +184,23 @@ def tile_fluxgnn1dlatent_pb_kernel(tc, edge_hid, u, enc, W2, b2, W3, b3, out):
                     stop=(ct == 3),
                 )
 
-        def op_coef(a, b):
-            ssum = bank["ssum"]
-            nc.vector.tensor_scalar_add(out=den[:], in0=ssum[:], scalar1=1e-12)
+        def op_den(a, b):
+            nc.scalar.add(out=den[:], in_=bank["ssum"][:], add=1e-12)
+
+        def op_rinv(a, b):
             nc.vector.reciprocal(out=rinv[:], in_=den[:])
-            nc.vector.tensor_mul(out=c_u[:], in0=ssum[:], in1=rinv[:])
-            nc.vector.tensor_scalar_mul(out=c_pos[:], in0=rinv[:], scalar1=COEF)
-            nc.vector.tensor_scalar_mul(out=c_neg[:], in0=rinv[:], scalar1=-COEF)
-            nc.vector.tensor_scalar_mul(out=u_s[:], in0=u_bf[:], scalar1=c_u[0:NB, 0:1])
+
+        def op_coef(a, b):
+            nc.scalar.activation(out=c_u[:], in_=bank["ssum"][:], func=ACT.Copy, scale=rinv[:, 0:1])
+            nc.scalar.mul(out=c_pos[:], in_=rinv[:], mul=COEF)
+            nc.scalar.mul(out=c_neg[:], in_=rinv[:], mul=-COEF)
+            nc.scalar.activation(out=u_s[:], in_=u_bf[:], func=ACT.Copy, scale=c_u[0:NB, 0:1])
 
         def op_rW2(h, g):
-            regroup(w2_grp[h][:, g, :], w2_raw[h][:, 4 * g : 4 * g + 4, :])
+            regroup(nc.vector.tensor_copy, w2_grp[h][:, g, :], w2_raw[h][:, 4 * g : 4 * g + 4, :], 0, 512 - S_COLS.get((h, g), 0))
+
+        def op_sW2(h, g):
+            regroup(nc.scalar.copy, w2_grp[h][:, g, :], w2_raw[h][:, 4 * g : 4 * g + 4, :], 512 - S_COLS[(h, g)], 512)
 
         def op_qW2(h, g):
             nc.vector.quantize_mx(
@@ -191,7 +208,7 @@ def tile_fluxgnn1dlatent_pb_kernel(tc, edge_hid, u, enc, W2, b2, W3, b3, out):
             )
 
         def op_rW3(g, b):
-            regroup(w3_grp[g][:], w3_raw[g][:])
+            regroup(nc.vector.tensor_copy, w3_grp[g][:], w3_raw[g][:], 0, LD)
 
         def op_qW3(g, b):
             nc.vector.quantize_mx(out=w3_cod[g][:].bitcast(FP8X4), scales=w3_scl[g][:], in_=w3_grp[g][:])
@@ -213,12 +230,19 @@ def tile_fluxgnn1dlatent_pb_kernel(tc, edge_hid, u, enc, W2, b2, W3, b3, out):
 
         def op_qE(b, z):
             k, i = home[b]
-            for g in range(2):
+            if len(BLOCKS[k]) == 1:
                 nc.vector.quantize_mx(
-                    out=e_cod[k][:, g, NE * i : NE * i + NE].bitcast(FP8X4),
-                    scales=e_scl[k][:, g, NE * i : NE * i + NE],
-                    in_=e_grp[b][:, g, :],
+                    out=e_cod[k][:].rearrange("p g r -> p (g r)").bitcast(FP8X4),
+                    scales=e_scl[k][:].rearrange("p g r -> p (g r)"),
+                    in_=e_grp[b][:].rearrange("p g c -> p (g c)"),
                 )
+            else:
+                for g in range(2):
+                    nc.vector.quantize_mx(
+                        out=e_cod[k][:, g, NE * i : NE * i + NE].bitcast(FP8X4),
+                        scales=e_scl[k][:, g, NE * i : NE * i + NE],
+                        in_=e_grp[b][:, g, :],
+                    )
 
         def op_mm1(m, k):
             h, t = divmod(m, 4)
@@ -242,7 +266,7 @@ def tile_fluxgnn1dlatent_pb_kernel(tc, edge_hid, u, enc, W2, b2, W3, b3, out):
             )
 
         def op_rX(g, k):
-            regroup(x_grp[g][k][:], x_pln[g][k][:])
+            regroup(nc.vector.tensor_copy, x_grp[g][k][:], x_pln[g][k][:], 0, width[k])
 
         def op_qX(g, k):
             nc.vector.quantize_mx(out=x_cod[g][k][:].bitcast(FP8X4), scales=x_scl[g][k][:], in_=x_grp[g][k][:])
@@ -283,17 +307,18 @@ def tile_fluxgnn1dlatent_pb_kernel(tc, edge_hid, u, enc, W2, b2, W3, b3, out):
                     op1=ALU.add,
                 )
 
+        def add_to_gsum(op, lhsT, rhs):
+            if op == sums[0]:
+                bank["gsum"] = psum.tile([P, NE], F32, name="gsum", tag="g", bufs=1)
+            nc.tensor.matmul(out=bank["gsum"][:], lhsT=lhsT, rhs=rhs, start=(op == sums[0]), stop=(op == sums[-1]))
+
         def op_ws(b, z):
             k, i = home[b]
-            if b == 0:
-                bank["gsum"] = psum.tile([P, NE], F32, name="gsum", tag="g", bufs=1)
-            nc.tensor.matmul(
-                out=bank["gsum"][:],
-                lhsT=pick[:, P * b : P * b + P],
-                rhs=wsum[k][:, NE * i : NE * i + NE],
-                start=(b == 0),
-                stop=(b == NB - 1),
-            )
+            add_to_gsum(("ws", b, z), pick[:, P * b : P * b + P], wsum[k][:, NE * i : NE * i + NE])
+
+        def op_wsd(ct, b):
+            k, i = home[b]
+            add_to_gsum(("wsd", ct, b), pick_enc[b][:, P * ct : P * ct + P], t_sb[ct][k][:, NE * i : NE * i + NE])
 
         def op_f1(a, b):
             nc.vector.scalar_tensor_tensor(
@@ -306,11 +331,11 @@ def tile_fluxgnn1dlatent_pb_kernel(tc, edge_hid, u, enc, W2, b2, W3, b3, out):
             )
 
         ops = {
-            "vecT": op_vecT, "cols": op_cols, "ssum": op_ssum, "coef": op_coef,
-            "rW2": op_rW2, "qW2": op_qW2, "rW3": op_rW3, "qW3": op_qW3,
+            "vecT": op_vecT, "cols": op_cols, "ssum": op_ssum, "den": op_den, "rinv": op_rinv, "coef": op_coef,
+            "rW2": op_rW2, "sW2": op_sW2, "qW2": op_qW2, "rW3": op_rW3, "qW3": op_qW3,
             "tE": op_tE, "cE": op_cE, "qE": op_qE, "mm1": op_mm1, "gelu": op_gelu,
             "rX": op_rX, "qX": op_qX, "mm2a": op_mm2a, "mm2b": op_mm2b, "tanh": op_tanh,
-            "vs": op_vs, "ws": op_ws, "f1": op_f1, "f2": op_f2,
+            "vs": op_vs, "ws": op_ws, "wsd": op_wsd, "f1": op_f1, "f2": op_f2,
         }
         for name, a, b in ORDER:
             ops[name](a, b)

@@ -18,39 +18,41 @@ NC = 255
 HID = 1024
 LD = 512
 COEF = 0.5 * 0.25
-BLOCKS = ((0,), (1, 2,), (3,))
-DIRECT = (0, 3)
-S_COLS = {(0, 0): 208, (0, 1): 208}
+BLOCKS = ((0,), (1,), (2,), (3,),)
+VSUM = {0: (2, 3,), 1: (0, 1, 2, 3,), 2: (0, 1, 2, 3,), 3: (1, 2, 3,)}
+DIRECT = tuple(b for b in range(NB) if len(VSUM[b]) < 4)
+S_COLS = {(0, 0): 160, (0, 1): 160, (1, 0): 160}
 
 FLOPS = 2 * NB * NE * HID * HID + 2 * NB * NE * HID * LD
 
 ORDER = (
-    ("rW2", 0, 0), ("sW2", 0, 0), ("tE", 0, 0), ("qW2", 0, 0), ("tE", 0, 1), ("vecT", 0, 0),
-    ("rW2", 0, 1), ("sW2", 0, 1), ("cE", 0, 1), ("rW2", 1, 0), ("cE", 0, 0), ("cols", 0, 0),
-    ("tE", 1, 1), ("ssum", 0, 0), ("qW2", 0, 1), ("tE", 1, 0), ("qE", 0, 0), ("cE", 1, 1),
-    ("den", 0, 0), ("cE", 1, 0), ("qW2", 1, 0), ("rinv", 0, 0), ("mm1", 3, 0), ("mm1", 0, 0),
-    ("rW2", 1, 1), ("tE", 2, 0), ("gelu", 0, 0), ("gelu", 3, 0), ("tE", 2, 1), ("cE", 2, 0),
-    ("coef", 0, 0), ("qE", 1, 0), ("mm1", 2, 0), ("cE", 2, 1), ("mm1", 1, 0), ("tE", 3, 1),
-    ("qW2", 1, 1), ("gelu", 2, 0), ("gelu", 1, 0), ("tE", 3, 0), ("qE", 2, 0), ("cE", 3, 1),
-    ("mm1", 6, 0), ("cE", 3, 0), ("mm1", 4, 0), ("rW3", 1, 0), ("mm1", 2, 1), ("gelu", 4, 0),
-    ("mm1", 7, 0), ("gelu", 6, 0), ("mm1", 0, 1), ("qE", 3, 0), ("gelu", 2, 1), ("mm1", 3, 1),
-    ("gelu", 7, 0), ("rW3", 0, 0), ("gelu", 0, 1), ("mm1", 6, 2), ("mm1", 1, 1), ("gelu", 3, 1),
-    ("rX", 0, 0), ("mm1", 5, 0), ("gelu", 6, 2), ("mm1", 5, 1), ("gelu", 1, 1), ("qW3", 0, 0),
-    ("mm1", 1, 2), ("mm1", 5, 2), ("gelu", 5, 1), ("qX", 0, 0), ("mm1", 7, 1), ("qW3", 1, 0),
-    ("gelu", 5, 0), ("mm1", 4, 2), ("gelu", 1, 2), ("mm1", 6, 1), ("rX", 1, 0), ("gelu", 7, 1),
-    ("mm1", 4, 1), ("rX", 0, 1), ("gelu", 5, 2), ("gelu", 6, 1), ("mm2a", 3, 0), ("mm1", 3, 2),
-    ("gelu", 4, 2), ("qX", 1, 0), ("mm1", 0, 2), ("gelu", 3, 2), ("mm2a", 0, 0), ("qX", 0, 1),
-    ("gelu", 4, 1), ("mm2b", 3, 0), ("mm2a", 1, 0), ("mm2b", 0, 0), ("mm2b", 1, 0), ("tanh", 3, 0),
-    ("mm1", 2, 2), ("rX", 1, 1), ("gelu", 0, 2), ("mm1", 7, 2), ("tanh", 1, 0), ("wsd", 3, 0),
-    ("gelu", 7, 2), ("mm2a", 2, 0), ("tanh", 0, 0), ("mm2a", 0, 1), ("qX", 1, 1), ("gelu", 2, 2),
-    ("mm2a", 3, 1), ("mm2b", 2, 0), ("wsd", 1, 0), ("rX", 0, 2), ("tanh", 2, 0), ("mm2b", 0, 1),
-    ("mm2a", 1, 1), ("qX", 0, 2), ("tanh", 0, 1), ("mm2a", 2, 1), ("mm2b", 1, 1), ("rX", 1, 2),
-    ("wsd", 2, 0), ("tanh", 1, 1), ("mm2b", 2, 1), ("qX", 1, 2), ("mm2a", 2, 2), ("mm2b", 3, 1),
-    ("tanh", 2, 1), ("vs", 0, 1), ("mm2b", 2, 2), ("mm2a", 0, 2), ("vs", 1, 1), ("mm2a", 3, 2),
-    ("tanh", 2, 2), ("mm2b", 3, 2), ("wsd", 0, 0), ("tanh", 3, 1), ("vs", 2, 1), ("mm2a", 1, 2),
-    ("wsd", 2, 3), ("tanh", 3, 2), ("vs", 3, 1), ("mm2b", 0, 2), ("mm2b", 1, 2), ("wsd", 3, 3),
-    ("tanh", 0, 2), ("tanh", 1, 2), ("ws", 1, 0), ("ws", 2, 0), ("wsd", 0, 3), ("wsd", 1, 3),
-    ("f1", 0, 0), ("f2", 0, 0),
+    ("rW2", 0, 0), ("rW2", 0, 1), ("sW2", 0, 0), ("sW2", 0, 1), ("tE", 0, 0), ("tE", 0, 1), ("qW2", 0, 0),
+    ("qW2", 0, 1), ("rW2", 1, 0), ("cE", 0, 0), ("cE", 0, 1), ("sW2", 1, 0), ("vecT", 0, 0), ("tE", 1, 0),
+    ("qE", 0, 0), ("coef", 0, 0), ("rW2", 1, 1), ("qW2", 1, 0), ("cols", 0, 0), ("cE", 1, 0), ("tE", 1, 1),
+    ("mm1", 0, 0), ("mm1", 1, 0), ("mm1", 2, 0), ("mm1", 3, 0), ("tE", 2, 0), ("cE", 1, 1), ("gelu", 0, 0),
+    ("gelu", 1, 0), ("gelu", 2, 0), ("gelu", 3, 0), ("cE", 2, 0), ("tE", 2, 1), ("qE", 1, 0), ("qW2", 1, 1),
+    ("rX", 0, 0), ("cE", 2, 1), ("mm1", 0, 1), ("mm1", 1, 1), ("mm1", 2, 1), ("mm1", 3, 1), ("tE", 3, 0),
+    ("tE", 3, 1), ("mm1", 4, 0), ("qE", 2, 0), ("rW3", 0, 0), ("gelu", 0, 1), ("gelu", 1, 1), ("gelu", 2, 1),
+    ("gelu", 3, 1), ("cE", 3, 0), ("cE", 3, 1), ("gelu", 4, 0), ("mm1", 5, 0), ("mm1", 6, 0), ("mm1", 7, 0),
+    ("mm1", 0, 2), ("mm1", 1, 2), ("qE", 3, 0), ("rX", 0, 1), ("qX", 0, 0), ("gelu", 5, 0), ("gelu", 6, 0),
+    ("gelu", 7, 0), ("gelu", 0, 2), ("gelu", 1, 2), ("mm1", 2, 2), ("mm1", 3, 2), ("mm1", 4, 1), ("mm1", 5, 1),
+    ("mm1", 6, 1), ("rX", 1, 0), ("qX", 0, 1), ("rW3", 1, 0), ("qX", 1, 0), ("qW3", 0, 0), ("qW3", 1, 0),
+    ("gelu", 2, 2), ("gelu", 3, 2), ("gelu", 4, 1), ("gelu", 5, 1), ("gelu", 6, 1), ("mm1", 7, 1), ("mm1", 0, 3),
+    ("mm1", 1, 3), ("mm1", 2, 3), ("mm1", 3, 3), ("gelu", 7, 1), ("gelu", 0, 3), ("gelu", 1, 3), ("gelu", 2, 3),
+    ("gelu", 3, 3), ("mm1", 4, 2), ("mm1", 5, 2), ("mm1", 6, 2), ("mm1", 7, 2), ("mm1", 4, 3), ("rX", 1, 1),
+    ("rX", 0, 2), ("qX", 1, 1), ("rX", 0, 3), ("qX", 0, 2), ("gelu", 4, 2), ("gelu", 5, 2), ("gelu", 6, 2),
+    ("gelu", 7, 2), ("gelu", 4, 3), ("mm1", 5, 3), ("mm1", 6, 3), ("mm1", 7, 3), ("mm2a", 0, 0), ("mm2b", 0, 0),
+    ("mm2a", 1, 0), ("mm2b", 1, 0), ("rX", 1, 2), ("qX", 0, 3), ("gelu", 5, 3), ("gelu", 6, 3), ("gelu", 7, 3),
+    ("tanh", 0, 0), ("tanh", 1, 0), ("mm2a", 2, 0), ("mm2b", 2, 0), ("mm2a", 3, 0), ("mm2b", 3, 0), ("mm2a", 0, 1),
+    ("mm2b", 0, 1), ("mm2a", 1, 1), ("mm2b", 1, 1), ("mm2a", 2, 1), ("mm2b", 2, 1), ("rX", 1, 3), ("qX", 1, 2),
+    ("qX", 1, 3), ("tanh", 2, 0), ("tanh", 3, 0), ("tanh", 0, 1), ("tanh", 1, 1), ("tanh", 2, 1), ("mm2a", 3, 1),
+    ("mm2b", 3, 1), ("wsd", 0, 0), ("wsd", 1, 0), ("mm2a", 0, 2), ("mm2b", 0, 2), ("mm2a", 1, 2), ("mm2b", 1, 2),
+    ("mm2a", 2, 2), ("mm2b", 2, 2), ("mm2a", 3, 2), ("mm2b", 3, 2), ("vs", 2, 0), ("vs", 0, 1), ("vs", 3, 0),
+    ("vs", 1, 1), ("tanh", 3, 1), ("tanh", 0, 2), ("tanh", 1, 2), ("tanh", 2, 2), ("tanh", 3, 2), ("mm2a", 0, 3),
+    ("mm2b", 0, 3), ("mm2a", 1, 3), ("mm2b", 1, 3), ("mm2a", 2, 3), ("mm2b", 2, 3), ("mm2a", 3, 3), ("mm2b", 3, 3),
+    ("ws", 0, 0), ("vs", 0, 2), ("vs", 2, 1), ("vs", 1, 2), ("vs", 3, 1), ("vs", 2, 2), ("tanh", 0, 3),
+    ("tanh", 1, 3), ("tanh", 2, 3), ("tanh", 3, 3), ("wsd", 0, 3), ("ws", 1, 0), ("vs", 1, 3), ("vs", 3, 2),
+    ("vs", 2, 3), ("vs", 3, 3), ("ws", 2, 0), ("ws", 3, 0), ("f1", 0, 0), ("f2", 0, 0),
 )
 
 
@@ -108,15 +110,19 @@ def tile_fluxgnn1dlatent_pb_kernel(tc, edge_hid, u, enc, W2, b2, W3, b3, out):
         junk1 = keep.tile([P, 1], F32, name="junk1")
         u_bf = keep.tile([NB, NC], BF16, name="u_bf")
         u_s = keep.tile([NB, NC], F32, name="u_s")
-        den = keep.tile([P, 1], F32, name="den")
-        rinv = keep.tile([P, 1], F32, name="rinv")
-        c_u = keep.tile([P, 1], F32, name="c_u")
-        c_pos = keep.tile([P, 1], F32, name="c_pos")
-        c_neg = keep.tile([P, 1], F32, name="c_neg")
+        enc_rows = keep.tile([NB, LD], BF16, name="enc_rows")
+        enc_sq = keep.tile([NB, LD], F32, name="enc_sq")
+        ssum = keep.tile([NB, 1], F32, name="ssum")
+        den = keep.tile([NB, 1], F32, name="den")
+        rinv = keep.tile([NB, 1], F32, name="rinv")
+        c_u = keep.tile([NB, 1], F32, name="c_u")
+        c_pos = keep.tile([NB, 1], F32, name="c_pos")
+        c_neg = keep.tile([NB, 1], F32, name="c_neg")
         part = keep.tile([NB, NC], F32, name="part")
         res = keep.tile([NB, NC], F32, name="res")
         bank = {}
 
+        nc.scalar.dma_start(out=enc_rows[:], in_=enc.partition_broadcast(NB))
         nc.scalar.dma_start(out=vec_rows[0:8, :], in_=b2.rearrange("(j c) -> j c", c=P))
         nc.scalar.dma_start(out=vec_rows[8:12, :], in_=b3.rearrange("(j c) -> j c", c=P))
         nc.scalar.dma_start(out=vec_rows[12:16, :], in_=enc.rearrange("(j c) -> j c", c=P))
@@ -138,8 +144,8 @@ def tile_fluxgnn1dlatent_pb_kernel(tc, edge_hid, u, enc, W2, b2, W3, b3, out):
             )
 
         load_w2(0, 0)
-        load_e(0)
         load_w2(0, 1)
+        load_e(0)
         load_w2(1, 0)
         load_e(1)
         load_w2(1, 1)
@@ -157,6 +163,9 @@ def tile_fluxgnn1dlatent_pb_kernel(tc, edge_hid, u, enc, W2, b2, W3, b3, out):
         nc.gpsimd.memset(pick[:, 0 : (NB - 1) * (P + 1) + 1 : P + 1], 1.0)
         for b in DIRECT:
             nc.gpsimd.memset(pick_enc[b][:], 0.0)
+        nc.vector.scalar_tensor_tensor(
+            out=enc_sq[:], in0=enc_rows[:], scalar=1.0, in1=enc_rows[:], op0=ALU.mult, op1=ALU.mult, accum_out=ssum[:]
+        )
 
         def regroup(engine_copy, dst, src, c0, c1):
             engine_copy(
@@ -173,28 +182,13 @@ def tile_fluxgnn1dlatent_pb_kernel(tc, edge_hid, u, enc, W2, b2, W3, b3, out):
             for d in DIRECT:
                 nc.gpsimd.tensor_copy(out=pick_enc[d][:, d : 4 * P : P], in_=cols[:, 12:16])
 
-        def op_ssum(a, b):
-            bank["ssum"] = psum.tile([P, 1], F32, name="ssum", tag="g", bufs=1)
-            for ct in range(4):
-                nc.tensor.matmul(
-                    out=bank["ssum"][:],
-                    lhsT=cols[:, 12 + ct : 13 + ct].to_broadcast([P, P]),
-                    rhs=cols[:, 12 + ct : 13 + ct],
-                    start=(ct == 0),
-                    stop=(ct == 3),
-                )
-
-        def op_den(a, b):
-            nc.scalar.add(out=den[:], in_=bank["ssum"][:], add=1e-12)
-
-        def op_rinv(a, b):
-            nc.vector.reciprocal(out=rinv[:], in_=den[:])
-
         def op_coef(a, b):
-            nc.scalar.activation(out=c_u[:], in_=bank["ssum"][:], func=ACT.Copy, scale=rinv[:, 0:1])
-            nc.scalar.mul(out=c_pos[:], in_=rinv[:], mul=COEF)
-            nc.scalar.mul(out=c_neg[:], in_=rinv[:], mul=-COEF)
-            nc.scalar.activation(out=u_s[:], in_=u_bf[:], func=ACT.Copy, scale=c_u[0:NB, 0:1])
+            nc.gpsimd.tensor_scalar_add(out=den[:], in0=ssum[:], scalar1=1e-12)
+            nc.vector.reciprocal(out=rinv[:], in_=den[:])
+            nc.gpsimd.tensor_scalar_mul(out=c_u[:], in0=ssum[:], scalar1=rinv[:, 0:1])
+            nc.gpsimd.tensor_scalar_mul(out=c_pos[:], in0=rinv[:], scalar1=COEF)
+            nc.gpsimd.tensor_scalar_mul(out=c_neg[:], in0=rinv[:], scalar1=-COEF)
+            nc.gpsimd.tensor_scalar_mul(out=u_s[:], in0=u_bf[:], scalar1=c_u[:, 0:1])
 
         def op_rW2(h, g):
             regroup(nc.vector.tensor_copy, w2_grp[h][:, g, :], w2_raw[h][:, 4 * g : 4 * g + 4, :], 0, 512 - S_COLS.get((h, g), 0))
@@ -295,8 +289,8 @@ def tile_fluxgnn1dlatent_pb_kernel(tc, edge_hid, u, enc, W2, b2, W3, b3, out):
             )
 
         def op_vs(ct, k):
-            if ct == 0:
-                nc.vector.tensor_scalar_mul(out=wsum[k][:], in0=t_sb[ct][k][:], scalar1=cols[:, 12:13])
+            if ct == VSUM[BLOCKS[k][0]][0]:
+                nc.vector.tensor_scalar_mul(out=wsum[k][:], in0=t_sb[ct][k][:], scalar1=cols[:, 12 + ct : 13 + ct])
             else:
                 nc.vector.scalar_tensor_tensor(
                     out=wsum[k][:],
@@ -322,16 +316,16 @@ def tile_fluxgnn1dlatent_pb_kernel(tc, edge_hid, u, enc, W2, b2, W3, b3, out):
 
         def op_f1(a, b):
             nc.vector.scalar_tensor_tensor(
-                out=part[:], in0=bank["gsum"][0:NB, 0:NC], scalar=c_pos[0:NB, 0:1], in1=u_s[:], op0=ALU.mult, op1=ALU.add
+                out=part[:], in0=bank["gsum"][0:NB, 0:NC], scalar=c_pos[:, 0:1], in1=u_s[:], op0=ALU.mult, op1=ALU.add
             )
 
         def op_f2(a, b):
             nc.vector.scalar_tensor_tensor(
-                out=res[:], in0=bank["gsum"][0:NB, 1:NE], scalar=c_neg[0:NB, 0:1], in1=part[:], op0=ALU.mult, op1=ALU.add
+                out=res[:], in0=bank["gsum"][0:NB, 1:NE], scalar=c_neg[:, 0:1], in1=part[:], op0=ALU.mult, op1=ALU.add
             )
 
         ops = {
-            "vecT": op_vecT, "cols": op_cols, "ssum": op_ssum, "den": op_den, "rinv": op_rinv, "coef": op_coef,
+            "vecT": op_vecT, "cols": op_cols, "coef": op_coef,
             "rW2": op_rW2, "sW2": op_sW2, "qW2": op_qW2, "rW3": op_rW3, "qW3": op_qW3,
             "tE": op_tE, "cE": op_cE, "qE": op_qE, "mm1": op_mm1, "gelu": op_gelu,
             "rX": op_rX, "qX": op_qX, "mm2a": op_mm2a, "mm2b": op_mm2b, "tanh": op_tanh,

@@ -26,33 +26,33 @@ S_COLS = {(0, 0): 160, (0, 1): 160, (1, 0): 160}
 FLOPS = 2 * NB * NE * HID * HID + 2 * NB * NE * HID * LD
 
 ORDER = (
-    ("rW2", 0, 0), ("rW2", 0, 1), ("sW2", 0, 0), ("sW2", 0, 1), ("tE", 0, 0), ("tE", 0, 1), ("qW2", 0, 0),
-    ("qW2", 0, 1), ("rW2", 1, 0), ("cE", 0, 0), ("cE", 0, 1), ("sW2", 1, 0), ("vecT", 0, 0), ("tE", 1, 0),
-    ("qE", 0, 0), ("coef", 0, 0), ("rW2", 1, 1), ("qW2", 1, 0), ("cols", 0, 0), ("cE", 1, 0), ("tE", 1, 1),
+    ("rW2", 0, 0), ("rW2", 0, 1), ("den", 0, 0), ("sW2", 0, 0), ("sW2", 0, 1), ("tE", 0, 0), ("tE", 0, 1),
+    ("qW2", 0, 0), ("qW2", 0, 1), ("rW2", 1, 0), ("cE", 0, 0), ("cE", 0, 1), ("sW2", 1, 0), ("vecT", 0, 0),
+    ("tE", 1, 0), ("qE", 0, 0), ("rW2", 1, 1), ("qW2", 1, 0), ("cols", 0, 0), ("cE", 1, 0), ("tE", 1, 1),
     ("mm1", 0, 0), ("mm1", 1, 0), ("mm1", 2, 0), ("mm1", 3, 0), ("tE", 2, 0), ("cE", 1, 1), ("gelu", 0, 0),
     ("gelu", 1, 0), ("gelu", 2, 0), ("gelu", 3, 0), ("cE", 2, 0), ("tE", 2, 1), ("qE", 1, 0), ("qW2", 1, 1),
     ("rX", 0, 0), ("cE", 2, 1), ("mm1", 0, 1), ("mm1", 1, 1), ("mm1", 2, 1), ("mm1", 3, 1), ("tE", 3, 0),
     ("tE", 3, 1), ("mm1", 4, 0), ("qE", 2, 0), ("rW3", 0, 0), ("gelu", 0, 1), ("gelu", 1, 1), ("gelu", 2, 1),
     ("gelu", 3, 1), ("cE", 3, 0), ("cE", 3, 1), ("gelu", 4, 0), ("mm1", 5, 0), ("mm1", 6, 0), ("mm1", 7, 0),
-    ("mm1", 0, 2), ("mm1", 1, 2), ("qE", 3, 0), ("rX", 0, 1), ("qX", 0, 0), ("gelu", 5, 0), ("gelu", 6, 0),
-    ("gelu", 7, 0), ("gelu", 0, 2), ("gelu", 1, 2), ("mm1", 2, 2), ("mm1", 3, 2), ("mm1", 4, 1), ("mm1", 5, 1),
-    ("mm1", 6, 1), ("rX", 1, 0), ("qX", 0, 1), ("rW3", 1, 0), ("qX", 1, 0), ("qW3", 0, 0), ("qW3", 1, 0),
-    ("gelu", 2, 2), ("gelu", 3, 2), ("gelu", 4, 1), ("gelu", 5, 1), ("gelu", 6, 1), ("mm1", 7, 1), ("mm1", 0, 3),
-    ("mm1", 1, 3), ("mm1", 2, 3), ("mm1", 3, 3), ("gelu", 7, 1), ("gelu", 0, 3), ("gelu", 1, 3), ("gelu", 2, 3),
-    ("gelu", 3, 3), ("mm1", 4, 2), ("mm1", 5, 2), ("mm1", 6, 2), ("mm1", 7, 2), ("mm1", 4, 3), ("rX", 1, 1),
-    ("rX", 0, 2), ("qX", 1, 1), ("rX", 0, 3), ("qX", 0, 2), ("gelu", 4, 2), ("gelu", 5, 2), ("gelu", 6, 2),
-    ("gelu", 7, 2), ("gelu", 4, 3), ("mm1", 5, 3), ("mm1", 6, 3), ("mm1", 7, 3), ("mm2a", 0, 0), ("mm2b", 0, 0),
-    ("mm2a", 1, 0), ("mm2b", 1, 0), ("rX", 1, 2), ("qX", 0, 3), ("gelu", 5, 3), ("gelu", 6, 3), ("gelu", 7, 3),
-    ("tanh", 0, 0), ("tanh", 1, 0), ("mm2a", 2, 0), ("mm2b", 2, 0), ("mm2a", 3, 0), ("mm2b", 3, 0), ("mm2a", 0, 1),
-    ("mm2b", 0, 1), ("mm2a", 1, 1), ("mm2b", 1, 1), ("mm2a", 2, 1), ("mm2b", 2, 1), ("rX", 1, 3), ("qX", 1, 2),
-    ("qX", 1, 3), ("tanh", 2, 0), ("tanh", 3, 0), ("tanh", 0, 1), ("tanh", 1, 1), ("tanh", 2, 1), ("mm2a", 3, 1),
-    ("mm2b", 3, 1), ("wsd", 0, 0), ("wsd", 1, 0), ("mm2a", 0, 2), ("mm2b", 0, 2), ("mm2a", 1, 2), ("mm2b", 1, 2),
-    ("mm2a", 2, 2), ("mm2b", 2, 2), ("mm2a", 3, 2), ("mm2b", 3, 2), ("vs", 2, 0), ("vs", 0, 1), ("vs", 3, 0),
-    ("vs", 1, 1), ("tanh", 3, 1), ("tanh", 0, 2), ("tanh", 1, 2), ("tanh", 2, 2), ("tanh", 3, 2), ("mm2a", 0, 3),
-    ("mm2b", 0, 3), ("mm2a", 1, 3), ("mm2b", 1, 3), ("mm2a", 2, 3), ("mm2b", 2, 3), ("mm2a", 3, 3), ("mm2b", 3, 3),
-    ("ws", 0, 0), ("vs", 0, 2), ("vs", 2, 1), ("vs", 1, 2), ("vs", 3, 1), ("vs", 2, 2), ("tanh", 0, 3),
-    ("tanh", 1, 3), ("tanh", 2, 3), ("tanh", 3, 3), ("wsd", 0, 3), ("ws", 1, 0), ("vs", 1, 3), ("vs", 3, 2),
-    ("vs", 2, 3), ("vs", 3, 3), ("ws", 2, 0), ("ws", 3, 0), ("f1", 0, 0), ("f2", 0, 0),
+    ("mm1", 0, 2), ("mm1", 1, 2), ("qE", 3, 0), ("rX", 0, 1), ("rinv", 0, 0), ("qX", 0, 0), ("gelu", 5, 0),
+    ("gelu", 6, 0), ("gelu", 7, 0), ("gelu", 0, 2), ("gelu", 1, 2), ("mm1", 2, 2), ("mm1", 3, 2), ("mm1", 4, 1),
+    ("mm1", 5, 1), ("mm1", 6, 1), ("rX", 1, 0), ("qX", 0, 1), ("rW3", 1, 0), ("qX", 1, 0), ("qW3", 0, 0),
+    ("qW3", 1, 0), ("gelu", 2, 2), ("gelu", 3, 2), ("gelu", 4, 1), ("gelu", 5, 1), ("gelu", 6, 1), ("mm1", 7, 1),
+    ("mm1", 0, 3), ("mm1", 1, 3), ("mm1", 2, 3), ("mm1", 3, 3), ("gelu", 7, 1), ("gelu", 0, 3), ("gelu", 1, 3),
+    ("gelu", 2, 3), ("gelu", 3, 3), ("mm1", 4, 2), ("mm1", 5, 2), ("mm1", 6, 2), ("mm1", 7, 2), ("mm1", 4, 3),
+    ("rX", 1, 1), ("rX", 0, 2), ("qX", 1, 1), ("rX", 0, 3), ("qX", 0, 2), ("gelu", 4, 2), ("gelu", 5, 2),
+    ("gelu", 6, 2), ("gelu", 7, 2), ("gelu", 4, 3), ("mm1", 5, 3), ("mm1", 6, 3), ("mm1", 7, 3), ("mm2a", 0, 0),
+    ("mm2b", 0, 0), ("mm2a", 1, 0), ("mm2b", 1, 0), ("rX", 1, 2), ("qX", 0, 3), ("gelu", 5, 3), ("gelu", 6, 3),
+    ("gelu", 7, 3), ("tanh", 0, 0), ("tanh", 1, 0), ("mm2a", 2, 0), ("mm2b", 2, 0), ("mm2a", 3, 0), ("mm2b", 3, 0),
+    ("mm2a", 0, 1), ("mm2b", 0, 1), ("mm2a", 1, 1), ("mm2b", 1, 1), ("mm2a", 2, 1), ("mm2b", 2, 1), ("rX", 1, 3),
+    ("qX", 1, 2), ("qX", 1, 3), ("tanh", 2, 0), ("tanh", 3, 0), ("tanh", 0, 1), ("tanh", 1, 1), ("tanh", 2, 1),
+    ("mm2a", 3, 1), ("mm2b", 3, 1), ("wsd", 0, 0), ("wsd", 1, 0), ("mm2a", 0, 2), ("mm2b", 0, 2), ("mm2a", 1, 2),
+    ("mm2b", 1, 2), ("mm2a", 2, 2), ("mm2b", 2, 2), ("mm2a", 3, 2), ("mm2b", 3, 2), ("vs", 2, 0), ("vs", 0, 1),
+    ("vs", 3, 0), ("vs", 1, 1), ("tanh", 3, 1), ("coef", 0, 0), ("tanh", 0, 2), ("tanh", 1, 2), ("tanh", 2, 2),
+    ("tanh", 3, 2), ("mm2a", 0, 3), ("mm2b", 0, 3), ("mm2a", 1, 3), ("mm2b", 1, 3), ("mm2a", 2, 3), ("mm2b", 2, 3),
+    ("mm2a", 3, 3), ("mm2b", 3, 3), ("ws", 0, 0), ("vs", 0, 2), ("vs", 2, 1), ("vs", 1, 2), ("vs", 3, 1),
+    ("vs", 2, 2), ("tanh", 0, 3), ("tanh", 1, 3), ("tanh", 2, 3), ("tanh", 3, 3), ("wsd", 0, 3), ("ws", 1, 0),
+    ("vs", 1, 3), ("vs", 3, 2), ("vs", 2, 3), ("vs", 3, 3), ("ws", 2, 0), ("ws", 3, 0), ("f1", 0, 0), ("f2", 0, 0),
 )
 
 
@@ -122,12 +122,6 @@ def tile_fluxgnn1dlatent_pb_kernel(tc, edge_hid, u, enc, W2, b2, W3, b3, out):
         res = keep.tile([NB, NC], F32, name="res")
         bank = {}
 
-        nc.scalar.dma_start(out=enc_rows[:], in_=enc.partition_broadcast(NB))
-        nc.scalar.dma_start(out=vec_rows[0:8, :], in_=b2.rearrange("(j c) -> j c", c=P))
-        nc.scalar.dma_start(out=vec_rows[8:12, :], in_=b3.rearrange("(j c) -> j c", c=P))
-        nc.scalar.dma_start(out=vec_rows[12:16, :], in_=enc.rearrange("(j c) -> j c", c=P))
-        nc.scalar.dma_start(out=u_bf[:], in_=u)
-
         def load_w2(h, g):
             for j in (2 * g, 2 * g + 1):
                 nc.sync.dma_start(
@@ -143,6 +137,7 @@ def tile_fluxgnn1dlatent_pb_kernel(tc, edge_hid, u, enc, W2, b2, W3, b3, out):
                 out=w3_raw[g][:], in_=W3[512 * g : 512 * g + 512, :].rearrange("(t p) c -> p t c", p=P)
             )
 
+        nc.sync.dma_start(out=enc_rows[:], in_=enc.partition_broadcast(NB))
         load_w2(0, 0)
         load_w2(0, 1)
         load_e(0)
@@ -154,15 +149,19 @@ def tile_fluxgnn1dlatent_pb_kernel(tc, edge_hid, u, enc, W2, b2, W3, b3, out):
         load_w3(0)
         load_w3(1)
 
-        nc.gpsimd.memset(zero1[:], 0.0)
+        nc.vector.memset(zero1[:], 0.0)
+        nc.vector.memset(vec_f32[:], 0.0)
         nc.scalar.activation(out=junk1[:], in_=zero1[:], func=ACT.Gelu)
+        nc.gpsimd.dma_start(out=vec_rows[0:8, :], in_=b2.rearrange("(j c) -> j c", c=P))
+        nc.gpsimd.dma_start(out=vec_rows[8:12, :], in_=b3.rearrange("(j c) -> j c", c=P))
+        nc.gpsimd.dma_start(out=vec_rows[12:16, :], in_=enc.rearrange("(j c) -> j c", c=P))
         make_identity(nc, ident[:])
-        nc.gpsimd.memset(vec_f32[:], 0.0)
+        nc.gpsimd.dma_start(out=u_bf[:], in_=u)
         nc.gpsimd.tensor_copy(out=vec_f32[0:16, :], in_=vec_rows[:])
-        nc.gpsimd.memset(pick[:], 0.0)
-        nc.gpsimd.memset(pick[:, 0 : (NB - 1) * (P + 1) + 1 : P + 1], 1.0)
+        nc.vector.memset(pick[:], 0.0)
+        nc.vector.memset(pick[:, 0 : (NB - 1) * (P + 1) + 1 : P + 1], 1.0)
         for b in DIRECT:
-            nc.gpsimd.memset(pick_enc[b][:], 0.0)
+            nc.vector.memset(pick_enc[b][:], 0.0)
         nc.vector.scalar_tensor_tensor(
             out=enc_sq[:], in0=enc_rows[:], scalar=1.0, in1=enc_rows[:], op0=ALU.mult, op1=ALU.mult, accum_out=ssum[:]
         )
@@ -182,13 +181,17 @@ def tile_fluxgnn1dlatent_pb_kernel(tc, edge_hid, u, enc, W2, b2, W3, b3, out):
             for d in DIRECT:
                 nc.gpsimd.tensor_copy(out=pick_enc[d][:, d : 4 * P : P], in_=cols[:, 12:16])
 
-        def op_coef(a, b):
-            nc.gpsimd.tensor_scalar_add(out=den[:], in0=ssum[:], scalar1=1e-12)
+        def op_den(a, b):
+            nc.vector.tensor_scalar_add(out=den[:], in0=ssum[:], scalar1=1e-12)
+
+        def op_rinv(a, b):
             nc.vector.reciprocal(out=rinv[:], in_=den[:])
-            nc.gpsimd.tensor_scalar_mul(out=c_u[:], in0=ssum[:], scalar1=rinv[:, 0:1])
-            nc.gpsimd.tensor_scalar_mul(out=c_pos[:], in0=rinv[:], scalar1=COEF)
-            nc.gpsimd.tensor_scalar_mul(out=c_neg[:], in0=rinv[:], scalar1=-COEF)
-            nc.gpsimd.tensor_scalar_mul(out=u_s[:], in0=u_bf[:], scalar1=c_u[:, 0:1])
+
+        def op_coef(a, b):
+            nc.scalar.activation(out=c_u[:], in_=ssum[:], func=ACT.Copy, scale=rinv[:, 0:1])
+            nc.scalar.mul(out=c_pos[:], in_=rinv[:], mul=COEF)
+            nc.scalar.mul(out=c_neg[:], in_=rinv[:], mul=-COEF)
+            nc.scalar.activation(out=u_s[:], in_=u_bf[:], func=ACT.Copy, scale=c_u[:, 0:1])
 
         def op_rW2(h, g):
             regroup(nc.vector.tensor_copy, w2_grp[h][:, g, :], w2_raw[h][:, 4 * g : 4 * g + 4, :], 0, 512 - S_COLS.get((h, g), 0))
@@ -325,7 +328,7 @@ def tile_fluxgnn1dlatent_pb_kernel(tc, edge_hid, u, enc, W2, b2, W3, b3, out):
             )
 
         ops = {
-            "vecT": op_vecT, "cols": op_cols, "coef": op_coef,
+            "vecT": op_vecT, "cols": op_cols, "den": op_den, "rinv": op_rinv, "coef": op_coef,
             "rW2": op_rW2, "sW2": op_sW2, "qW2": op_qW2, "rW3": op_rW3, "qW3": op_qW3,
             "tE": op_tE, "cE": op_cE, "qE": op_qE, "mm1": op_mm1, "gelu": op_gelu,
             "rX": op_rX, "qX": op_qX, "mm2a": op_mm2a, "mm2b": op_mm2b, "tanh": op_tanh,

@@ -138,6 +138,9 @@ def tile_fluxgnn1dlatent_pb_kernel(tc, edge_hid, u, enc, W2, b2, W3, b3, out):
             )
 
         nc.sync.dma_start(out=enc_rows[:], in_=enc.partition_broadcast(NB))
+        nc.scalar.dma_start(out=vec_rows[0:8, :], in_=b2.rearrange("(j c) -> j c", c=P))
+        nc.scalar.dma_start(out=vec_rows[8:12, :], in_=b3.rearrange("(j c) -> j c", c=P))
+        nc.scalar.dma_start(out=vec_rows[12:16, :], in_=enc.rearrange("(j c) -> j c", c=P))
         load_w2(0, 0)
         load_w2(0, 1)
         load_e(0)
@@ -148,15 +151,12 @@ def tile_fluxgnn1dlatent_pb_kernel(tc, edge_hid, u, enc, W2, b2, W3, b3, out):
         load_e(3)
         load_w3(0)
         load_w3(1)
+        nc.sync.dma_start(out=u_bf[:], in_=u)
 
         nc.vector.memset(zero1[:], 0.0)
         nc.vector.memset(vec_f32[:], 0.0)
         nc.scalar.activation(out=junk1[:], in_=zero1[:], func=ACT.Gelu)
-        nc.gpsimd.dma_start(out=vec_rows[0:8, :], in_=b2.rearrange("(j c) -> j c", c=P))
-        nc.gpsimd.dma_start(out=vec_rows[8:12, :], in_=b3.rearrange("(j c) -> j c", c=P))
-        nc.gpsimd.dma_start(out=vec_rows[12:16, :], in_=enc.rearrange("(j c) -> j c", c=P))
         make_identity(nc, ident[:])
-        nc.gpsimd.dma_start(out=u_bf[:], in_=u)
         nc.gpsimd.tensor_copy(out=vec_f32[0:16, :], in_=vec_rows[:])
         nc.vector.memset(pick[:], 0.0)
         nc.vector.memset(pick[:, 0 : (NB - 1) * (P + 1) + 1 : P + 1], 1.0)

@@ -19,39 +19,41 @@ HID = 1024
 LD = 512
 COEF = 0.5 * 0.25
 BLOCKS = ((0,), (1,), (2,), (3,),)
-VSUM = {0: (2, 3,), 1: (0, 1, 2, 3,), 2: (0, 1, 2, 3,), 3: (1, 2, 3,)}
+VSUM = {0: (0, 1, 2, 3,), 1: (0, 1, 2, 3,), 2: (0, 1, 2, 3,), 3: (1, 2, 3,)}
 DIRECT = tuple(b for b in range(NB) if len(VSUM[b]) < 4)
-S_COLS = {(0, 0): 160, (0, 1): 160, (1, 0): 160}
+S_COLS = {(0, 0): 160, (0, 1): 140}
+
+S3_COLS = {0: 192, 1: 192}
 
 FLOPS = 2 * NB * NE * HID * HID + 2 * NB * NE * HID * LD
 
 ORDER = (
-    ("rW2", 0, 0), ("rW2", 0, 1), ("den", 0, 0), ("sW2", 0, 0), ("sW2", 0, 1), ("tE", 0, 0), ("tE", 0, 1),
-    ("qW2", 0, 0), ("qW2", 0, 1), ("rW2", 1, 0), ("cE", 0, 0), ("cE", 0, 1), ("sW2", 1, 0), ("vecT", 0, 0),
-    ("tE", 1, 0), ("qE", 0, 0), ("rW2", 1, 1), ("qW2", 1, 0), ("cols", 0, 0), ("cE", 1, 0), ("tE", 1, 1),
-    ("mm1", 0, 0), ("mm1", 1, 0), ("mm1", 2, 0), ("mm1", 3, 0), ("tE", 2, 0), ("cE", 1, 1), ("gelu", 0, 0),
-    ("gelu", 1, 0), ("gelu", 2, 0), ("gelu", 3, 0), ("cE", 2, 0), ("tE", 2, 1), ("qE", 1, 0), ("qW2", 1, 1),
-    ("rX", 0, 0), ("cE", 2, 1), ("mm1", 0, 1), ("mm1", 1, 1), ("mm1", 2, 1), ("mm1", 3, 1), ("tE", 3, 0),
-    ("tE", 3, 1), ("mm1", 4, 0), ("qE", 2, 0), ("rW3", 0, 0), ("gelu", 0, 1), ("gelu", 1, 1), ("gelu", 2, 1),
-    ("gelu", 3, 1), ("cE", 3, 0), ("cE", 3, 1), ("gelu", 4, 0), ("mm1", 5, 0), ("mm1", 6, 0), ("mm1", 7, 0),
-    ("mm1", 0, 2), ("mm1", 1, 2), ("qE", 3, 0), ("rX", 0, 1), ("rinv", 0, 0), ("qX", 0, 0), ("gelu", 5, 0),
-    ("gelu", 6, 0), ("gelu", 7, 0), ("gelu", 0, 2), ("gelu", 1, 2), ("mm1", 2, 2), ("mm1", 3, 2), ("mm1", 4, 1),
-    ("mm1", 5, 1), ("mm1", 6, 1), ("rX", 1, 0), ("qX", 0, 1), ("rW3", 1, 0), ("qX", 1, 0), ("qW3", 0, 0),
-    ("qW3", 1, 0), ("gelu", 2, 2), ("gelu", 3, 2), ("gelu", 4, 1), ("gelu", 5, 1), ("gelu", 6, 1), ("mm1", 7, 1),
-    ("mm1", 0, 3), ("mm1", 1, 3), ("mm1", 2, 3), ("mm1", 3, 3), ("gelu", 7, 1), ("gelu", 0, 3), ("gelu", 1, 3),
-    ("gelu", 2, 3), ("gelu", 3, 3), ("mm1", 4, 2), ("mm1", 5, 2), ("mm1", 6, 2), ("mm1", 7, 2), ("mm1", 4, 3),
-    ("rX", 1, 1), ("rX", 0, 2), ("qX", 1, 1), ("rX", 0, 3), ("qX", 0, 2), ("gelu", 4, 2), ("gelu", 5, 2),
-    ("gelu", 6, 2), ("gelu", 7, 2), ("gelu", 4, 3), ("mm1", 5, 3), ("mm1", 6, 3), ("mm1", 7, 3), ("mm2a", 0, 0),
-    ("mm2b", 0, 0), ("mm2a", 1, 0), ("mm2b", 1, 0), ("rX", 1, 2), ("qX", 0, 3), ("gelu", 5, 3), ("gelu", 6, 3),
-    ("gelu", 7, 3), ("tanh", 0, 0), ("tanh", 1, 0), ("mm2a", 2, 0), ("mm2b", 2, 0), ("mm2a", 3, 0), ("mm2b", 3, 0),
-    ("mm2a", 0, 1), ("mm2b", 0, 1), ("mm2a", 1, 1), ("mm2b", 1, 1), ("mm2a", 2, 1), ("mm2b", 2, 1), ("rX", 1, 3),
-    ("qX", 1, 2), ("qX", 1, 3), ("tanh", 2, 0), ("tanh", 3, 0), ("tanh", 0, 1), ("tanh", 1, 1), ("tanh", 2, 1),
-    ("mm2a", 3, 1), ("mm2b", 3, 1), ("wsd", 0, 0), ("wsd", 1, 0), ("mm2a", 0, 2), ("mm2b", 0, 2), ("mm2a", 1, 2),
-    ("mm2b", 1, 2), ("mm2a", 2, 2), ("mm2b", 2, 2), ("mm2a", 3, 2), ("mm2b", 3, 2), ("vs", 2, 0), ("vs", 0, 1),
-    ("vs", 3, 0), ("vs", 1, 1), ("tanh", 3, 1), ("coef", 0, 0), ("tanh", 0, 2), ("tanh", 1, 2), ("tanh", 2, 2),
-    ("tanh", 3, 2), ("mm2a", 0, 3), ("mm2b", 0, 3), ("mm2a", 1, 3), ("mm2b", 1, 3), ("mm2a", 2, 3), ("mm2b", 2, 3),
-    ("mm2a", 3, 3), ("mm2b", 3, 3), ("ws", 0, 0), ("vs", 0, 2), ("vs", 2, 1), ("vs", 1, 2), ("vs", 3, 1),
-    ("vs", 2, 2), ("tanh", 0, 3), ("tanh", 1, 3), ("tanh", 2, 3), ("tanh", 3, 3), ("wsd", 0, 3), ("ws", 1, 0),
+    ("rW2", 0, 0), ("den", 0, 0), ("sW2", 0, 0), ("tE", 0, 0), ("tE", 0, 1), ("vecT", 0, 0), ("qW2", 0, 0),
+    ("rinv", 0, 0), ("rW2", 0, 1), ("cE", 0, 0), ("cE", 0, 1), ("sW2", 0, 1), ("cols", 0, 0), ("coef", 0, 0),
+    ("tE", 1, 0), ("tE", 1, 1), ("qE", 0, 0), ("qW2", 0, 1), ("rW2", 1, 0), ("cE", 1, 0), ("cE", 1, 1), ("mm1", 0, 0),
+    ("mm1", 1, 0), ("mm1", 2, 0), ("mm1", 3, 0), ("tE", 2, 0), ("tE", 2, 1), ("qE", 1, 0), ("qW2", 1, 0),
+    ("rW2", 1, 1), ("gelu", 0, 0), ("gelu", 1, 0), ("gelu", 2, 0), ("gelu", 3, 0), ("cE", 2, 0), ("cE", 2, 1),
+    ("mm1", 0, 1), ("mm1", 1, 1), ("mm1", 2, 1), ("mm1", 3, 1), ("tE", 3, 0), ("tE", 3, 1), ("rX", 0, 0),
+    ("qW2", 1, 1), ("qE", 2, 0), ("gelu", 0, 1), ("gelu", 1, 1), ("gelu", 2, 1), ("gelu", 3, 1), ("cE", 3, 0),
+    ("cE", 3, 1), ("mm1", 4, 0), ("mm1", 5, 0), ("mm1", 6, 0), ("mm1", 7, 0), ("mm1", 0, 2), ("rX", 0, 1),
+    ("qE", 3, 0), ("qX", 0, 0), ("gelu", 4, 0), ("gelu", 5, 0), ("gelu", 6, 0), ("gelu", 7, 0), ("sW3", 0, 0),
+    ("gelu", 0, 2), ("mm1", 1, 2), ("mm1", 2, 2), ("mm1", 3, 2), ("mm1", 4, 1), ("mm1", 5, 1), ("rX", 1, 0),
+    ("qX", 0, 1), ("rW3", 0, 0), ("qX", 1, 0), ("rW3", 1, 0), ("qW3", 0, 0), ("gelu", 1, 2), ("gelu", 2, 2),
+    ("gelu", 3, 2), ("gelu", 4, 1), ("gelu", 5, 1), ("mm1", 6, 1), ("mm1", 7, 1), ("mm1", 4, 2), ("mm1", 5, 2),
+    ("mm1", 6, 2), ("rX", 0, 2), ("gelu", 6, 1), ("gelu", 7, 1), ("sW3", 1, 0), ("gelu", 4, 2), ("gelu", 5, 2),
+    ("gelu", 6, 2), ("mm1", 7, 2), ("mm1", 0, 3), ("mm1", 1, 3), ("mm1", 2, 3), ("mm1", 3, 3), ("qW3", 1, 0),
+    ("rX", 1, 1), ("qX", 0, 2), ("gelu", 7, 2), ("gelu", 0, 3), ("gelu", 1, 3), ("gelu", 2, 3), ("gelu", 3, 3),
+    ("mm1", 4, 3), ("mm1", 5, 3), ("mm1", 6, 3), ("mm1", 7, 3), ("mm2a", 0, 0), ("mm2b", 0, 0), ("rX", 1, 2),
+    ("qX", 1, 1), ("rX", 0, 3), ("qX", 1, 2), ("gelu", 4, 3), ("gelu", 5, 3), ("gelu", 6, 3), ("gelu", 7, 3),
+    ("tanh", 0, 0), ("mm2a", 1, 0), ("mm2b", 1, 0), ("mm2a", 2, 0), ("mm2b", 2, 0), ("mm2a", 3, 0), ("mm2b", 3, 0),
+    ("mm2a", 0, 1), ("mm2b", 0, 1), ("mm2a", 1, 1), ("mm2b", 1, 1), ("rX", 1, 3), ("qX", 0, 3), ("qX", 1, 3),
+    ("vs", 0, 0), ("tanh", 1, 0), ("tanh", 2, 0), ("tanh", 3, 0), ("tanh", 0, 1), ("tanh", 1, 1), ("mm2a", 2, 1),
+    ("mm2b", 2, 1), ("mm2a", 3, 1), ("mm2b", 3, 1), ("mm2a", 0, 2), ("mm2b", 0, 2), ("mm2a", 1, 2), ("mm2b", 1, 2),
+    ("mm2a", 2, 2), ("mm2b", 2, 2), ("vs", 0, 1), ("vs", 1, 0), ("vs", 1, 1), ("vs", 2, 0), ("tanh", 2, 1),
+    ("tanh", 3, 1), ("tanh", 0, 2), ("tanh", 1, 2), ("tanh", 2, 2), ("mm2a", 3, 2), ("mm2b", 3, 2), ("mm2a", 0, 3),
+    ("mm2b", 0, 3), ("mm2a", 1, 3), ("mm2b", 1, 3), ("mm2a", 2, 3), ("mm2b", 2, 3), ("mm2a", 3, 3), ("mm2b", 3, 3),
+    ("vs", 0, 2), ("vs", 2, 1), ("vs", 3, 0), ("vs", 1, 2), ("vs", 3, 1), ("vs", 2, 2), ("tanh", 3, 2),
+    ("tanh", 0, 3), ("tanh", 1, 3), ("tanh", 2, 3), ("tanh", 3, 3), ("ws", 0, 0), ("ws", 1, 0), ("wsd", 0, 3),
     ("vs", 1, 3), ("vs", 3, 2), ("vs", 2, 3), ("vs", 3, 3), ("ws", 2, 0), ("ws", 3, 0), ("f1", 0, 0), ("f2", 0, 0),
 )
 
@@ -142,16 +144,16 @@ def tile_fluxgnn1dlatent_pb_kernel(tc, edge_hid, u, enc, W2, b2, W3, b3, out):
         nc.scalar.dma_start(out=vec_rows[8:12, :], in_=b3.rearrange("(j c) -> j c", c=P))
         nc.scalar.dma_start(out=vec_rows[12:16, :], in_=enc.rearrange("(j c) -> j c", c=P))
         load_w2(0, 0)
-        load_w2(0, 1)
         load_e(0)
-        load_w2(1, 0)
+        load_w2(0, 1)
         load_e(1)
-        load_w2(1, 1)
+        nc.sync.dma_start(out=u_bf[:], in_=u)
+        load_w2(1, 0)
         load_e(2)
+        load_w2(1, 1)
         load_e(3)
         load_w3(0)
         load_w3(1)
-        nc.sync.dma_start(out=u_bf[:], in_=u)
 
         nc.vector.memset(zero1[:], 0.0)
         nc.vector.memset(vec_f32[:], 0.0)
@@ -173,7 +175,7 @@ def tile_fluxgnn1dlatent_pb_kernel(tc, edge_hid, u, enc, W2, b2, W3, b3, out):
             )
 
         def op_vecT(a, b):
-            bank["vec"] = psum.tile([P, P], F32, name="vec_t", tag="tp", bufs=2)
+            bank["vec"] = psum.tile([P, P], F32, name="vec_t", tag="g", bufs=1)
             nc.tensor.transpose(bank["vec"][:], vec_f32[:], ident[:])
 
         def op_cols(a, b):
@@ -205,7 +207,10 @@ def tile_fluxgnn1dlatent_pb_kernel(tc, edge_hid, u, enc, W2, b2, W3, b3, out):
             )
 
         def op_rW3(g, b):
-            regroup(nc.vector.tensor_copy, w3_grp[g][:], w3_raw[g][:], 0, LD)
+            regroup(nc.vector.tensor_copy, w3_grp[g][:], w3_raw[g][:], 0, LD - S3_COLS.get(g, 0))
+
+        def op_sW3(g, b):
+            regroup(nc.scalar.copy, w3_grp[g][:], w3_raw[g][:], LD - S3_COLS[g], LD)
 
         def op_qW3(g, b):
             nc.vector.quantize_mx(out=w3_cod[g][:].bitcast(FP8X4), scales=w3_scl[g][:], in_=w3_grp[g][:])
@@ -329,7 +334,7 @@ def tile_fluxgnn1dlatent_pb_kernel(tc, edge_hid, u, enc, W2, b2, W3, b3, out):
 
         ops = {
             "vecT": op_vecT, "cols": op_cols, "den": op_den, "rinv": op_rinv, "coef": op_coef,
-            "rW2": op_rW2, "sW2": op_sW2, "qW2": op_qW2, "rW3": op_rW3, "qW3": op_qW3,
+            "rW2": op_rW2, "sW2": op_sW2, "qW2": op_qW2, "rW3": op_rW3, "sW3": op_sW3, "qW3": op_qW3,
             "tE": op_tE, "cE": op_cE, "qE": op_qE, "mm1": op_mm1, "gelu": op_gelu,
             "rX": op_rX, "qX": op_qX, "mm2a": op_mm2a, "mm2b": op_mm2b, "tanh": op_tanh,
             "vs": op_vs, "ws": op_ws, "wsd": op_wsd, "f1": op_f1, "f2": op_f2,

@@ -29,32 +29,33 @@ FLOPS = 2 * NB * NE * HID * HID + 2 * NB * NE * HID * LD
 
 ORDER = (
     ("rW2", 0, 0), ("den", 0, 0), ("sW2", 0, 0), ("tE", 0, 0), ("tE", 0, 1), ("vecT", 0, 0), ("qW2", 0, 0),
-    ("rinv", 0, 0), ("rW2", 0, 1), ("cE", 0, 0), ("cE", 0, 1), ("sW2", 0, 1), ("cols", 0, 0), ("coef", 0, 0),
-    ("tE", 1, 0), ("tE", 1, 1), ("qE", 0, 0), ("qW2", 0, 1), ("rW2", 1, 0), ("cE", 1, 0), ("cE", 1, 1), ("mm1", 0, 0),
-    ("mm1", 1, 0), ("mm1", 2, 0), ("mm1", 3, 0), ("tE", 2, 0), ("tE", 2, 1), ("qE", 1, 0), ("qW2", 1, 0),
-    ("rW2", 1, 1), ("gelu", 0, 0), ("gelu", 1, 0), ("gelu", 2, 0), ("gelu", 3, 0), ("cE", 2, 0), ("cE", 2, 1),
-    ("mm1", 0, 1), ("mm1", 1, 1), ("mm1", 2, 1), ("mm1", 3, 1), ("tE", 3, 0), ("tE", 3, 1), ("rX", 0, 0),
-    ("qW2", 1, 1), ("qE", 2, 0), ("gelu", 0, 1), ("gelu", 1, 1), ("gelu", 2, 1), ("gelu", 3, 1), ("cE", 3, 0),
-    ("cE", 3, 1), ("mm1", 4, 0), ("mm1", 5, 0), ("mm1", 6, 0), ("mm1", 7, 0), ("mm1", 0, 2), ("rX", 0, 1),
-    ("qE", 3, 0), ("qX", 0, 0), ("gelu", 4, 0), ("gelu", 5, 0), ("gelu", 6, 0), ("gelu", 7, 0), ("sW3", 0, 0),
-    ("gelu", 0, 2), ("mm1", 1, 2), ("mm1", 2, 2), ("mm1", 3, 2), ("mm1", 4, 1), ("mm1", 5, 1), ("rX", 1, 0),
-    ("qX", 0, 1), ("rW3", 0, 0), ("qX", 1, 0), ("rW3", 1, 0), ("qW3", 0, 0), ("gelu", 1, 2), ("gelu", 2, 2),
-    ("gelu", 3, 2), ("gelu", 4, 1), ("gelu", 5, 1), ("mm1", 6, 1), ("mm1", 7, 1), ("mm1", 4, 2), ("mm1", 5, 2),
-    ("mm1", 6, 2), ("rX", 0, 2), ("gelu", 6, 1), ("gelu", 7, 1), ("sW3", 1, 0), ("gelu", 4, 2), ("gelu", 5, 2),
-    ("gelu", 6, 2), ("mm1", 7, 2), ("mm1", 0, 3), ("mm1", 1, 3), ("mm1", 2, 3), ("mm1", 3, 3), ("qW3", 1, 0),
-    ("rX", 1, 1), ("qX", 0, 2), ("gelu", 7, 2), ("gelu", 0, 3), ("gelu", 1, 3), ("gelu", 2, 3), ("gelu", 3, 3),
-    ("mm1", 4, 3), ("mm1", 5, 3), ("mm1", 6, 3), ("mm1", 7, 3), ("mm2a", 0, 0), ("mm2b", 0, 0), ("rX", 1, 2),
-    ("qX", 1, 1), ("rX", 0, 3), ("qX", 1, 2), ("gelu", 4, 3), ("gelu", 5, 3), ("gelu", 6, 3), ("gelu", 7, 3),
-    ("tanh", 0, 0), ("mm2a", 1, 0), ("mm2b", 1, 0), ("mm2a", 2, 0), ("mm2b", 2, 0), ("mm2a", 3, 0), ("mm2b", 3, 0),
-    ("mm2a", 0, 1), ("mm2b", 0, 1), ("mm2a", 1, 1), ("mm2b", 1, 1), ("rX", 1, 3), ("qX", 0, 3), ("qX", 1, 3),
-    ("vs", 0, 0), ("tanh", 1, 0), ("tanh", 2, 0), ("tanh", 3, 0), ("tanh", 0, 1), ("tanh", 1, 1), ("mm2a", 2, 1),
-    ("mm2b", 2, 1), ("mm2a", 3, 1), ("mm2b", 3, 1), ("mm2a", 0, 2), ("mm2b", 0, 2), ("mm2a", 1, 2), ("mm2b", 1, 2),
-    ("mm2a", 2, 2), ("mm2b", 2, 2), ("vs", 0, 1), ("vs", 1, 0), ("vs", 1, 1), ("vs", 2, 0), ("tanh", 2, 1),
-    ("tanh", 3, 1), ("tanh", 0, 2), ("tanh", 1, 2), ("tanh", 2, 2), ("mm2a", 3, 2), ("mm2b", 3, 2), ("mm2a", 0, 3),
-    ("mm2b", 0, 3), ("mm2a", 1, 3), ("mm2b", 1, 3), ("mm2a", 2, 3), ("mm2b", 2, 3), ("mm2a", 3, 3), ("mm2b", 3, 3),
-    ("vs", 0, 2), ("vs", 2, 1), ("vs", 3, 0), ("vs", 1, 2), ("vs", 3, 1), ("vs", 2, 2), ("tanh", 3, 2),
-    ("tanh", 0, 3), ("tanh", 1, 3), ("tanh", 2, 3), ("tanh", 3, 3), ("ws", 0, 0), ("ws", 1, 0), ("wsd", 0, 3),
-    ("vs", 1, 3), ("vs", 3, 2), ("vs", 2, 3), ("vs", 3, 3), ("ws", 2, 0), ("ws", 3, 0), ("f1", 0, 0), ("f2", 0, 0),
+    ("rW2", 0, 1), ("cE", 0, 0), ("cE", 0, 1), ("sW2", 0, 1), ("cols", 0, 0), ("tE", 1, 0), ("tE", 1, 1),
+    ("qE", 0, 0), ("qW2", 0, 1), ("rW2", 1, 0), ("cE", 1, 0), ("cE", 1, 1), ("mm1", 0, 0), ("mm1", 1, 0),
+    ("mm1", 2, 0), ("mm1", 3, 0), ("tE", 2, 0), ("tE", 2, 1), ("qE", 1, 0), ("qW2", 1, 0), ("rW2", 1, 1),
+    ("gelu", 0, 0), ("gelu", 1, 0), ("gelu", 2, 0), ("gelu", 3, 0), ("cE", 2, 0), ("cE", 2, 1), ("mm1", 0, 1),
+    ("mm1", 1, 1), ("mm1", 2, 1), ("mm1", 3, 1), ("tE", 3, 0), ("tE", 3, 1), ("rX", 0, 0), ("qW2", 1, 1),
+    ("qE", 2, 0), ("gelu", 0, 1), ("gelu", 1, 1), ("gelu", 2, 1), ("gelu", 3, 1), ("cE", 3, 0), ("cE", 3, 1),
+    ("mm1", 4, 0), ("mm1", 5, 0), ("mm1", 6, 0), ("mm1", 7, 0), ("mm1", 0, 2), ("rX", 0, 1), ("qE", 3, 0),
+    ("qX", 0, 0), ("gelu", 4, 0), ("gelu", 5, 0), ("gelu", 6, 0), ("gelu", 7, 0), ("sW3", 0, 0), ("gelu", 0, 2),
+    ("mm1", 1, 2), ("mm1", 2, 2), ("mm1", 3, 2), ("mm1", 4, 1), ("mm1", 5, 1), ("rX", 1, 0), ("qX", 0, 1),
+    ("rW3", 0, 0), ("qX", 1, 0), ("rW3", 1, 0), ("qW3", 0, 0), ("gelu", 1, 2), ("gelu", 2, 2), ("gelu", 3, 2),
+    ("gelu", 4, 1), ("gelu", 5, 1), ("mm1", 6, 1), ("mm1", 7, 1), ("mm1", 4, 2), ("mm1", 5, 2), ("mm1", 6, 2),
+    ("rX", 0, 2), ("gelu", 6, 1), ("gelu", 7, 1), ("sW3", 1, 0), ("gelu", 4, 2), ("gelu", 5, 2), ("gelu", 6, 2),
+    ("mm1", 7, 2), ("mm1", 0, 3), ("mm1", 1, 3), ("mm1", 2, 3), ("mm1", 3, 3), ("qW3", 1, 0), ("rX", 1, 1),
+    ("qX", 0, 2), ("gelu", 7, 2), ("gelu", 0, 3), ("gelu", 1, 3), ("gelu", 2, 3), ("gelu", 3, 3), ("mm1", 4, 3),
+    ("mm1", 5, 3), ("mm1", 6, 3), ("mm1", 7, 3), ("mm2a", 0, 0), ("mm2b", 0, 0), ("rX", 1, 2), ("qX", 1, 1),
+    ("rX", 0, 3), ("qX", 1, 2), ("gelu", 4, 3), ("gelu", 5, 3), ("gelu", 6, 3), ("gelu", 7, 3), ("tanh", 0, 0),
+    ("mm2a", 1, 0), ("mm2b", 1, 0), ("mm2a", 2, 0), ("mm2b", 2, 0), ("mm2a", 3, 0), ("mm2b", 3, 0), ("mm2a", 0, 1),
+    ("mm2b", 0, 1), ("mm2a", 1, 1), ("mm2b", 1, 1), ("rX", 1, 3), ("qX", 0, 3), ("qX", 1, 3), ("vs", 0, 0),
+    ("tanh", 1, 0), ("tanh", 2, 0), ("tanh", 3, 0), ("tanh", 0, 1), ("tanh", 1, 1), ("mm2a", 2, 1), ("mm2b", 2, 1),
+    ("mm2a", 3, 1), ("mm2b", 3, 1), ("mm2a", 0, 2), ("mm2b", 0, 2), ("mm2a", 1, 2), ("mm2b", 1, 2), ("mm2a", 2, 2),
+    ("mm2b", 2, 2), ("vs", 0, 1), ("vs", 1, 0), ("vs", 1, 1), ("vs", 2, 0), ("tanh", 2, 1), ("tanh", 3, 1),
+    ("tanh", 0, 2), ("tanh", 1, 2), ("tanh", 2, 2), ("mm2a", 3, 2), ("mm2b", 3, 2), ("mm2a", 0, 3), ("mm2b", 0, 3),
+    ("mm2a", 1, 3), ("mm2b", 1, 3), ("mm2a", 2, 3), ("mm2b", 2, 3), ("mm2a", 3, 3), ("mm2b", 3, 3), ("vs", 0, 2),
+    ("vs", 2, 1), ("vs", 3, 0), ("vs", 1, 2), ("vs", 3, 1), ("vs", 2, 2), ("tanh", 3, 2), ("tanh", 0, 3),
+    ("tanh", 1, 3), ("tanh", 2, 3), ("tanh", 3, 3), ("ws", 0, 0), ("ws", 1, 0), ("wsd", 0, 3), ("vs", 1, 3),
+    ("vs", 3, 2), ("rinv", 0, 0), ("vs", 2, 3), ("coef", 0, 0), ("vs", 3, 3), ("us", 0, 0), ("ws", 2, 0),
+    ("ws", 3, 0), ("f1", 0, 0), ("f2", 0, 0),
 )
 
 
@@ -134,6 +135,9 @@ def tile_fluxgnn1dlatent_pb_kernel(tc, edge_hid, u, enc, W2, b2, W3, b3, out):
         def load_e(b):
             nc.sync.dma_start(out=e_raw[b][:], in_=edge_hid[b, :, :].rearrange("(j p) k -> p j k", p=P))
 
+        def load_e_half(b, j):
+            nc.sync.dma_start(out=e_raw[b][:, j, :], in_=edge_hid[b, P * j : P * j + P, :])
+
         def load_w3(g):
             nc.sync.dma_start(
                 out=w3_raw[g][:], in_=W3[512 * g : 512 * g + 512, :].rearrange("(t p) c -> p t c", p=P)
@@ -144,9 +148,11 @@ def tile_fluxgnn1dlatent_pb_kernel(tc, edge_hid, u, enc, W2, b2, W3, b3, out):
         nc.scalar.dma_start(out=vec_rows[8:12, :], in_=b3.rearrange("(j c) -> j c", c=P))
         nc.scalar.dma_start(out=vec_rows[12:16, :], in_=enc.rearrange("(j c) -> j c", c=P))
         load_w2(0, 0)
-        load_e(0)
+        load_e_half(0, 0)
+        load_e_half(0, 1)
         load_w2(0, 1)
-        load_e(1)
+        load_e_half(1, 0)
+        load_e_half(1, 1)
         nc.sync.dma_start(out=u_bf[:], in_=u)
         load_w2(1, 0)
         load_e(2)
@@ -190,10 +196,12 @@ def tile_fluxgnn1dlatent_pb_kernel(tc, edge_hid, u, enc, W2, b2, W3, b3, out):
             nc.vector.reciprocal(out=rinv[:], in_=den[:])
 
         def op_coef(a, b):
-            nc.scalar.activation(out=c_u[:], in_=ssum[:], func=ACT.Copy, scale=rinv[:, 0:1])
-            nc.scalar.mul(out=c_pos[:], in_=rinv[:], mul=COEF)
-            nc.scalar.mul(out=c_neg[:], in_=rinv[:], mul=-COEF)
-            nc.scalar.activation(out=u_s[:], in_=u_bf[:], func=ACT.Copy, scale=c_u[:, 0:1])
+            nc.vector.tensor_scalar_mul(out=c_u[:], in0=ssum[:], scalar1=rinv[:, 0:1])
+            nc.vector.tensor_scalar_mul(out=c_pos[:], in0=rinv[:], scalar1=COEF)
+            nc.vector.tensor_scalar_mul(out=c_neg[:], in0=rinv[:], scalar1=-COEF)
+
+        def op_us(a, b):
+            nc.vector.tensor_scalar_mul(out=u_s[:], in0=u_bf[:], scalar1=c_u[:, 0:1])
 
         def op_rW2(h, g):
             regroup(nc.vector.tensor_copy, w2_grp[h][:, g, :], w2_raw[h][:, 4 * g : 4 * g + 4, :], 0, 512 - S_COLS.get((h, g), 0))
@@ -215,19 +223,19 @@ def tile_fluxgnn1dlatent_pb_kernel(tc, edge_hid, u, enc, W2, b2, W3, b3, out):
         def op_qW3(g, b):
             nc.vector.quantize_mx(out=w3_cod[g][:].bitcast(FP8X4), scales=w3_scl[g][:], in_=w3_grp[g][:])
 
-        def op_tE(b, g):
-            tp = psum.tile([P, 2, NE], F32, name="tp", tag="tp", bufs=2)
-            bank[("tp", b, g)] = tp
-            for jj in range(2):
-                words = e_raw[b][:, jj, :].bitcast(F32)
+        def op_tE(b, jj):
+            tp = psum.tile([P, 2, 2, P], F32, name="tp", tag="tp", bufs=2)
+            bank[("tp", b, jj)] = tp
+            words = e_raw[b][:, jj, :].bitcast(F32)
+            for g in range(2):
                 for uu in range(2):
                     w0 = 256 * g + 128 * uu
-                    nc.tensor.transpose(tp[:, uu, P * jj : P * jj + P], words[:, w0 : w0 + P], ident[:])
+                    nc.tensor.transpose(tp[:, g, uu, :], words[:, w0 : w0 + P], ident[:])
 
-        def op_cE(b, g):
+        def op_cE(b, jj):
             nc.scalar.copy(
-                out=e_grp[b][:, g, :].bitcast(F32).rearrange("p (r w) -> p r w", w=2),
-                in_=bank[("tp", b, g)][:].rearrange("p w r -> p r w"),
+                out=e_grp[b][:, :, 512 * jj : 512 * jj + 512].bitcast(F32).rearrange("p g (r w) -> p g r w", w=2),
+                in_=bank[("tp", b, jj)][:].rearrange("p g w r -> p g r w"),
             )
 
         def op_qE(b, z):
@@ -333,7 +341,7 @@ def tile_fluxgnn1dlatent_pb_kernel(tc, edge_hid, u, enc, W2, b2, W3, b3, out):
             )
 
         ops = {
-            "vecT": op_vecT, "cols": op_cols, "den": op_den, "rinv": op_rinv, "coef": op_coef,
+            "vecT": op_vecT, "cols": op_cols, "den": op_den, "rinv": op_rinv, "coef": op_coef, "us": op_us,
             "rW2": op_rW2, "sW2": op_sW2, "qW2": op_qW2, "rW3": op_rW3, "sW3": op_sW3, "qW3": op_qW3,
             "tE": op_tE, "cE": op_cE, "qE": op_qE, "mm1": op_mm1, "gelu": op_gelu,
             "rX": op_rX, "qX": op_qX, "mm2a": op_mm2a, "mm2b": op_mm2b, "tanh": op_tanh,

@@ -18,44 +18,40 @@ NC = 255
 HID = 1024
 LD = 512
 COEF = 0.5 * 0.25
-BLOCKS = ((0,), (1,), (2,), (3,),)
+S_COLS = {(0, 0): 160, (0, 1): 140}
+S3_COLS = {0: 192, 1: 192}
 VSUM = {0: (0, 1, 2, 3,), 1: (0, 1, 2, 3,), 2: (0, 1, 2, 3,), 3: (1, 2, 3,)}
 DIRECT = tuple(b for b in range(NB) if len(VSUM[b]) < 4)
-S_COLS = {(0, 0): 160, (0, 1): 140}
-
-S3_COLS = {0: 192, 1: 192}
 
 FLOPS = 2 * NB * NE * HID * HID + 2 * NB * NE * HID * LD
 
 ORDER = (
-    ("rW2", 0, 0), ("den", 0, 0), ("sW2", 0, 0), ("tE", 0, 0), ("tE", 0, 1), ("vecT", 0, 0), ("qW2", 0, 0),
-    ("rW2", 0, 1), ("cE", 0, 0), ("cE", 0, 1), ("sW2", 0, 1), ("cols", 0, 0), ("tE", 1, 0), ("tE", 1, 1),
-    ("qE", 0, 0), ("qW2", 0, 1), ("rW2", 1, 0), ("cE", 1, 0), ("cE", 1, 1), ("mm1", 0, 0), ("mm1", 1, 0),
-    ("mm1", 2, 0), ("mm1", 3, 0), ("tE", 2, 0), ("tE", 2, 1), ("qE", 1, 0), ("qW2", 1, 0), ("rW2", 1, 1),
-    ("gelu", 0, 0), ("gelu", 1, 0), ("gelu", 2, 0), ("gelu", 3, 0), ("cE", 2, 0), ("cE", 2, 1), ("mm1", 0, 1),
-    ("mm1", 1, 1), ("mm1", 2, 1), ("mm1", 3, 1), ("tE", 3, 0), ("tE", 3, 1), ("rX", 0, 0), ("qW2", 1, 1),
-    ("qE", 2, 0), ("gelu", 0, 1), ("gelu", 1, 1), ("gelu", 2, 1), ("gelu", 3, 1), ("cE", 3, 0), ("cE", 3, 1),
-    ("mm1", 4, 0), ("mm1", 5, 0), ("mm1", 6, 0), ("mm1", 7, 0), ("mm1", 0, 2), ("rX", 0, 1), ("qE", 3, 0),
-    ("qX", 0, 0), ("gelu", 4, 0), ("gelu", 5, 0), ("gelu", 6, 0), ("gelu", 7, 0), ("sW3", 0, 0), ("gelu", 0, 2),
-    ("mm1", 1, 2), ("mm1", 2, 2), ("mm1", 3, 2), ("mm1", 4, 1), ("mm1", 5, 1), ("rX", 1, 0), ("qX", 0, 1),
-    ("rW3", 0, 0), ("qX", 1, 0), ("rW3", 1, 0), ("qW3", 0, 0), ("gelu", 1, 2), ("gelu", 2, 2), ("gelu", 3, 2),
-    ("gelu", 4, 1), ("gelu", 5, 1), ("mm1", 6, 1), ("mm1", 7, 1), ("mm1", 4, 2), ("mm1", 5, 2), ("mm1", 6, 2),
-    ("rX", 0, 2), ("gelu", 6, 1), ("gelu", 7, 1), ("sW3", 1, 0), ("gelu", 4, 2), ("gelu", 5, 2), ("gelu", 6, 2),
-    ("mm1", 7, 2), ("mm1", 0, 3), ("mm1", 1, 3), ("mm1", 2, 3), ("mm1", 3, 3), ("qW3", 1, 0), ("rX", 1, 1),
-    ("qX", 0, 2), ("gelu", 7, 2), ("gelu", 0, 3), ("gelu", 1, 3), ("gelu", 2, 3), ("gelu", 3, 3), ("mm1", 4, 3),
-    ("mm1", 5, 3), ("mm1", 6, 3), ("mm1", 7, 3), ("mm2a", 0, 0), ("mm2b", 0, 0), ("rX", 1, 2), ("qX", 1, 1),
-    ("rX", 0, 3), ("qX", 1, 2), ("gelu", 4, 3), ("gelu", 5, 3), ("gelu", 6, 3), ("gelu", 7, 3), ("tanh", 0, 0),
-    ("mm2a", 1, 0), ("mm2b", 1, 0), ("mm2a", 2, 0), ("mm2b", 2, 0), ("mm2a", 3, 0), ("mm2b", 3, 0), ("mm2a", 0, 1),
-    ("mm2b", 0, 1), ("mm2a", 1, 1), ("mm2b", 1, 1), ("rX", 1, 3), ("qX", 0, 3), ("qX", 1, 3), ("vs", 0, 0),
-    ("tanh", 1, 0), ("tanh", 2, 0), ("tanh", 3, 0), ("tanh", 0, 1), ("tanh", 1, 1), ("mm2a", 2, 1), ("mm2b", 2, 1),
-    ("mm2a", 3, 1), ("mm2b", 3, 1), ("mm2a", 0, 2), ("mm2b", 0, 2), ("mm2a", 1, 2), ("mm2b", 1, 2), ("mm2a", 2, 2),
-    ("mm2b", 2, 2), ("vs", 0, 1), ("vs", 1, 0), ("vs", 1, 1), ("vs", 2, 0), ("tanh", 2, 1), ("tanh", 3, 1),
-    ("tanh", 0, 2), ("tanh", 1, 2), ("tanh", 2, 2), ("mm2a", 3, 2), ("mm2b", 3, 2), ("mm2a", 0, 3), ("mm2b", 0, 3),
-    ("mm2a", 1, 3), ("mm2b", 1, 3), ("mm2a", 2, 3), ("mm2b", 2, 3), ("mm2a", 3, 3), ("mm2b", 3, 3), ("vs", 0, 2),
-    ("vs", 2, 1), ("vs", 3, 0), ("vs", 1, 2), ("vs", 3, 1), ("vs", 2, 2), ("tanh", 3, 2), ("tanh", 0, 3),
-    ("tanh", 1, 3), ("tanh", 2, 3), ("tanh", 3, 3), ("ws", 0, 0), ("ws", 1, 0), ("wsd", 0, 3), ("vs", 1, 3),
-    ("vs", 3, 2), ("rinv", 0, 0), ("vs", 2, 3), ("coef", 0, 0), ("vs", 3, 3), ("us", 0, 0), ("ws", 2, 0),
-    ("ws", 3, 0), ("f1", 0, 0), ("f2", 0, 0),
+    ("rW2", 0, 0), ("den", 0, 0), ("sW2", 0, 0), ("warm", 8, 0), ("tE", 0, 0), ("tE", 0, 1), ("vecT", 0, 0),
+    ("warm", 4, 1), ("qW2", 0, 0), ("rW2", 0, 1), ("cE", 0, 0), ("cE", 0, 1), ("sW2", 0, 1), ("cols", 0, 0),
+    ("tE", 1, 0), ("tE", 1, 1), ("warm", 2, 2), ("qE", 0, 0), ("qW2", 0, 1), ("rW2", 1, 0), ("cE", 1, 0),
+    ("cE", 1, 1), ("mm1", 0, 0), ("mm1", 1, 0), ("mm1", 2, 0), ("mm1", 3, 0), ("tE", 2, 0), ("tE", 2, 1),
+    ("qE", 1, 0), ("qW2", 1, 0), ("rW2", 1, 1), ("gelu", 0, 0), ("gelu", 1, 0), ("gelu", 2, 0), ("gelu", 3, 0),
+    ("cE", 2, 0), ("cE", 2, 1), ("mm1", 0, 1), ("mm1", 1, 1), ("mm1", 2, 1), ("mm1", 3, 1), ("tE", 3, 0),
+    ("tE", 3, 1), ("rX", 0, 0), ("qW2", 1, 1), ("qE", 2, 0), ("gelu", 0, 1), ("gelu", 1, 1), ("gelu", 2, 1),
+    ("gelu", 3, 1), ("cE", 3, 0), ("cE", 3, 1), ("mm1", 4, 0), ("mm1", 5, 0), ("mm1", 6, 0), ("mm1", 7, 0),
+    ("mm1", 0, 2), ("rX", 0, 1), ("qE", 3, 0), ("qX", 0, 0), ("gelu", 4, 0), ("gelu", 5, 0), ("gelu", 6, 0),
+    ("gelu", 7, 0), ("sW3", 0, 0), ("gelu", 0, 2), ("mm1", 1, 2), ("mm1", 2, 2), ("mm1", 3, 2), ("mm1", 4, 1),
+    ("mm1", 5, 1), ("rX", 1, 0), ("qX", 0, 1), ("rW3", 0, 0), ("qX", 1, 0), ("rW3", 1, 0), ("qW3", 0, 0),
+    ("gelu", 1, 2), ("gelu", 2, 2), ("gelu", 3, 2), ("gelu", 4, 1), ("gelu", 5, 1), ("mm1", 6, 1), ("mm1", 7, 1),
+    ("mm1", 4, 2), ("mm1", 5, 2), ("mm1", 6, 2), ("rX", 0, 2), ("gelu", 6, 1), ("gelu", 7, 1), ("sW3", 1, 0),
+    ("gelu", 4, 2), ("gelu", 5, 2), ("gelu", 6, 2), ("mm1", 7, 2), ("mm1", 0, 3), ("mm1", 1, 3), ("mm1", 2, 3),
+    ("mm1", 3, 3), ("qW3", 1, 0), ("rX", 1, 1), ("qX", 0, 2), ("gelu", 7, 2), ("gelu", 0, 3), ("gelu", 1, 3),
+    ("gelu", 2, 3), ("gelu", 3, 3), ("mm1", 4, 3), ("mm1", 5, 3), ("mm1", 6, 3), ("mm1", 7, 3), ("mm2", 0, 0),
+    ("rX", 1, 2), ("qX", 1, 1), ("rX", 0, 3), ("qX", 1, 2), ("gelu", 4, 3), ("gelu", 5, 3), ("gelu", 6, 3),
+    ("gelu", 7, 3), ("tanh", 0, 0), ("mm2", 1, 0), ("mm2", 2, 0), ("mm2", 3, 0), ("mm2", 0, 1), ("mm2", 1, 1),
+    ("rX", 1, 3), ("qX", 0, 3), ("qX", 1, 3), ("vs", 0, 0), ("tanh", 1, 0), ("tanh", 2, 0), ("tanh", 3, 0),
+    ("tanh", 0, 1), ("tanh", 1, 1), ("mm2", 2, 1), ("mm2", 3, 1), ("mm2", 0, 2), ("mm2", 1, 2), ("mm2", 2, 2),
+    ("vs", 0, 1), ("vs", 1, 0), ("vs", 1, 1), ("vs", 2, 0), ("tanh", 2, 1), ("tanh", 3, 1), ("tanh", 0, 2),
+    ("tanh", 1, 2), ("tanh", 2, 2), ("mm2", 3, 2), ("mm2", 0, 3), ("mm2", 1, 3), ("mm2", 2, 3), ("mm2", 3, 3),
+    ("vs", 0, 2), ("vs", 2, 1), ("vs", 3, 0), ("vs", 1, 2), ("vs", 3, 1), ("vs", 2, 2), ("tanh", 3, 2),
+    ("tanh", 0, 3), ("tanh", 1, 3), ("tanh", 2, 3), ("tanh", 3, 3), ("ws", 0, 0), ("ws", 1, 0), ("wsd", 0, 3),
+    ("vs", 1, 3), ("vs", 3, 2), ("rinv", 0, 0), ("vs", 2, 3), ("coef", 0, 0), ("vs", 3, 3), ("us", 0, 0),
+    ("ws", 2, 0), ("ws", 3, 0), ("f1", 0, 0), ("f2", 0, 0),
 )
 
 
@@ -65,18 +61,12 @@ def tile_fluxgnn1dlatent_pb_kernel(tc, edge_hid, u, enc, W2, b2, W3, b3, out):
         keep = ctx.enter_context(tc.tile_pool(name="keep", bufs=1))
         psum = ctx.enter_context(tc.psum_pool(name="psum", bufs=1))
         ctx.enter_context(tc.manual_schedule())
-        nblk = len(BLOCKS)
-        width = [NE * len(bs) for bs in BLOCKS]
-        home = {}
-        for k, bs in enumerate(BLOCKS):
-            for i, b in enumerate(bs):
-                home[b] = (k, i)
         sums = [op for op in ORDER if op[0] in ("ws", "wsd")]
 
         e_raw = [keep.tile([P, 2, HID], BF16, name="e_raw%d" % b) for b in range(NB)]
         e_grp = [keep.tile([P, 2, 4 * NE], BF16, name="e_grp%d" % b, align_bytes=64) for b in range(NB)]
-        e_cod = [keep.tile([P, 2, width[k]], U32, name="e_cod%d" % k, align_bytes=64) for k in range(nblk)]
-        e_scl = [keep.tile([P, 2, width[k]], U8, name="e_scl%d" % k, align_bytes=64) for k in range(nblk)]
+        e_cod = [keep.tile([P, 2, NE], U32, name="e_cod%d" % b, align_bytes=64) for b in range(NB)]
+        e_scl = [keep.tile([P, 2, NE], U8, name="e_scl%d" % b, align_bytes=64) for b in range(NB)]
         w2_raw = [keep.tile([P, 8, 512], BF16, name="w2_raw%d" % h) for h in range(2)]
         w2_grp = [keep.tile([P, 2, 2048], BF16, name="w2_grp%d" % h, align_bytes=64) for h in range(2)]
         w2_cod = [keep.tile([P, 2, 512], U32, name="w2_cod%d" % h, align_bytes=64) for h in range(2)]
@@ -85,21 +75,12 @@ def tile_fluxgnn1dlatent_pb_kernel(tc, edge_hid, u, enc, W2, b2, W3, b3, out):
         w3_grp = [keep.tile([P, 4 * LD], BF16, name="w3_grp%d" % g, align_bytes=64) for g in range(2)]
         w3_cod = [keep.tile([P, LD], U32, name="w3_cod%d" % g, align_bytes=64) for g in range(2)]
         w3_scl = [keep.tile([P, LD], U8, name="w3_scl%d" % g, align_bytes=64) for g in range(2)]
-        x_pln = [[keep.tile([P, 4, width[k]], BF16, name="x_pln%d_%d" % (g, k)) for k in range(nblk)] for g in range(2)]
-        x_grp = [
-            [keep.tile([P, 4 * width[k]], BF16, name="x_grp%d_%d" % (g, k), align_bytes=64) for k in range(nblk)]
-            for g in range(2)
-        ]
-        x_cod = [
-            [keep.tile([P, width[k]], U32, name="x_cod%d_%d" % (g, k), align_bytes=64) for k in range(nblk)]
-            for g in range(2)
-        ]
-        x_scl = [
-            [keep.tile([P, width[k]], U8, name="x_scl%d_%d" % (g, k), align_bytes=64) for k in range(nblk)]
-            for g in range(2)
-        ]
-        t_sb = [[keep.tile([P, width[k]], F32, name="t_sb%d_%d" % (ct, k)) for k in range(nblk)] for ct in range(4)]
-        wsum = [keep.tile([P, width[k]], F32, name="wsum%d" % k) for k in range(nblk)]
+        x_pln = [[keep.tile([P, 2, 4, NE], BF16, name="x_pln%d_%d" % (h, q)) for q in range(2)] for h in range(2)]
+        x_grp = [[keep.tile([P, 4 * NE], BF16, name="x_grp%d_%d" % (h, b), align_bytes=64) for b in range(NB)] for h in range(2)]
+        x_cod = [[keep.tile([P, NE], U32, name="x_cod%d_%d" % (h, b), align_bytes=64) for b in range(NB)] for h in range(2)]
+        x_scl = [[keep.tile([P, NE], U8, name="x_scl%d_%d" % (h, b), align_bytes=64) for b in range(NB)] for h in range(2)]
+        t_sb = [[keep.tile([P, 2, NE], F32, name="t_sb%d_%d" % (ct, q)) for q in range(2)] for ct in range(4)]
+        wsum = [keep.tile([P, 2, NE], F32, name="wsum%d" % q) for q in range(2)]
 
         ident = keep.tile([P, P], F32, name="ident")
         pick = keep.tile([P, NB * P], F32, name="pick")
@@ -111,6 +92,7 @@ def tile_fluxgnn1dlatent_pb_kernel(tc, edge_hid, u, enc, W2, b2, W3, b3, out):
         cols = keep.tile([P, 16], F32, name="cols")
         zero1 = keep.tile([P, 1], F32, name="zero1")
         junk1 = keep.tile([P, 1], F32, name="junk1")
+        warm = keep.tile([P, 512], BF16, name="warm")
         u_bf = keep.tile([NB, NC], BF16, name="u_bf")
         u_s = keep.tile([NB, NC], F32, name="u_s")
         enc_rows = keep.tile([NB, LD], BF16, name="enc_rows")
@@ -125,6 +107,13 @@ def tile_fluxgnn1dlatent_pb_kernel(tc, edge_hid, u, enc, W2, b2, W3, b3, out):
         res = keep.tile([NB, NC], F32, name="res")
         bank = {}
 
+        def grids(sel):
+            return (sel,) if sel < NB else (2 * (sel - NB), 2 * (sel - NB) + 1)
+
+        def span(sel):
+            bs = grids(sel)
+            return bs[0] // 2, slice(bs[0] % 2, bs[0] % 2 + len(bs)), len(bs)
+
         def load_w2(h, g):
             for j in (2 * g, 2 * g + 1):
                 nc.sync.dma_start(
@@ -133,10 +122,9 @@ def tile_fluxgnn1dlatent_pb_kernel(tc, edge_hid, u, enc, W2, b2, W3, b3, out):
                 )
 
         def load_e(b):
-            nc.sync.dma_start(out=e_raw[b][:], in_=edge_hid[b, :, :].rearrange("(j p) k -> p j k", p=P))
-
-        def load_e_half(b, j):
-            nc.sync.dma_start(out=e_raw[b][:, j, :], in_=edge_hid[b, P * j : P * j + P, :])
+            nc.sync.dma_start(
+                out=e_raw[b][:].rearrange("p j k -> p (j k)"), in_=edge_hid[b, :, :].rearrange("(p j) k -> p (j k)", j=2)
+            )
 
         def load_w3(g):
             nc.sync.dma_start(
@@ -148,11 +136,9 @@ def tile_fluxgnn1dlatent_pb_kernel(tc, edge_hid, u, enc, W2, b2, W3, b3, out):
         nc.scalar.dma_start(out=vec_rows[8:12, :], in_=b3.rearrange("(j c) -> j c", c=P))
         nc.scalar.dma_start(out=vec_rows[12:16, :], in_=enc.rearrange("(j c) -> j c", c=P))
         load_w2(0, 0)
-        load_e_half(0, 0)
-        load_e_half(0, 1)
+        load_e(0)
         load_w2(0, 1)
-        load_e_half(1, 0)
-        load_e_half(1, 1)
+        load_e(1)
         nc.sync.dma_start(out=u_bf[:], in_=u)
         load_w2(1, 0)
         load_e(2)
@@ -162,6 +148,7 @@ def tile_fluxgnn1dlatent_pb_kernel(tc, edge_hid, u, enc, W2, b2, W3, b3, out):
         load_w3(1)
 
         nc.vector.memset(zero1[:], 0.0)
+        nc.vector.memset(warm[:], 0.0)
         nc.vector.memset(vec_f32[:], 0.0)
         nc.scalar.activation(out=junk1[:], in_=zero1[:], func=ACT.Gelu)
         make_identity(nc, ident[:])
@@ -179,6 +166,11 @@ def tile_fluxgnn1dlatent_pb_kernel(tc, edge_hid, u, enc, W2, b2, W3, b3, out):
                 out=dst[:, 4 * c0 : 4 * c1].rearrange("p (c i t) -> p c t i", i=4, t=4),
                 in_=src[:, :, c0:c1].rearrange("p t (c i) -> p c t i", i=4),
             )
+
+        def op_warm(n, b):
+            pad = psum.tile([P, 512], F32, name="pad", tag="mm", bufs=5)
+            for i in range(n):
+                nc.tensor.matmul(out=pad[:], lhsT=warm[:, 0:P], rhs=warm[:], start=True, stop=True)
 
         def op_vecT(a, b):
             bank["vec"] = psum.tile([P, P], F32, name="vec_t", tag="g", bufs=1)
@@ -223,96 +215,94 @@ def tile_fluxgnn1dlatent_pb_kernel(tc, edge_hid, u, enc, W2, b2, W3, b3, out):
         def op_qW3(g, b):
             nc.vector.quantize_mx(out=w3_cod[g][:].bitcast(FP8X4), scales=w3_scl[g][:], in_=w3_grp[g][:])
 
-        def op_tE(b, jj):
+        def op_tE(b, g):
             tp = psum.tile([P, 2, 2, P], F32, name="tp", tag="tp", bufs=2)
-            bank[("tp", b, jj)] = tp
-            words = e_raw[b][:, jj, :].bitcast(F32)
-            for g in range(2):
+            bank[("tp", b, g)] = tp
+            for jj in range(2):
+                words = e_raw[b][:, jj, :].bitcast(F32)
                 for uu in range(2):
                     w0 = 256 * g + 128 * uu
-                    nc.tensor.transpose(tp[:, g, uu, :], words[:, w0 : w0 + P], ident[:])
+                    nc.tensor.transpose(tp[:, jj, uu, :], words[:, w0 : w0 + P], ident[:])
 
-        def op_cE(b, jj):
+        def op_cE(b, g):
             nc.scalar.copy(
-                out=e_grp[b][:, :, 512 * jj : 512 * jj + 512].bitcast(F32).rearrange("p g (r w) -> p g r w", w=2),
-                in_=bank[("tp", b, jj)][:].rearrange("p g w r -> p g r w"),
+                out=e_grp[b][:, g, :].bitcast(F32).rearrange("p (r j w) -> p r j w", j=2, w=2),
+                in_=bank[("tp", b, g)][:].rearrange("p j w r -> p r j w"),
+            )
+
+        def op_vE(b, g):
+            nc.vector.tensor_copy(
+                out=e_grp[b][:, g, :].bitcast(F32).rearrange("p (r j w) -> p r j w", j=2, w=2),
+                in_=bank[("tp", b, g)][:].rearrange("p j w r -> p r j w"),
             )
 
         def op_qE(b, z):
-            k, i = home[b]
-            if len(BLOCKS[k]) == 1:
-                nc.vector.quantize_mx(
-                    out=e_cod[k][:].rearrange("p g r -> p (g r)").bitcast(FP8X4),
-                    scales=e_scl[k][:].rearrange("p g r -> p (g r)"),
-                    in_=e_grp[b][:].rearrange("p g c -> p (g c)"),
-                )
-            else:
+            nc.vector.quantize_mx(
+                out=e_cod[b][:].rearrange("p g r -> p (g r)").bitcast(FP8X4),
+                scales=e_scl[b][:].rearrange("p g r -> p (g r)"),
+                in_=e_grp[b][:].rearrange("p g c -> p (g c)"),
+            )
+
+        def op_mm1(m, sel):
+            h, t = divmod(m, 4)
+            acc = psum.tile([P, 2, NE], F32, name="acc1", tag="mm", bufs=5)
+            bank[("a1", m, sel)] = acc
+            for i, b in enumerate(grids(sel)):
                 for g in range(2):
-                    nc.vector.quantize_mx(
-                        out=e_cod[k][:, g, NE * i : NE * i + NE].bitcast(FP8X4),
-                        scales=e_scl[k][:, g, NE * i : NE * i + NE],
-                        in_=e_grp[b][:, g, :],
+                    nc.tensor.matmul_mx(
+                        out=acc[:, i, :],
+                        lhsT=w2_cod[h][:, g, P * t : P * t + P].bitcast(FP8X4),
+                        lhsT_scale=w2_scl[h][:, g, P * t : P * t + P],
+                        rhs=e_cod[b][:, g, :].bitcast(FP8X4),
+                        rhs_scale=e_scl[b][:, g, :],
+                        start=(g == 0),
+                        stop=(g == 1),
                     )
 
-        def op_mm1(m, k):
+        def op_gelu(m, sel):
             h, t = divmod(m, 4)
-            acc = psum.tile([P, 512], F32, name="acc1", tag="mm", bufs=5)
-            bank[("a1", m, k)] = acc
-            for g in range(2):
-                nc.tensor.matmul_mx(
-                    out=acc[:, 0 : width[k]],
-                    lhsT=w2_cod[h][:, g, P * t : P * t + P].bitcast(FP8X4),
-                    lhsT_scale=w2_scl[h][:, g, P * t : P * t + P],
-                    rhs=e_cod[k][:, g, :].bitcast(FP8X4),
-                    rhs_scale=e_scl[k][:, g, :],
-                    start=(g == 0),
-                    stop=(g == 1),
-                )
-
-        def op_gelu(m, k):
-            h, t = divmod(m, 4)
+            q, rows, n = span(sel)
             nc.scalar.activation(
-                out=x_pln[h][k][:, t, :], in_=bank[("a1", m, k)][:, 0 : width[k]], func=ACT.Gelu, bias=cols[:, m : m + 1]
+                out=x_pln[h][q][:, rows, t, :], in_=bank[("a1", m, sel)][:, 0:n, :], func=ACT.Gelu, bias=cols[:, m : m + 1]
             )
 
-        def op_rX(g, k):
-            regroup(nc.vector.tensor_copy, x_grp[g][k][:], x_pln[g][k][:], 0, width[k])
+        def op_rX(h, b):
+            regroup(nc.vector.tensor_copy, x_grp[h][b][:], x_pln[h][b // 2][:, b % 2, :, :], 0, NE)
 
-        def op_qX(g, k):
-            nc.vector.quantize_mx(out=x_cod[g][k][:].bitcast(FP8X4), scales=x_scl[g][k][:], in_=x_grp[g][k][:])
+        def op_qX(h, b):
+            nc.vector.quantize_mx(out=x_cod[h][b][:].bitcast(FP8X4), scales=x_scl[h][b][:], in_=x_grp[h][b][:])
 
-        def mm2(ct, k, g):
-            nc.tensor.matmul_mx(
-                out=bank[("a2", ct, k)][:, 0 : width[k]],
-                lhsT=w3_cod[g][:, P * ct : P * ct + P].bitcast(FP8X4),
-                lhsT_scale=w3_scl[g][:, P * ct : P * ct + P],
-                rhs=x_cod[g][k][:].bitcast(FP8X4),
-                rhs_scale=x_scl[g][k][:],
-                start=(g == 0),
-                stop=(g == 1),
-            )
+        def op_mm2(ct, sel):
+            acc = psum.tile([P, 2, NE], F32, name="acc2", tag="mm", bufs=5)
+            bank[("a2", ct, sel)] = acc
+            for i, b in enumerate(grids(sel)):
+                for g in range(2):
+                    nc.tensor.matmul_mx(
+                        out=acc[:, i, :],
+                        lhsT=w3_cod[g][:, P * ct : P * ct + P].bitcast(FP8X4),
+                        lhsT_scale=w3_scl[g][:, P * ct : P * ct + P],
+                        rhs=x_cod[g][b][:].bitcast(FP8X4),
+                        rhs_scale=x_scl[g][b][:],
+                        start=(g == 0),
+                        stop=(g == 1),
+                    )
 
-        def op_mm2a(ct, k):
-            bank[("a2", ct, k)] = psum.tile([P, 512], F32, name="acc2", tag="mm", bufs=5)
-            mm2(ct, k, 0)
-
-        def op_mm2b(ct, k):
-            mm2(ct, k, 1)
-
-        def op_tanh(ct, k):
+        def op_tanh(ct, sel):
+            q, rows, n = span(sel)
             nc.scalar.activation(
-                out=t_sb[ct][k][:], in_=bank[("a2", ct, k)][:, 0 : width[k]], func=ACT.Tanh, bias=cols[:, 8 + ct : 9 + ct]
+                out=t_sb[ct][q][:, rows, :], in_=bank[("a2", ct, sel)][:, 0:n, :], func=ACT.Tanh, bias=cols[:, 8 + ct : 9 + ct]
             )
 
-        def op_vs(ct, k):
-            if ct == VSUM[BLOCKS[k][0]][0]:
-                nc.vector.tensor_scalar_mul(out=wsum[k][:], in0=t_sb[ct][k][:], scalar1=cols[:, 12 + ct : 13 + ct])
+        def op_vs(ct, sel):
+            q, rows, n = span(sel)
+            if ct == VSUM[grids(sel)[0]][0]:
+                nc.vector.tensor_scalar_mul(out=wsum[q][:, rows, :], in0=t_sb[ct][q][:, rows, :], scalar1=cols[:, 12 + ct : 13 + ct])
             else:
                 nc.vector.scalar_tensor_tensor(
-                    out=wsum[k][:],
-                    in0=t_sb[ct][k][:],
+                    out=wsum[q][:, rows, :],
+                    in0=t_sb[ct][q][:, rows, :],
                     scalar=cols[:, 12 + ct : 13 + ct],
-                    in1=wsum[k][:],
+                    in1=wsum[q][:, rows, :],
                     op0=ALU.mult,
                     op1=ALU.add,
                 )
@@ -323,12 +313,10 @@ def tile_fluxgnn1dlatent_pb_kernel(tc, edge_hid, u, enc, W2, b2, W3, b3, out):
             nc.tensor.matmul(out=bank["gsum"][:], lhsT=lhsT, rhs=rhs, start=(op == sums[0]), stop=(op == sums[-1]))
 
         def op_ws(b, z):
-            k, i = home[b]
-            add_to_gsum(("ws", b, z), pick[:, P * b : P * b + P], wsum[k][:, NE * i : NE * i + NE])
+            add_to_gsum(("ws", b, z), pick[:, P * b : P * b + P], wsum[b // 2][:, b % 2, :])
 
         def op_wsd(ct, b):
-            k, i = home[b]
-            add_to_gsum(("wsd", ct, b), pick_enc[b][:, P * ct : P * ct + P], t_sb[ct][k][:, NE * i : NE * i + NE])
+            add_to_gsum(("wsd", ct, b), pick_enc[b][:, P * ct : P * ct + P], t_sb[ct][b // 2][:, b % 2, :])
 
         def op_f1(a, b):
             nc.vector.scalar_tensor_tensor(
@@ -341,10 +329,10 @@ def tile_fluxgnn1dlatent_pb_kernel(tc, edge_hid, u, enc, W2, b2, W3, b3, out):
             )
 
         ops = {
-            "vecT": op_vecT, "cols": op_cols, "den": op_den, "rinv": op_rinv, "coef": op_coef, "us": op_us,
+            "warm": op_warm, "vecT": op_vecT, "cols": op_cols, "den": op_den, "rinv": op_rinv, "coef": op_coef, "us": op_us,
             "rW2": op_rW2, "sW2": op_sW2, "qW2": op_qW2, "rW3": op_rW3, "sW3": op_sW3, "qW3": op_qW3,
-            "tE": op_tE, "cE": op_cE, "qE": op_qE, "mm1": op_mm1, "gelu": op_gelu,
-            "rX": op_rX, "qX": op_qX, "mm2a": op_mm2a, "mm2b": op_mm2b, "tanh": op_tanh,
+            "tE": op_tE, "cE": op_cE, "vE": op_vE, "qE": op_qE, "mm1": op_mm1, "gelu": op_gelu,
+            "rX": op_rX, "qX": op_qX, "mm2": op_mm2, "tanh": op_tanh,
             "vs": op_vs, "ws": op_ws, "wsd": op_wsd, "f1": op_f1, "f2": op_f2,
         }
         for name, a, b in ORDER:

@@ -18,40 +18,40 @@ NC = 255
 HID = 1024
 LD = 512
 COEF = 0.5 * 0.25
-S_COLS = {(0, 0): 160, (0, 1): 140}
-S3_COLS = {0: 192, 1: 192}
+S_COLS = {}
+S3_COLS = {0: 128, 1: 128}
 VSUM = {0: (0, 1, 2, 3,), 1: (0, 1, 2, 3,), 2: (0, 1, 2, 3,), 3: (1, 2, 3,)}
 DIRECT = tuple(b for b in range(NB) if len(VSUM[b]) < 4)
 
 FLOPS = 2 * NB * NE * HID * HID + 2 * NB * NE * HID * LD
 
 ORDER = (
-    ("rW2", 0, 0), ("den", 0, 0), ("sW2", 0, 0), ("warm", 8, 0), ("tE", 0, 0), ("tE", 0, 1), ("vecT", 0, 0),
-    ("warm", 4, 1), ("qW2", 0, 0), ("rW2", 0, 1), ("cE", 0, 0), ("cE", 0, 1), ("sW2", 0, 1), ("cols", 0, 0),
-    ("tE", 1, 0), ("tE", 1, 1), ("warm", 2, 2), ("qE", 0, 0), ("qW2", 0, 1), ("rW2", 1, 0), ("cE", 1, 0),
-    ("cE", 1, 1), ("mm1", 0, 0), ("mm1", 1, 0), ("mm1", 2, 0), ("mm1", 3, 0), ("tE", 2, 0), ("tE", 2, 1),
-    ("qE", 1, 0), ("qW2", 1, 0), ("rW2", 1, 1), ("gelu", 0, 0), ("gelu", 1, 0), ("gelu", 2, 0), ("gelu", 3, 0),
-    ("cE", 2, 0), ("cE", 2, 1), ("mm1", 0, 1), ("mm1", 1, 1), ("mm1", 2, 1), ("mm1", 3, 1), ("tE", 3, 0),
-    ("tE", 3, 1), ("rX", 0, 0), ("qW2", 1, 1), ("qE", 2, 0), ("gelu", 0, 1), ("gelu", 1, 1), ("gelu", 2, 1),
-    ("gelu", 3, 1), ("cE", 3, 0), ("cE", 3, 1), ("mm1", 4, 0), ("mm1", 5, 0), ("mm1", 6, 0), ("mm1", 7, 0),
-    ("mm1", 0, 2), ("rX", 0, 1), ("qE", 3, 0), ("qX", 0, 0), ("gelu", 4, 0), ("gelu", 5, 0), ("gelu", 6, 0),
-    ("gelu", 7, 0), ("sW3", 0, 0), ("gelu", 0, 2), ("mm1", 1, 2), ("mm1", 2, 2), ("mm1", 3, 2), ("mm1", 4, 1),
-    ("mm1", 5, 1), ("rX", 1, 0), ("qX", 0, 1), ("rW3", 0, 0), ("qX", 1, 0), ("rW3", 1, 0), ("qW3", 0, 0),
-    ("gelu", 1, 2), ("gelu", 2, 2), ("gelu", 3, 2), ("gelu", 4, 1), ("gelu", 5, 1), ("mm1", 6, 1), ("mm1", 7, 1),
-    ("mm1", 4, 2), ("mm1", 5, 2), ("mm1", 6, 2), ("rX", 0, 2), ("gelu", 6, 1), ("gelu", 7, 1), ("sW3", 1, 0),
-    ("gelu", 4, 2), ("gelu", 5, 2), ("gelu", 6, 2), ("mm1", 7, 2), ("mm1", 0, 3), ("mm1", 1, 3), ("mm1", 2, 3),
-    ("mm1", 3, 3), ("qW3", 1, 0), ("rX", 1, 1), ("qX", 0, 2), ("gelu", 7, 2), ("gelu", 0, 3), ("gelu", 1, 3),
-    ("gelu", 2, 3), ("gelu", 3, 3), ("mm1", 4, 3), ("mm1", 5, 3), ("mm1", 6, 3), ("mm1", 7, 3), ("mm2", 0, 0),
-    ("rX", 1, 2), ("qX", 1, 1), ("rX", 0, 3), ("qX", 1, 2), ("gelu", 4, 3), ("gelu", 5, 3), ("gelu", 6, 3),
-    ("gelu", 7, 3), ("tanh", 0, 0), ("mm2", 1, 0), ("mm2", 2, 0), ("mm2", 3, 0), ("mm2", 0, 1), ("mm2", 1, 1),
-    ("rX", 1, 3), ("qX", 0, 3), ("qX", 1, 3), ("vs", 0, 0), ("tanh", 1, 0), ("tanh", 2, 0), ("tanh", 3, 0),
-    ("tanh", 0, 1), ("tanh", 1, 1), ("mm2", 2, 1), ("mm2", 3, 1), ("mm2", 0, 2), ("mm2", 1, 2), ("mm2", 2, 2),
-    ("vs", 0, 1), ("vs", 1, 0), ("vs", 1, 1), ("vs", 2, 0), ("tanh", 2, 1), ("tanh", 3, 1), ("tanh", 0, 2),
-    ("tanh", 1, 2), ("tanh", 2, 2), ("mm2", 3, 2), ("mm2", 0, 3), ("mm2", 1, 3), ("mm2", 2, 3), ("mm2", 3, 3),
-    ("vs", 0, 2), ("vs", 2, 1), ("vs", 3, 0), ("vs", 1, 2), ("vs", 3, 1), ("vs", 2, 2), ("tanh", 3, 2),
-    ("tanh", 0, 3), ("tanh", 1, 3), ("tanh", 2, 3), ("tanh", 3, 3), ("ws", 0, 0), ("ws", 1, 0), ("wsd", 0, 3),
-    ("vs", 1, 3), ("vs", 3, 2), ("rinv", 0, 0), ("vs", 2, 3), ("coef", 0, 0), ("vs", 3, 3), ("us", 0, 0),
-    ("ws", 2, 0), ("ws", 3, 0), ("f1", 0, 0), ("f2", 0, 0),
+    ("rW2", 0, 0), ("den", 0, 0), ("qW2", 0, 0), ("rW2", 0, 1), ("warm", 8, 0), ("tE", 0, 0), ("tE", 0, 1),
+    ("vecT", 0, 0), ("warm", 4, 1), ("cE", 0, 0), ("cE", 0, 1), ("cols", 0, 0), ("tE", 1, 0), ("tE", 1, 1),
+    ("warm", 2, 2), ("qE", 0, 0), ("qW2", 0, 1), ("rW2", 1, 0), ("cE", 1, 0), ("cE", 1, 1), ("mm1", 0, 0),
+    ("mm1", 1, 0), ("mm1", 2, 0), ("mm1", 3, 0), ("tE", 2, 0), ("tE", 2, 1), ("qE", 1, 0), ("qW2", 1, 0),
+    ("rW2", 1, 1), ("gelu", 0, 0), ("gelu", 1, 0), ("gelu", 2, 0), ("gelu", 3, 0), ("cE", 2, 0), ("cE", 2, 1),
+    ("mm1", 0, 1), ("mm1", 1, 1), ("mm1", 2, 1), ("mm1", 3, 1), ("tE", 3, 0), ("tE", 3, 1), ("rX", 0, 0),
+    ("qW2", 1, 1), ("qE", 2, 0), ("gelu", 0, 1), ("gelu", 1, 1), ("gelu", 2, 1), ("gelu", 3, 1), ("cE", 3, 0),
+    ("cE", 3, 1), ("mm1", 4, 0), ("mm1", 5, 0), ("mm1", 6, 0), ("mm1", 7, 0), ("mm1", 0, 2), ("rX", 0, 1),
+    ("qE", 3, 0), ("rW3", 0, 0), ("qX", 0, 0), ("gelu", 4, 0), ("gelu", 5, 0), ("gelu", 6, 0), ("gelu", 7, 0),
+    ("sW3", 0, 0), ("gelu", 0, 2), ("mm1", 1, 2), ("mm1", 2, 2), ("mm1", 3, 2), ("mm1", 4, 1), ("mm1", 5, 1),
+    ("rX", 1, 0), ("qX", 0, 1), ("qX", 1, 0), ("rW3", 1, 0), ("qW3", 0, 0), ("gelu", 1, 2), ("gelu", 2, 2),
+    ("gelu", 3, 2), ("gelu", 4, 1), ("gelu", 5, 1), ("mm1", 6, 1), ("mm1", 7, 1), ("mm1", 4, 2), ("mm1", 5, 2),
+    ("mm1", 6, 2), ("rX", 0, 2), ("gelu", 6, 1), ("gelu", 7, 1), ("sW3", 1, 0), ("gelu", 4, 2), ("gelu", 5, 2),
+    ("gelu", 6, 2), ("mm1", 7, 2), ("mm1", 0, 3), ("mm1", 1, 3), ("mm1", 2, 3), ("mm1", 3, 3), ("qW3", 1, 0),
+    ("rX", 1, 1), ("qX", 0, 2), ("gelu", 7, 2), ("gelu", 0, 3), ("gelu", 1, 3), ("gelu", 2, 3), ("gelu", 3, 3),
+    ("mm1", 4, 3), ("mm1", 5, 3), ("mm1", 6, 3), ("mm1", 7, 3), ("mm2", 0, 0), ("rX", 1, 2), ("qX", 1, 1),
+    ("rX", 0, 3), ("qX", 1, 2), ("gelu", 4, 3), ("gelu", 5, 3), ("gelu", 6, 3), ("gelu", 7, 3), ("tanh", 0, 0),
+    ("mm2", 1, 0), ("mm2", 2, 0), ("mm2", 3, 0), ("mm2", 0, 1), ("mm2", 1, 1), ("rX", 1, 3), ("qX", 0, 3),
+    ("qX", 1, 3), ("vs", 0, 0), ("tanh", 1, 0), ("tanh", 2, 0), ("tanh", 3, 0), ("tanh", 0, 1), ("tanh", 1, 1),
+    ("mm2", 2, 1), ("mm2", 3, 1), ("mm2", 0, 2), ("mm2", 1, 2), ("mm2", 2, 2), ("vs", 0, 1), ("vs", 1, 0),
+    ("vs", 1, 1), ("vs", 2, 0), ("tanh", 2, 1), ("tanh", 3, 1), ("tanh", 0, 2), ("tanh", 1, 2), ("tanh", 2, 2),
+    ("mm2", 3, 2), ("mm2", 0, 3), ("mm2", 1, 3), ("mm2", 2, 3), ("mm2", 3, 3), ("vs", 0, 2), ("vs", 2, 1),
+    ("vs", 3, 0), ("vs", 1, 2), ("vs", 3, 1), ("vs", 2, 2), ("tanh", 3, 2), ("tanh", 0, 3), ("tanh", 1, 3),
+    ("tanh", 2, 3), ("tanh", 3, 3), ("ws", 0, 0), ("ws", 1, 0), ("wsd", 0, 3), ("vs", 1, 3), ("vs", 3, 2),
+    ("rinv", 0, 0), ("vs", 2, 3), ("coef", 0, 0), ("vs", 3, 3), ("us", 0, 0), ("ws", 2, 0), ("ws", 3, 0),
+    ("f1", 0, 0), ("f2", 0, 0),
 )
 
 

@@ -17,42 +17,13 @@ NE = 256
 NC = 255
 HID = 1024
 LD = 512
+HALF = 512
 COEF = 0.5 * 0.25
-S_COLS = {}
-S3_COLS = {0: 128, 1: 128}
-VSUM = {0: (0, 1, 2, 3,), 1: (0, 1, 2, 3,), 2: (0, 1, 2, 3,), 3: (1, 2, 3,)}
-DIRECT = tuple(b for b in range(NB) if len(VSUM[b]) < 4)
+W3_SCALAR = 128
+LAG = (0, 0, 2, 3)
+DIRECT = 3
 
 FLOPS = 2 * NB * NE * HID * HID + 2 * NB * NE * HID * LD
-
-ORDER = (
-    ("rW2", 0, 0), ("den", 0, 0), ("qW2", 0, 0), ("rW2", 0, 1), ("warm", 8, 0), ("tE", 0, 0), ("tE", 0, 1),
-    ("vecT", 0, 0), ("warm", 4, 1), ("cE", 0, 0), ("cE", 0, 1), ("cols", 0, 0), ("tE", 1, 0), ("tE", 1, 1),
-    ("warm", 2, 2), ("qE", 0, 0), ("qW2", 0, 1), ("rW2", 1, 0), ("cE", 1, 0), ("cE", 1, 1), ("mm1", 0, 0),
-    ("mm1", 1, 0), ("mm1", 2, 0), ("mm1", 3, 0), ("tE", 2, 0), ("tE", 2, 1), ("qE", 1, 0), ("qW2", 1, 0),
-    ("rW2", 1, 1), ("gelu", 0, 0), ("gelu", 1, 0), ("gelu", 2, 0), ("gelu", 3, 0), ("cE", 2, 0), ("cE", 2, 1),
-    ("mm1", 0, 1), ("mm1", 1, 1), ("mm1", 2, 1), ("mm1", 3, 1), ("tE", 3, 0), ("tE", 3, 1), ("rX", 0, 0),
-    ("qW2", 1, 1), ("qE", 2, 0), ("gelu", 0, 1), ("gelu", 1, 1), ("gelu", 2, 1), ("gelu", 3, 1), ("cE", 3, 0),
-    ("cE", 3, 1), ("mm1", 4, 0), ("mm1", 5, 0), ("mm1", 6, 0), ("mm1", 7, 0), ("mm1", 0, 2), ("rX", 0, 1),
-    ("qE", 3, 0), ("rW3", 0, 0), ("qX", 0, 0), ("gelu", 4, 0), ("gelu", 5, 0), ("gelu", 6, 0), ("gelu", 7, 0),
-    ("sW3", 0, 0), ("gelu", 0, 2), ("mm1", 1, 2), ("mm1", 2, 2), ("mm1", 3, 2), ("mm1", 4, 1), ("mm1", 5, 1),
-    ("rX", 1, 0), ("qX", 0, 1), ("qX", 1, 0), ("rW3", 1, 0), ("qW3", 0, 0), ("gelu", 1, 2), ("gelu", 2, 2),
-    ("gelu", 3, 2), ("gelu", 4, 1), ("gelu", 5, 1), ("mm1", 6, 1), ("mm1", 7, 1), ("mm1", 4, 2), ("mm1", 5, 2),
-    ("mm1", 6, 2), ("rX", 0, 2), ("gelu", 6, 1), ("gelu", 7, 1), ("sW3", 1, 0), ("gelu", 4, 2), ("gelu", 5, 2),
-    ("gelu", 6, 2), ("mm1", 7, 2), ("mm1", 0, 3), ("mm1", 1, 3), ("mm1", 2, 3), ("mm1", 3, 3), ("qW3", 1, 0),
-    ("rX", 1, 1), ("qX", 0, 2), ("gelu", 7, 2), ("gelu", 0, 3), ("gelu", 1, 3), ("gelu", 2, 3), ("gelu", 3, 3),
-    ("mm1", 4, 3), ("mm1", 5, 3), ("mm1", 6, 3), ("mm1", 7, 3), ("mm2", 0, 0), ("rX", 1, 2), ("qX", 1, 1),
-    ("rX", 0, 3), ("qX", 1, 2), ("gelu", 4, 3), ("gelu", 5, 3), ("gelu", 6, 3), ("gelu", 7, 3), ("tanh", 0, 0),
-    ("mm2", 1, 0), ("mm2", 2, 0), ("mm2", 3, 0), ("mm2", 0, 1), ("mm2", 1, 1), ("rX", 1, 3), ("qX", 0, 3),
-    ("qX", 1, 3), ("vs", 0, 0), ("tanh", 1, 0), ("tanh", 2, 0), ("tanh", 3, 0), ("tanh", 0, 1), ("tanh", 1, 1),
-    ("mm2", 2, 1), ("mm2", 3, 1), ("mm2", 0, 2), ("mm2", 1, 2), ("mm2", 2, 2), ("vs", 0, 1), ("vs", 1, 0),
-    ("vs", 1, 1), ("vs", 2, 0), ("tanh", 2, 1), ("tanh", 3, 1), ("tanh", 0, 2), ("tanh", 1, 2), ("tanh", 2, 2),
-    ("mm2", 3, 2), ("mm2", 0, 3), ("mm2", 1, 3), ("mm2", 2, 3), ("mm2", 3, 3), ("vs", 0, 2), ("vs", 2, 1),
-    ("vs", 3, 0), ("vs", 1, 2), ("vs", 3, 1), ("vs", 2, 2), ("tanh", 3, 2), ("tanh", 0, 3), ("tanh", 1, 3),
-    ("tanh", 2, 3), ("tanh", 3, 3), ("ws", 0, 0), ("ws", 1, 0), ("wsd", 0, 3), ("vs", 1, 3), ("vs", 3, 2),
-    ("rinv", 0, 0), ("vs", 2, 3), ("coef", 0, 0), ("vs", 3, 3), ("us", 0, 0), ("ws", 2, 0), ("ws", 3, 0),
-    ("f1", 0, 0), ("f2", 0, 0),
-)
 
 
 def tile_fluxgnn1dlatent_pb_kernel(tc, edge_hid, u, enc, W2, b2, W3, b3, out):
@@ -61,40 +32,39 @@ def tile_fluxgnn1dlatent_pb_kernel(tc, edge_hid, u, enc, W2, b2, W3, b3, out):
         keep = ctx.enter_context(tc.tile_pool(name="keep", bufs=1))
         psum = ctx.enter_context(tc.psum_pool(name="psum", bufs=1))
         ctx.enter_context(tc.manual_schedule())
-        sums = [op for op in ORDER if op[0] in ("ws", "wsd")]
 
         e_raw = [keep.tile([P, 2, HID], BF16, name="e_raw%d" % b) for b in range(NB)]
         e_grp = [keep.tile([P, 2, 4 * NE], BF16, name="e_grp%d" % b, align_bytes=64) for b in range(NB)]
         e_cod = [keep.tile([P, 2, NE], U32, name="e_cod%d" % b, align_bytes=64) for b in range(NB)]
         e_scl = [keep.tile([P, 2, NE], U8, name="e_scl%d" % b, align_bytes=64) for b in range(NB)]
-        w2_raw = [keep.tile([P, 8, 512], BF16, name="w2_raw%d" % h) for h in range(2)]
-        w2_grp = [keep.tile([P, 2, 2048], BF16, name="w2_grp%d" % h, align_bytes=64) for h in range(2)]
-        w2_cod = [keep.tile([P, 2, 512], U32, name="w2_cod%d" % h, align_bytes=64) for h in range(2)]
-        w2_scl = [keep.tile([P, 2, 512], U8, name="w2_scl%d" % h, align_bytes=64) for h in range(2)]
-        w3_raw = [keep.tile([P, 4, LD], BF16, name="w3_raw%d" % g) for g in range(2)]
-        w3_grp = [keep.tile([P, 4 * LD], BF16, name="w3_grp%d" % g, align_bytes=64) for g in range(2)]
-        w3_cod = [keep.tile([P, LD], U32, name="w3_cod%d" % g, align_bytes=64) for g in range(2)]
-        w3_scl = [keep.tile([P, LD], U8, name="w3_scl%d" % g, align_bytes=64) for g in range(2)]
-        x_pln = [[keep.tile([P, 2, 4, NE], BF16, name="x_pln%d_%d" % (h, q)) for q in range(2)] for h in range(2)]
-        x_grp = [[keep.tile([P, 4 * NE], BF16, name="x_grp%d_%d" % (h, b), align_bytes=64) for b in range(NB)] for h in range(2)]
+        w2_raw = [keep.tile([P, 8, HALF], BF16, name="w2_raw%d" % h) for h in range(2)]
+        w2_grp = [keep.tile([P, 2, 4 * HALF], BF16, name="w2_grp%d" % h, align_bytes=64) for h in range(2)]
+        w2_cod = [keep.tile([P, 2, HALF], U32, name="w2_cod%d" % h, align_bytes=64) for h in range(2)]
+        w2_scl = [keep.tile([P, 2, HALF], U8, name="w2_scl%d" % h, align_bytes=64) for h in range(2)]
+        w3_raw = [keep.tile([P, 4, LD], BF16, name="w3_raw%d" % h) for h in range(2)]
+        w3_grp = [keep.tile([P, 4 * LD], BF16, name="w3_grp%d" % h, align_bytes=64) for h in range(2)]
+        w3_cod = [keep.tile([P, LD], U32, name="w3_cod%d" % h, align_bytes=64) for h in range(2)]
+        w3_scl = [keep.tile([P, LD], U8, name="w3_scl%d" % h, align_bytes=64) for h in range(2)]
+        x_raw = [[keep.tile([P, 4, NE], BF16, name="x_raw%d_%d" % (h, b)) for b in range(NB)] for h in range(2)]
+        x_grp = [
+            [keep.tile([P, 4 * NE], BF16, name="x_grp%d_%d" % (h, b), align_bytes=64) for b in range(NB)] for h in range(2)
+        ]
         x_cod = [[keep.tile([P, NE], U32, name="x_cod%d_%d" % (h, b), align_bytes=64) for b in range(NB)] for h in range(2)]
         x_scl = [[keep.tile([P, NE], U8, name="x_scl%d_%d" % (h, b), align_bytes=64) for b in range(NB)] for h in range(2)]
-        t_sb = [[keep.tile([P, 2, NE], F32, name="t_sb%d_%d" % (ct, q)) for q in range(2)] for ct in range(4)]
-        wsum = [keep.tile([P, 2, NE], F32, name="wsum%d" % q) for q in range(2)]
+        flux = [[keep.tile([P, NE], F32, name="flux%d_%d" % (ct, b)) for b in range(NB)] for ct in range(4)]
+        wsum = [keep.tile([P, NE], F32, name="wsum%d" % b) for b in range(NB)]
 
         ident = keep.tile([P, P], F32, name="ident")
         pick = keep.tile([P, NB * P], F32, name="pick")
-        pick_enc = {}
-        for b in DIRECT:
-            pick_enc[b] = keep.tile([P, 4 * P], F32, name="pick_enc%d" % b)
+        pick_enc = keep.tile([P, P], F32, name="pick_enc")
         vec_rows = keep.tile([16, P], BF16, name="vec_rows")
         vec_f32 = keep.tile([P, P], F32, name="vec_f32")
         cols = keep.tile([P, 16], F32, name="cols")
-        zero1 = keep.tile([P, 1], F32, name="zero1")
-        junk1 = keep.tile([P, 1], F32, name="junk1")
-        warm = keep.tile([P, 512], BF16, name="warm")
-        u_bf = keep.tile([NB, NC], BF16, name="u_bf")
-        u_s = keep.tile([NB, NC], F32, name="u_s")
+        dummy_in = keep.tile([P, 1], F32, name="dummy_in")
+        dummy_out = keep.tile([P, 1], F32, name="dummy_out")
+        zeros = keep.tile([P, 512], BF16, name="zeros")
+        u_raw = keep.tile([NB, NC], BF16, name="u_raw")
+        u_part = keep.tile([NB, NC], F32, name="u_part")
         enc_rows = keep.tile([NB, LD], BF16, name="enc_rows")
         enc_sq = keep.tile([NB, LD], F32, name="enc_sq")
         ssum = keep.tile([NB, 1], F32, name="ssum")
@@ -105,20 +75,12 @@ def tile_fluxgnn1dlatent_pb_kernel(tc, edge_hid, u, enc, W2, b2, W3, b3, out):
         c_neg = keep.tile([NB, 1], F32, name="c_neg")
         part = keep.tile([NB, NC], F32, name="part")
         res = keep.tile([NB, NC], F32, name="res")
-        bank = {}
-
-        def grids(sel):
-            return (sel,) if sel < NB else (2 * (sel - NB), 2 * (sel - NB) + 1)
-
-        def span(sel):
-            bs = grids(sel)
-            return bs[0] // 2, slice(bs[0] % 2, bs[0] % 2 + len(bs)), len(bs)
 
         def load_w2(h, g):
             for j in (2 * g, 2 * g + 1):
                 nc.sync.dma_start(
                     out=w2_raw[h][:, 2 * j : 2 * j + 2, :],
-                    in_=W2[256 * j : 256 * j + 256, 512 * h : 512 * h + 512].rearrange("(p e) n -> p e n", e=2),
+                    in_=W2[256 * j : 256 * j + 256, HALF * h : HALF * h + HALF].rearrange("(p e) n -> p e n", e=2),
                 )
 
         def load_e(b):
@@ -126,9 +88,9 @@ def tile_fluxgnn1dlatent_pb_kernel(tc, edge_hid, u, enc, W2, b2, W3, b3, out):
                 out=e_raw[b][:].rearrange("p j k -> p (j k)"), in_=edge_hid[b, :, :].rearrange("(p j) k -> p (j k)", j=2)
             )
 
-        def load_w3(g):
+        def load_w3(h):
             nc.sync.dma_start(
-                out=w3_raw[g][:], in_=W3[512 * g : 512 * g + 512, :].rearrange("(t p) c -> p t c", p=P)
+                out=w3_raw[h][:], in_=W3[HALF * h : HALF * h + HALF, :].rearrange("(t p) c -> p t c", p=P)
             )
 
         nc.sync.dma_start(out=enc_rows[:], in_=enc.partition_broadcast(NB))
@@ -137,9 +99,9 @@ def tile_fluxgnn1dlatent_pb_kernel(tc, edge_hid, u, enc, W2, b2, W3, b3, out):
         nc.scalar.dma_start(out=vec_rows[12:16, :], in_=enc.rearrange("(j c) -> j c", c=P))
         load_w2(0, 0)
         load_e(0)
+        nc.sync.dma_start(out=u_raw[:], in_=u)
         load_w2(0, 1)
         load_e(1)
-        nc.sync.dma_start(out=u_bf[:], in_=u)
         load_w2(1, 0)
         load_e(2)
         load_w2(1, 1)
@@ -147,110 +109,90 @@ def tile_fluxgnn1dlatent_pb_kernel(tc, edge_hid, u, enc, W2, b2, W3, b3, out):
         load_w3(0)
         load_w3(1)
 
-        nc.vector.memset(zero1[:], 0.0)
-        nc.vector.memset(warm[:], 0.0)
+        nc.vector.memset(dummy_in[:], 0.0)
+        nc.vector.memset(zeros[:], 0.0)
         nc.vector.memset(vec_f32[:], 0.0)
-        nc.scalar.activation(out=junk1[:], in_=zero1[:], func=ACT.Gelu)
+        nc.scalar.activation(out=dummy_out[:], in_=dummy_in[:], func=ACT.Gelu)
         make_identity(nc, ident[:])
         nc.gpsimd.tensor_copy(out=vec_f32[0:16, :], in_=vec_rows[:])
         nc.vector.memset(pick[:], 0.0)
         nc.vector.memset(pick[:, 0 : (NB - 1) * (P + 1) + 1 : P + 1], 1.0)
-        for b in DIRECT:
-            nc.vector.memset(pick_enc[b][:], 0.0)
+        nc.vector.memset(pick_enc[:], 0.0)
         nc.vector.scalar_tensor_tensor(
             out=enc_sq[:], in0=enc_rows[:], scalar=1.0, in1=enc_rows[:], op0=ALU.mult, op1=ALU.mult, accum_out=ssum[:]
         )
+        nc.vector.tensor_scalar_add(out=den[:], in0=ssum[:], scalar1=1e-12)
+        nc.vector.reciprocal(out=rinv[:], in_=den[:])
 
-        def regroup(engine_copy, dst, src, c0, c1):
-            engine_copy(
-                out=dst[:, 4 * c0 : 4 * c1].rearrange("p (c i t) -> p c t i", i=4, t=4),
-                in_=src[:, :, c0:c1].rearrange("p t (c i) -> p c t i", i=4),
+        def warm_up(count):
+            spare = psum.tile([P, 512], F32, name="spare", tag="acc", bufs=5)
+            for i in range(count):
+                nc.tensor.matmul(out=spare[:], lhsT=zeros[:, 0:P], rhs=zeros[:], start=True, stop=True)
+
+        def interleave(copy, grp, raw, c0, c1):
+            copy(
+                out=grp[:, 4 * c0 : 4 * c1].rearrange("p (c i t) -> p c t i", i=4, t=4),
+                in_=raw[:, :, c0:c1].rearrange("p t (c i) -> p c t i", i=4),
             )
 
-        def op_warm(n, b):
-            pad = psum.tile([P, 512], F32, name="pad", tag="mm", bufs=5)
-            for i in range(n):
-                nc.tensor.matmul(out=pad[:], lhsT=warm[:, 0:P], rhs=warm[:], start=True, stop=True)
+        def interleave_w2(h, g):
+            interleave(nc.vector.tensor_copy, w2_grp[h][:, g, :], w2_raw[h][:, 4 * g : 4 * g + 4, :], 0, HALF)
 
-        def op_vecT(a, b):
-            bank["vec"] = psum.tile([P, P], F32, name="vec_t", tag="g", bufs=1)
-            nc.tensor.transpose(bank["vec"][:], vec_f32[:], ident[:])
-
-        def op_cols(a, b):
-            nc.scalar.copy(out=cols[:], in_=bank["vec"][:, 0:16])
-            for d in DIRECT:
-                nc.gpsimd.tensor_copy(out=pick_enc[d][:, d : 4 * P : P], in_=cols[:, 12:16])
-
-        def op_den(a, b):
-            nc.vector.tensor_scalar_add(out=den[:], in0=ssum[:], scalar1=1e-12)
-
-        def op_rinv(a, b):
-            nc.vector.reciprocal(out=rinv[:], in_=den[:])
-
-        def op_coef(a, b):
-            nc.vector.tensor_scalar_mul(out=c_u[:], in0=ssum[:], scalar1=rinv[:, 0:1])
-            nc.vector.tensor_scalar_mul(out=c_pos[:], in0=rinv[:], scalar1=COEF)
-            nc.vector.tensor_scalar_mul(out=c_neg[:], in0=rinv[:], scalar1=-COEF)
-
-        def op_us(a, b):
-            nc.vector.tensor_scalar_mul(out=u_s[:], in0=u_bf[:], scalar1=c_u[:, 0:1])
-
-        def op_rW2(h, g):
-            regroup(nc.vector.tensor_copy, w2_grp[h][:, g, :], w2_raw[h][:, 4 * g : 4 * g + 4, :], 0, 512 - S_COLS.get((h, g), 0))
-
-        def op_sW2(h, g):
-            regroup(nc.scalar.copy, w2_grp[h][:, g, :], w2_raw[h][:, 4 * g : 4 * g + 4, :], 512 - S_COLS[(h, g)], 512)
-
-        def op_qW2(h, g):
+        def quantise_w2(h, g):
             nc.vector.quantize_mx(
                 out=w2_cod[h][:, g, :].bitcast(FP8X4), scales=w2_scl[h][:, g, :], in_=w2_grp[h][:, g, :]
             )
 
-        def op_rW3(g, b):
-            regroup(nc.vector.tensor_copy, w3_grp[g][:], w3_raw[g][:], 0, LD - S3_COLS.get(g, 0))
+        def interleave_w3(h):
+            interleave(nc.vector.tensor_copy, w3_grp[h][:], w3_raw[h][:], 0, LD - W3_SCALAR)
+            interleave(nc.scalar.copy, w3_grp[h][:], w3_raw[h][:], LD - W3_SCALAR, LD)
 
-        def op_sW3(g, b):
-            regroup(nc.scalar.copy, w3_grp[g][:], w3_raw[g][:], LD - S3_COLS[g], LD)
+        def quantise_w3(h):
+            nc.vector.quantize_mx(out=w3_cod[h][:].bitcast(FP8X4), scales=w3_scl[h][:], in_=w3_grp[h][:])
 
-        def op_qW3(g, b):
-            nc.vector.quantize_mx(out=w3_cod[g][:].bitcast(FP8X4), scales=w3_scl[g][:], in_=w3_grp[g][:])
+        def turn_e(b):
+            turned = []
+            for g in range(2):
+                tp = psum.tile([P, 2, 2, P], F32, name="tp", tag="tp", bufs=2)
+                turned.append(tp)
+                for j in range(2):
+                    words = e_raw[b][:, j, :].bitcast(F32)
+                    for uu in range(2):
+                        w0 = 256 * g + 128 * uu
+                        nc.tensor.transpose(tp[:, j, uu, :], words[:, w0 : w0 + P], ident[:])
+            for g in range(2):
+                nc.scalar.copy(
+                    out=e_grp[b][:, g, :].bitcast(F32).rearrange("p (r j w) -> p r j w", j=2, w=2),
+                    in_=turned[g][:].rearrange("p j w r -> p r j w"),
+                )
 
-        def op_tE(b, g):
-            tp = psum.tile([P, 2, 2, P], F32, name="tp", tag="tp", bufs=2)
-            bank[("tp", b, g)] = tp
-            for jj in range(2):
-                words = e_raw[b][:, jj, :].bitcast(F32)
-                for uu in range(2):
-                    w0 = 256 * g + 128 * uu
-                    nc.tensor.transpose(tp[:, jj, uu, :], words[:, w0 : w0 + P], ident[:])
-
-        def op_cE(b, g):
-            nc.scalar.copy(
-                out=e_grp[b][:, g, :].bitcast(F32).rearrange("p (r j w) -> p r j w", j=2, w=2),
-                in_=bank[("tp", b, g)][:].rearrange("p j w r -> p r j w"),
-            )
-
-        def op_vE(b, g):
-            nc.vector.tensor_copy(
-                out=e_grp[b][:, g, :].bitcast(F32).rearrange("p (r j w) -> p r j w", j=2, w=2),
-                in_=bank[("tp", b, g)][:].rearrange("p j w r -> p r j w"),
-            )
-
-        def op_qE(b, z):
+        def quantise_e(b):
             nc.vector.quantize_mx(
                 out=e_cod[b][:].rearrange("p g r -> p (g r)").bitcast(FP8X4),
                 scales=e_scl[b][:].rearrange("p g r -> p (g r)"),
                 in_=e_grp[b][:].rearrange("p g c -> p (g c)"),
             )
 
-        def op_mm1(m, sel):
-            h, t = divmod(m, 4)
-            acc = psum.tile([P, 2, NE], F32, name="acc1", tag="mm", bufs=5)
-            bank[("a1", m, sel)] = acc
-            for i, b in enumerate(grids(sel)):
+        def turn_vectors():
+            vec_t = psum.tile([P, P], F32, name="vec_t", tag="sum", bufs=1)
+            nc.tensor.transpose(vec_t[:], vec_f32[:], ident[:])
+            nc.scalar.copy(out=cols[:], in_=vec_t[:, 0:16])
+            nc.gpsimd.tensor_copy(out=pick_enc[:, DIRECT : DIRECT + 1], in_=cols[:, 12:13])
+
+        def coefficients():
+            nc.vector.tensor_scalar_mul(out=c_u[:], in0=ssum[:], scalar1=rinv[:, 0:1])
+            nc.vector.tensor_scalar_mul(out=c_pos[:], in0=rinv[:], scalar1=COEF)
+            nc.vector.tensor_scalar_mul(out=c_neg[:], in0=rinv[:], scalar1=-COEF)
+
+        def scale_u():
+            nc.vector.tensor_scalar_mul(out=u_part[:], in0=u_raw[:], scalar1=c_u[:, 0:1])
+
+        def layer1(h, b):
+            for t in range(4):
+                acc = psum.tile([P, 512], F32, name="acc1", tag="acc", bufs=5)
                 for g in range(2):
                     nc.tensor.matmul_mx(
-                        out=acc[:, i, :],
+                        out=acc[:, 0:NE],
                         lhsT=w2_cod[h][:, g, P * t : P * t + P].bitcast(FP8X4),
                         lhsT_scale=w2_scl[h][:, g, P * t : P * t + P],
                         rhs=e_cod[b][:, g, :].bitcast(FP8X4),
@@ -258,84 +200,122 @@ def tile_fluxgnn1dlatent_pb_kernel(tc, edge_hid, u, enc, W2, b2, W3, b3, out):
                         start=(g == 0),
                         stop=(g == 1),
                     )
+                m = 4 * h + t
+                nc.scalar.activation(
+                    out=x_raw[h][b][:, t, :], in_=acc[:, 0:NE], func=ACT.Gelu, bias=cols[:, m : m + 1]
+                )
 
-        def op_gelu(m, sel):
-            h, t = divmod(m, 4)
-            q, rows, n = span(sel)
-            nc.scalar.activation(
-                out=x_pln[h][q][:, rows, t, :], in_=bank[("a1", m, sel)][:, 0:n, :], func=ACT.Gelu, bias=cols[:, m : m + 1]
-            )
+        def interleave_x(h, b):
+            interleave(nc.vector.tensor_copy, x_grp[h][b][:], x_raw[h][b][:], 0, NE)
 
-        def op_rX(h, b):
-            regroup(nc.vector.tensor_copy, x_grp[h][b][:], x_pln[h][b // 2][:, b % 2, :, :], 0, NE)
-
-        def op_qX(h, b):
+        def quantise_x(h, b):
             nc.vector.quantize_mx(out=x_cod[h][b][:].bitcast(FP8X4), scales=x_scl[h][b][:], in_=x_grp[h][b][:])
 
-        def op_mm2(ct, sel):
-            acc = psum.tile([P, 2, NE], F32, name="acc2", tag="mm", bufs=5)
-            bank[("a2", ct, sel)] = acc
-            for i, b in enumerate(grids(sel)):
-                for g in range(2):
+        def layer2(b):
+            for ct in range(4):
+                acc = psum.tile([P, 512], F32, name="acc2", tag="acc", bufs=5)
+                for h in range(2):
                     nc.tensor.matmul_mx(
-                        out=acc[:, i, :],
-                        lhsT=w3_cod[g][:, P * ct : P * ct + P].bitcast(FP8X4),
-                        lhsT_scale=w3_scl[g][:, P * ct : P * ct + P],
-                        rhs=x_cod[g][b][:].bitcast(FP8X4),
-                        rhs_scale=x_scl[g][b][:],
-                        start=(g == 0),
-                        stop=(g == 1),
+                        out=acc[:, 0:NE],
+                        lhsT=w3_cod[h][:, P * ct : P * ct + P].bitcast(FP8X4),
+                        lhsT_scale=w3_scl[h][:, P * ct : P * ct + P],
+                        rhs=x_cod[h][b][:].bitcast(FP8X4),
+                        rhs_scale=x_scl[h][b][:],
+                        start=(h == 0),
+                        stop=(h == 1),
                     )
+                nc.scalar.activation(
+                    out=flux[ct][b][:], in_=acc[:, 0:NE], func=ACT.Tanh, bias=cols[:, 8 + ct : 9 + ct]
+                )
 
-        def op_tanh(ct, sel):
-            q, rows, n = span(sel)
-            nc.scalar.activation(
-                out=t_sb[ct][q][:, rows, :], in_=bank[("a2", ct, sel)][:, 0:n, :], func=ACT.Tanh, bias=cols[:, 8 + ct : 9 + ct]
-            )
-
-        def op_vs(ct, sel):
-            q, rows, n = span(sel)
-            if ct == VSUM[grids(sel)[0]][0]:
-                nc.vector.tensor_scalar_mul(out=wsum[q][:, rows, :], in0=t_sb[ct][q][:, rows, :], scalar1=cols[:, 12 + ct : 13 + ct])
+        def weigh(ct, b, first):
+            if first:
+                nc.vector.tensor_scalar_mul(out=wsum[b][:], in0=flux[ct][b][:], scalar1=cols[:, 12 + ct : 13 + ct])
             else:
                 nc.vector.scalar_tensor_tensor(
-                    out=wsum[q][:, rows, :],
-                    in0=t_sb[ct][q][:, rows, :],
+                    out=wsum[b][:],
+                    in0=flux[ct][b][:],
                     scalar=cols[:, 12 + ct : 13 + ct],
-                    in1=wsum[q][:, rows, :],
+                    in1=wsum[b][:],
                     op0=ALU.mult,
                     op1=ALU.add,
                 )
 
-        def add_to_gsum(op, lhsT, rhs):
-            if op == sums[0]:
-                bank["gsum"] = psum.tile([P, NE], F32, name="gsum", tag="g", bufs=1)
-            nc.tensor.matmul(out=bank["gsum"][:], lhsT=lhsT, rhs=rhs, start=(op == sums[0]), stop=(op == sums[-1]))
-
-        def op_ws(b, z):
-            add_to_gsum(("ws", b, z), pick[:, P * b : P * b + P], wsum[b // 2][:, b % 2, :])
-
-        def op_wsd(ct, b):
-            add_to_gsum(("wsd", ct, b), pick_enc[b][:, P * ct : P * ct + P], t_sb[ct][b // 2][:, b % 2, :])
-
-        def op_f1(a, b):
-            nc.vector.scalar_tensor_tensor(
-                out=part[:], in0=bank["gsum"][0:NB, 0:NC], scalar=c_pos[:, 0:1], in1=u_s[:], op0=ALU.mult, op1=ALU.add
+        warm_up(8)
+        interleave_w2(0, 0)
+        coefficients()
+        turn_e(0)
+        turn_vectors()
+        quantise_w2(0, 0)
+        scale_u()
+        interleave_w2(0, 1)
+        quantise_e(0)
+        quantise_w2(0, 1)
+        warm_up(4)
+        turn_e(1)
+        warm_up(2)
+        interleave_w2(1, 0)
+        layer1(0, 0)
+        quantise_e(1)
+        quantise_w2(1, 0)
+        turn_e(2)
+        interleave_w2(1, 1)
+        layer1(0, 1)
+        interleave_x(0, 0)
+        quantise_w2(1, 1)
+        quantise_e(2)
+        turn_e(3)
+        layer1(1, 0)
+        interleave_x(0, 1)
+        quantise_e(3)
+        interleave_w3(0)
+        quantise_x(0, 0)
+        layer1(0, 2)
+        interleave_x(1, 0)
+        quantise_x(0, 1)
+        layer1(1, 1)
+        quantise_x(1, 0)
+        interleave_w3(1)
+        quantise_w3(0)
+        layer1(1, 2)
+        interleave_x(0, 2)
+        quantise_w3(1)
+        layer1(0, 3)
+        interleave_x(1, 1)
+        quantise_x(0, 2)
+        layer1(1, 3)
+        interleave_x(1, 2)
+        quantise_x(1, 1)
+        interleave_x(0, 3)
+        quantise_x(1, 2)
+        layer2(0)
+        interleave_x(1, 3)
+        layer2(1)
+        quantise_x(0, 3)
+        quantise_x(1, 3)
+        layer2(2)
+        layer2(3)
+        for step in range(4 + max(LAG)):
+            for b in (0, 2, 1, 3):
+                ct = step - LAG[b]
+                skip = 1 if b == DIRECT else 0
+                if skip <= ct < 4:
+                    weigh(ct, b, ct == skip)
+        sums = psum.tile([P, NE], F32, name="sums", tag="sum", bufs=1)
+        products = [(pick, b, wsum[b]) for b in range(NB)]
+        products.insert(2, (pick_enc, 0, flux[0][DIRECT]))
+        for i, (stationary, b, moving) in enumerate(products):
+            nc.tensor.matmul(
+                out=sums[:],
+                lhsT=stationary[:, P * b : P * b + P],
+                rhs=moving[:],
+                start=(i == 0),
+                stop=(i == len(products) - 1),
             )
-
-        def op_f2(a, b):
-            nc.vector.scalar_tensor_tensor(
-                out=res[:], in0=bank["gsum"][0:NB, 1:NE], scalar=c_neg[:, 0:1], in1=part[:], op0=ALU.mult, op1=ALU.add
-            )
-
-        ops = {
-            "warm": op_warm, "vecT": op_vecT, "cols": op_cols, "den": op_den, "rinv": op_rinv, "coef": op_coef, "us": op_us,
-            "rW2": op_rW2, "sW2": op_sW2, "qW2": op_qW2, "rW3": op_rW3, "sW3": op_sW3, "qW3": op_qW3,
-            "tE": op_tE, "cE": op_cE, "vE": op_vE, "qE": op_qE, "mm1": op_mm1, "gelu": op_gelu,
-            "rX": op_rX, "qX": op_qX, "mm2": op_mm2, "tanh": op_tanh,
-            "vs": op_vs, "ws": op_ws, "wsd": op_wsd, "f1": op_f1, "f2": op_f2,
-        }
-        for name, a, b in ORDER:
-            ops[name](a, b)
-
+        nc.vector.scalar_tensor_tensor(
+            out=part[:], in0=sums[0:NB, 0:NC], scalar=c_pos[:, 0:1], in1=u_part[:], op0=ALU.mult, op1=ALU.add
+        )
+        nc.vector.scalar_tensor_tensor(
+            out=res[:], in0=sums[0:NB, 1:NE], scalar=c_neg[:, 0:1], in1=part[:], op0=ALU.mult, op1=ALU.add
+        )
         nc.sync.dma_start(out=out, in_=res[:])

@@ -19,7 +19,8 @@ HID = 1024
 LD = 512
 HALF = 512
 COEF = 0.5 * 0.25
-W3_SCALAR = 128
+W2_SCALAR = {(0, 1): 160}
+W3_SCALAR = 96
 LAG = (0, 0, 2, 3)
 DIRECT = 3
 
@@ -136,7 +137,10 @@ def tile_fluxgnn1dlatent_pb_kernel(tc, edge_hid, u, enc, W2, b2, W3, b3, out):
             )
 
         def interleave_w2(h, g):
-            interleave(nc.vector.tensor_copy, w2_grp[h][:, g, :], w2_raw[h][:, 4 * g : 4 * g + 4, :], 0, HALF)
+            grp, raw, n = w2_grp[h][:, g, :], w2_raw[h][:, 4 * g : 4 * g + 4, :], W2_SCALAR.get((h, g), 0)
+            interleave(nc.vector.tensor_copy, grp, raw, 0, HALF - n)
+            if n:
+                interleave(nc.scalar.copy, grp, raw, HALF - n, HALF)
 
         def quantise_w2(h, g):
             nc.vector.quantize_mx(
@@ -312,10 +316,13 @@ def tile_fluxgnn1dlatent_pb_kernel(tc, edge_hid, u, enc, W2, b2, W3, b3, out):
                 start=(i == 0),
                 stop=(i == len(products) - 1),
             )
-        nc.vector.scalar_tensor_tensor(
-            out=part[:], in0=sums[0:NB, 0:NC], scalar=c_pos[:, 0:1], in1=u_part[:], op0=ALU.mult, op1=ALU.add
-        )
-        nc.vector.scalar_tensor_tensor(
-            out=res[:], in0=sums[0:NB, 1:NE], scalar=c_neg[:, 0:1], in1=part[:], op0=ALU.mult, op1=ALU.add
-        )
+        runs = ((0, P), (P, NC))
+        for c0, c1 in runs:
+            nc.vector.scalar_tensor_tensor(
+                out=part[:, c0:c1], in0=sums[0:NB, c0:c1], scalar=c_pos[:, 0:1], in1=u_part[:, c0:c1], op0=ALU.mult, op1=ALU.add
+            )
+        for c0, c1 in runs:
+            nc.vector.scalar_tensor_tensor(
+                out=res[:, c0:c1], in0=sums[0:NB, c0 + 1 : c1 + 1], scalar=c_neg[:, 0:1], in1=part[:, c0:c1], op0=ALU.mult, op1=ALU.add
+            )
         nc.sync.dma_start(out=out, in_=res[:])

@@ -132,8 +132,8 @@ def tile_fluxgnn1dlatent_pb_kernel(tc, edge_hid, u, enc, W2, b2, W3, b3, out):
 
         def interleave(copy, grp, raw, c0, c1):
             copy(
-                out=grp[:, 4 * c0 : 4 * c1].rearrange("p (c i t) -> p c t i", i=4, t=4),
-                in_=raw[:, :, c0:c1].rearrange("p t (c i) -> p c t i", i=4),
+                out=grp[:, 4 * c0 : 4 * c1].rearrange("p (c i t) -> p c t i", i=8, t=4),
+                in_=raw[:, :, c0:c1].rearrange("p t (c i) -> p c t i", i=8),
             )
 
         def interleave_w2(h, g):

from contextlib import ExitStack

import concourse.mybir as mybir
from concourse.masks import make_identity

F32 = mybir.dt.float32
BF16 = mybir.dt.bfloat16
U32 = mybir.dt.uint32
U8 = mybir.dt.uint8
FP8X4 = mybir.dt.float8_e4m3fn_x4
ACT = mybir.ActivationFunctionType
ALU = mybir.AluOpType

P = 128
NB = 4
NE = 256
NC = 255
HID = 1024
LD = 512
HALF = 512
COEF = 0.5 * 0.25
W2_SCALAR = {(0, 1): 160}
W3_SCALAR = 96
LAG = (0, 0, 2, 3)
DIRECT = 3

FLOPS = 2 * NB * NE * HID * HID + 2 * NB * NE * HID * LD


def tile_fluxgnn1dlatent_pb_kernel(tc, edge_hid, u, enc, W2, b2, W3, b3, out):
    nc = tc.nc
    with ExitStack() as ctx:
        keep = ctx.enter_context(tc.tile_pool(name="keep", bufs=1))
        psum = ctx.enter_context(tc.psum_pool(name="psum", bufs=1))
        ctx.enter_context(tc.manual_schedule())

        e_raw = [keep.tile([P, 2, HID], BF16, name="e_raw%d" % b) for b in range(NB)]
        e_grp = [keep.tile([P, 2, 4 * NE], BF16, name="e_grp%d" % b, align_bytes=64) for b in range(NB)]
        e_cod = [keep.tile([P, 2, NE], U32, name="e_cod%d" % b, align_bytes=64) for b in range(NB)]
        e_scl = [keep.tile([P, 2, NE], U8, name="e_scl%d" % b, align_bytes=64) for b in range(NB)]
        w2_raw = [keep.tile([P, 8, HALF], BF16, name="w2_raw%d" % h) for h in range(2)]
        w2_grp = [keep.tile([P, 2, 4 * HALF], BF16, name="w2_grp%d" % h, align_bytes=64) for h in range(2)]
        w2_cod = [keep.tile([P, 2, HALF], U32, name="w2_cod%d" % h, align_bytes=64) for h in range(2)]
        w2_scl = [keep.tile([P, 2, HALF], U8, name="w2_scl%d" % h, align_bytes=64) for h in range(2)]
        w3_raw = [keep.tile([P, 4, LD], BF16, name="w3_raw%d" % h) for h in range(2)]
        w3_grp = [keep.tile([P, 4 * LD], BF16, name="w3_grp%d" % h, align_bytes=64) for h in range(2)]
        w3_cod = [keep.tile([P, LD], U32, name="w3_cod%d" % h, align_bytes=64) for h in range(2)]
        w3_scl = [keep.tile([P, LD], U8, name="w3_scl%d" % h, align_bytes=64) for h in range(2)]
        x_raw = [[keep.tile([P, 4, NE], BF16, name="x_raw%d_%d" % (h, b)) for b in range(NB)] for h in range(2)]
        x_grp = [
            [keep.tile([P, 4 * NE], BF16, name="x_grp%d_%d" % (h, b), align_bytes=64) for b in range(NB)] for h in range(2)
        ]
        x_cod = [[keep.tile([P, NE], U32, name="x_cod%d_%d" % (h, b), align_bytes=64) for b in range(NB)] for h in range(2)]
        x_scl = [[keep.tile([P, NE], U8, name="x_scl%d_%d" % (h, b), align_bytes=64) for b in range(NB)] for h in range(2)]
        flux = [[keep.tile([P, NE], F32, name="flux%d_%d" % (ct, b)) for b in range(NB)] for ct in range(4)]
        wsum = [keep.tile([P, NE], F32, name="wsum%d" % b) for b in range(NB)]

        ident = keep.tile([P, P], F32, name="ident")
        pick = keep.tile([P, NB * P], F32, name="pick")
        pick_enc = keep.tile([P, P], F32, name="pick_enc")
        vec_rows = keep.tile([16, P], BF16, name="vec_rows")
        vec_f32 = keep.tile([P, P], F32, name="vec_f32")
        cols = keep.tile([P, 16], F32, name="cols")
        dummy_in = keep.tile([P, 1], F32, name="dummy_in")
        dummy_out = keep.tile([P, 1], F32, name="dummy_out")
        zeros = keep.tile([P, 512], BF16, name="zeros")
        u_raw = keep.tile([NB, NC], BF16, name="u_raw")
        u_part = keep.tile([NB, NC], F32, name="u_part")
        enc_rows = keep.tile([NB, LD], BF16, name="enc_rows")
        enc_sq = keep.tile([NB, LD], F32, name="enc_sq")
        ssum = keep.tile([NB, 1], F32, name="ssum")
        den = keep.tile([NB, 1], F32, name="den")
        rinv = keep.tile([NB, 1], F32, name="rinv")
        c_u = keep.tile([NB, 1], F32, name="c_u")
        c_pos = keep.tile([NB, 1], F32, name="c_pos")
        c_neg = keep.tile([NB, 1], F32, name="c_neg")
        part = keep.tile([NB, NC], F32, name="part")
        res = keep.tile([NB, NC], F32, name="res")

        def load_w2(h, g):
            for j in (2 * g, 2 * g + 1):
                nc.sync.dma_start(
                    out=w2_raw[h][:, 2 * j : 2 * j + 2, :],
                    in_=W2[256 * j : 256 * j + 256, HALF * h : HALF * h + HALF].rearrange("(p e) n -> p e n", e=2),
                )

        def load_e(b):
            nc.sync.dma_start(
                out=e_raw[b][:].rearrange("p j k -> p (j k)"), in_=edge_hid[b, :, :].rearrange("(p j) k -> p (j k)", j=2)
            )

        def load_w3(h):
            nc.sync.dma_start(
                out=w3_raw[h][:], in_=W3[HALF * h : HALF * h + HALF, :].rearrange("(t p) c -> p t c", p=P)
            )

        nc.sync.dma_start(out=enc_rows[:], in_=enc.partition_broadcast(NB))
        nc.scalar.dma_start(out=vec_rows[0:8, :], in_=b2.rearrange("(j c) -> j c", c=P))
        nc.scalar.dma_start(out=vec_rows[8:12, :], in_=b3.rearrange("(j c) -> j c", c=P))
        nc.scalar.dma_start(out=vec_rows[12:16, :], in_=enc.rearrange("(j c) -> j c", c=P))
        load_w2(0, 0)
        load_e(0)
        nc.sync.dma_start(out=u_raw[:], in_=u)
        load_w2(0, 1)
        load_e(1)
        load_w2(1, 0)
        load_e(2)
        load_w2(1, 1)
        load_e(3)
        load_w3(0)
        load_w3(1)

        nc.vector.memset(dummy_in[:], 0.0)
        nc.vector.memset(zeros[:], 0.0)
        nc.vector.memset(vec_f32[:], 0.0)
        nc.scalar.activation(out=dummy_out[:], in_=dummy_in[:], func=ACT.Gelu)
        make_identity(nc, ident[:])
        nc.gpsimd.tensor_copy(out=vec_f32[0:16, :], in_=vec_rows[:])
        nc.vector.memset(pick[:], 0.0)
        nc.vector.memset(pick[:, 0 : (NB - 1) * (P + 1) + 1 : P + 1], 1.0)
        nc.vector.memset(pick_enc[:], 0.0)
        nc.vector.scalar_tensor_tensor(
            out=enc_sq[:], in0=enc_rows[:], scalar=1.0, in1=enc_rows[:], op0=ALU.mult, op1=ALU.mult, accum_out=ssum[:]
        )
        nc.vector.tensor_scalar_add(out=den[:], in0=ssum[:], scalar1=1e-12)
        nc.vector.reciprocal(out=rinv[:], in_=den[:])

        def warm_up(count):
            spare = psum.tile([P, 512], F32, name="spare", tag="acc", bufs=5)
            for i in range(count):
                nc.tensor.matmul(out=spare[:], lhsT=zeros[:, 0:P], rhs=zeros[:], start=True, stop=True)

        def interleave(copy, grp, raw, c0, c1):
            copy(
                out=grp[:, 4 * c0 : 4 * c1].rearrange("p (c i t) -> p c t i", i=8, t=4),
                in_=raw[:, :, c0:c1].rearrange("p t (c i) -> p c t i", i=8),
            )

        def interleave_w2(h, g):
            grp, raw, n = w2_grp[h][:, g, :], w2_raw[h][:, 4 * g : 4 * g + 4, :], W2_SCALAR.get((h, g), 0)
            interleave(nc.vector.tensor_copy, grp, raw, 0, HALF - n)
            if n:
                interleave(nc.scalar.copy, grp, raw, HALF - n, HALF)

        def quantise_w2(h, g):
            nc.vector.quantize_mx(
                out=w2_cod[h][:, g, :].bitcast(FP8X4), scales=w2_scl[h][:, g, :], in_=w2_grp[h][:, g, :]
            )

        def interleave_w3(h):
            interleave(nc.vector.tensor_copy, w3_grp[h][:], w3_raw[h][:], 0, LD - W3_SCALAR)
            interleave(nc.scalar.copy, w3_grp[h][:], w3_raw[h][:], LD - W3_SCALAR, LD)

        def quantise_w3(h):
            nc.vector.quantize_mx(out=w3_cod[h][:].bitcast(FP8X4), scales=w3_scl[h][:], in_=w3_grp[h][:])

        def turn_e(b):
            turned = []
            for g in range(2):
                tp = psum.tile([P, 2, 2, P], F32, name="tp", tag="tp", bufs=2)
                turned.append(tp)
                for j in range(2):
                    words = e_raw[b][:, j, :].bitcast(F32)
                    for uu in range(2):
                        w0 = 256 * g + 128 * uu
                        nc.tensor.transpose(tp[:, j, uu, :], words[:, w0 : w0 + P], ident[:])
            for g in range(2):
                nc.scalar.copy(
                    out=e_grp[b][:, g, :].bitcast(F32).rearrange("p (r j w) -> p r j w", j=2, w=2),
                    in_=turned[g][:].rearrange("p j w r -> p r j w"),
                )

        def quantise_e(b):
            nc.vector.quantize_mx(
                out=e_cod[b][:].rearrange("p g r -> p (g r)").bitcast(FP8X4),
                scales=e_scl[b][:].rearrange("p g r -> p (g r)"),
                in_=e_grp[b][:].rearrange("p g c -> p (g c)"),
            )

        def turn_vectors():
            vec_t = psum.tile([P, P], F32, name="vec_t", tag="sum", bufs=1)
            nc.tensor.transpose(vec_t[:], vec_f32[:], ident[:])
            nc.scalar.copy(out=cols[:], in_=vec_t[:, 0:16])
            nc.gpsimd.tensor_copy(out=pick_enc[:, DIRECT : DIRECT + 1], in_=cols[:, 12:13])

        def coefficients():
            nc.vector.tensor_scalar_mul(out=c_u[:], in0=ssum[:], scalar1=rinv[:, 0:1])
            nc.vector.tensor_scalar_mul(out=c_pos[:], in0=rinv[:], scalar1=COEF)
            nc.vector.tensor_scalar_mul(out=c_neg[:], in0=rinv[:], scalar1=-COEF)

        def scale_u():
            nc.vector.tensor_scalar_mul(out=u_part[:], in0=u_raw[:], scalar1=c_u[:, 0:1])

        def layer1(h, b):
            for t in range(4):
                acc = psum.tile([P, 512], F32, name="acc1", tag="acc", bufs=5)
                for g in range(2):
                    nc.tensor.matmul_mx(
                        out=acc[:, 0:NE],
                        lhsT=w2_cod[h][:, g, P * t : P * t + P].bitcast(FP8X4),
                        lhsT_scale=w2_scl[h][:, g, P * t : P * t + P],
                        rhs=e_cod[b][:, g, :].bitcast(FP8X4),
                        rhs_scale=e_scl[b][:, g, :],
                        start=(g == 0),
                        stop=(g == 1),
                    )
                m = 4 * h + t
                nc.scalar.activation(
                    out=x_raw[h][b][:, t, :], in_=acc[:, 0:NE], func=ACT.Gelu, bias=cols[:, m : m + 1]
                )

        def interleave_x(h, b):
            interleave(nc.vector.tensor_copy, x_grp[h][b][:], x_raw[h][b][:], 0, NE)

        def quantise_x(h, b):
            nc.vector.quantize_mx(out=x_cod[h][b][:].bitcast(FP8X4), scales=x_scl[h][b][:], in_=x_grp[h][b][:])

        def layer2(b):
            for ct in range(4):
                acc = psum.tile([P, 512], F32, name="acc2", tag="acc", bufs=5)
                for h in range(2):
                    nc.tensor.matmul_mx(
                        out=acc[:, 0:NE],
                        lhsT=w3_cod[h][:, P * ct : P * ct + P].bitcast(FP8X4),
                        lhsT_scale=w3_scl[h][:, P * ct : P * ct + P],
                        rhs=x_cod[h][b][:].bitcast(FP8X4),
                        rhs_scale=x_scl[h][b][:],
                        start=(h == 0),
                        stop=(h == 1),
                    )
                nc.scalar.activation(
                    out=flux[ct][b][:], in_=acc[:, 0:NE], func=ACT.Tanh, bias=cols[:, 8 + ct : 9 + ct]
                )

        def weigh(ct, b, first):
            if first:
                nc.vector.tensor_scalar_mul(out=wsum[b][:], in0=flux[ct][b][:], scalar1=cols[:, 12 + ct : 13 + ct])
            else:
                nc.vector.scalar_tensor_tensor(
                    out=wsum[b][:],
                    in0=flux[ct][b][:],
                    scalar=cols[:, 12 + ct : 13 + ct],
                    in1=wsum[b][:],
                    op0=ALU.mult,
                    op1=ALU.add,
                )

        warm_up(8)
        interleave_w2(0, 0)
        coefficients()
        turn_e(0)
        turn_vectors()
        quantise_w2(0, 0)
        scale_u()
        interleave_w2(0, 1)
        quantise_e(0)
        quantise_w2(0, 1)
        warm_up(4)
        turn_e(1)
        warm_up(2)
        interleave_w2(1, 0)
        layer1(0, 0)
        quantise_e(1)
        quantise_w2(1, 0)
        turn_e(2)
        interleave_w2(1, 1)
        layer1(0, 1)
        interleave_x(0, 0)
        quantise_w2(1, 1)
        quantise_e(2)
        turn_e(3)
        layer1(1, 0)
        interleave_x(0, 1)
        quantise_e(3)
        interleave_w3(0)
        quantise_x(0, 0)
        layer1(0, 2)
        interleave_x(1, 0)
        quantise_x(0, 1)
        layer1(1, 1)
        quantise_x(1, 0)
        interleave_w3(1)
        quantise_w3(0)
        layer1(1, 2)
        interleave_x(0, 2)
        quantise_w3(1)
        layer1(0, 3)
        interleave_x(1, 1)
        quantise_x(0, 2)
        layer1(1, 3)
        interleave_x(1, 2)
        quantise_x(1, 1)
        interleave_x(0, 3)
        quantise_x(1, 2)
        layer2(0)
        interleave_x(1, 3)
        layer2(1)
        quantise_x(0, 3)
        quantise_x(1, 3)
        layer2(2)
        layer2(3)
        for step in range(4 + max(LAG)):
            for b in (0, 2, 1, 3):
                ct = step - LAG[b]
                skip = 1 if b == DIRECT else 0
                if skip <= ct < 4:
                    weigh(ct, b, ct == skip)
        sums = psum.tile([P, NE], F32, name="sums", tag="sum", bufs=1)
        products = [(pick, b, wsum[b]) for b in range(NB)]
        products.insert(2, (pick_enc, 0, flux[0][DIRECT]))
        for i, (stationary, b, moving) in enumerate(products):
            nc.tensor.matmul(
                out=sums[:],
                lhsT=stationary[:, P * b : P * b + P],
                rhs=moving[:],
                start=(i == 0),
                stop=(i == len(products) - 1),
            )
        runs = ((0, P), (P, NC))
        for c0, c1 in runs:
            nc.vector.scalar_tensor_tensor(
                out=part[:, c0:c1], in0=sums[0:NB, c0:c1], scalar=c_pos[:, 0:1], in1=u_part[:, c0:c1], op0=ALU.mult, op1=ALU.add
            )
        for c0, c1 in runs:
            nc.vector.scalar_tensor_tensor(
                out=res[:, c0:c1], in0=sums[0:NB, c0 + 1 : c1 + 1], scalar=c_neg[:, 0:1], in1=part[:, c0:c1], op0=ALU.mult, op1=ALU.add
            )
        nc.sync.dma_start(out=out, in_=res[:])
